import numpy as np
import ml_dtypes


def mxq(x, axis, fmt="e4m3"):
    dtype, down = {"e4m3": (ml_dtypes.float8_e4m3fn, 7), "e5m2": (ml_dtypes.float8_e5m2, 14)}[fmt]
    v = np.moveaxis(np.asarray(x, np.float32).astype(ml_dtypes.bfloat16).astype(np.float64), axis, -1)
    blocks = v.reshape(v.shape[:-1] + (-1, 32))
    amax = np.abs(blocks).max(-1, keepdims=True)
    byte = np.maximum(np.where(amax > 0, np.frexp(amax)[1] - 1 + 127, 0) - down, 1)
    scale = np.exp2(byte - 127.0)
    codes = (blocks / scale).astype(np.float32).astype(dtype).astype(np.float64)
    return np.moveaxis((codes * scale).reshape(v.shape), -1, axis)


WIDE = False


def mx_kscale(k):
    if not WIDE:
        return np.ones(k)
    levels = np.array([18, -18])
    if k % 512:
        return np.exp2(np.random.permutation(np.resize(levels, k // 32))).repeat(32)
    a = np.empty((k // 512, 16))
    for p in range(k // 512):
        a[p, :8] = np.random.permutation(np.resize(levels, 8))
        for g in range(8):
            far = levels[np.abs(levels - a[p, g]) >= 10]
            a[p, g + 8] = far[np.random.randint(len(far))]
    return np.exp2(a.ravel()).repeat(32)


BF16 = ml_dtypes.bfloat16


def bf(x):
    return np.asarray(x, np.float32).astype(BF16)


def f64(x):
    return np.asarray(x).astype(np.float64)


S, B, D1, D2 = 8, 512, 512, 512


def sample(eps, logvar, mean):
    return eps * np.exp(0.5 * logvar) + mean


def setup_inputs():
    s = mx_kscale(S * B).reshape(S, B, 1)
    u = mx_kscale(D2)
    h00 = bf(np.maximum(np.random.standard_normal((S, B, D1)), 0.0) * 1.1)
    wm10 = bf(np.random.standard_normal((D1, D2)) * 0.8 / np.sqrt(D1))
    wv1 = bf(2.0 * np.log(0.6 / np.sqrt(D1)) + 0.5 * np.random.standard_normal((D1, D2)))
    bm1 = bf(np.random.standard_normal(D2) * 0.3)
    bv1 = bf(2.0 * np.log(0.3) + 0.5 * np.random.standard_normal(D2))
    we10 = bf(np.random.standard_normal((S, D1, D2)))
    be1 = bf(np.random.standard_normal((S, 1, D2)))
    g = bf(np.random.standard_normal((S, B, D2)) * np.exp2(np.random.randint(-6, 1, (S, B, 1))) / s * u)
    z = f64(h00) @ sample(f64(we10), f64(wv1), f64(wm10)) + sample(f64(be1), f64(bv1), f64(bm1))
    return {
        "h0": bf(f64(h00) * s),
        "wm1": bf(f64(wm10) / u),
        "wv1": wv1,
        "bm1": bm1,
        "bv1": bv1,
        "we1": bf(f64(we10) / u),
        "be1": be1,
        "z": np.asarray(z, np.float32),
        "grad_out": g,
    }


def reference(h0, wm1, wv1, bm1, bv1, we1, be1, z, grad_out):
    dz = np.where(f64(z) > 0.0, f64(grad_out), 0.0)
    w1 = sample(f64(we1), f64(wv1), f64(wm1))
    dh0 = mxq(dz, 2, "e5m2") @ mxq(w1, 2, "e4m3").transpose(0, 2, 1)
    ht = f64(h0).reshape(S * B, D1)
    dzt = dz.reshape(S * B, D2)
    dwm1 = mxq(ht, 0, "e4m3").T @ mxq(dzt, 0, "e5m2")
    return dh0, dwm1

@@ -1,0 +1,252 @@
+from contextlib import ExitStack
+
+import concourse.mybir as mybir
+from concourse.masks import make_identity
+
+S, B, D1, D2 = 8, 512, 512, 512
+FLOPS = 2 * 2 * S * B * D1 * D2
+BYTES = S * B * (2 * D1 + 4 * D2 + 2 * D2 + 4 * D1) + 2 * S * D1 * D2 + (2 + 2 + 4) * D1 * D2
+
+F32 = mybir.dt.float32
+BF16 = mybir.dt.bfloat16
+U32 = mybir.dt.uint32
+U8 = mybir.dt.uint8
+E4M3 = mybir.dt.float8_e4m3fn_x4
+E5M2 = mybir.dt.float8_e5m2_x4
+ALU = mybir.AluOpType
+ACT = mybir.ActivationFunctionType
+
+P = 128
+H_SPLIT = 192
+
+
+def tile_bnn_pb_v_kernel(tc, h0, wm1, wv1, bm1, bv1, we1, be1, z, grad_out, out_0, out_1):
+    nc = tc.nc
+    with ExitStack() as ctx:
+        const = ctx.enter_context(tc.tile_pool(name="const", bufs=1))
+        loads = ctx.enter_context(tc.tile_pool(name="loads", bufs=4))
+        mid = ctx.enter_context(tc.tile_pool(name="mid", bufs=2))
+        codes = ctx.enter_context(tc.tile_pool(name="codes", bufs=2))
+        outs = ctx.enter_context(tc.tile_pool(name="outs", bufs=3))
+        acc_pool = ctx.enter_context(tc.psum_pool(name="acc", bufs=1))
+        psum = ctx.enter_context(tc.psum_pool(name="psum", bufs=4))
+
+        ident_f = const.tile([P, P], F32, name="ident_f")
+        make_identity(nc, ident_f[:])
+
+        acc = [acc_pool.tile([P, D2], F32, name="acc%d" % b) for b in range(4)]
+
+        we_t, z_t, g_t, h_t = {}, {}, {}, {}
+        hi_t, di_t, p_t, wt_t, dz_t, dt_t = {}, {}, {}, {}, {}, {}
+        wq_t, dq_t, hq_t, tq_t, o_t = {}, {}, {}, {}, {}
+
+        def load_we(s):
+            we_t[s] = loads.tile([P, 4, D2], BF16, name="we")
+            nc.sync.dma_start(out=we_t[s][:], in_=we1[s].rearrange("(p j) w -> p j w", j=4))
+
+        def load_zg(s):
+            z_t[s] = loads.tile([P, 4, D2], F32, name="z")
+            g_t[s] = loads.tile([P, 4, D2], BF16, name="g")
+            for js in row_pieces(s):
+                nc.sync.dma_start(out=z_t[s][:, js, :], in_=z[s].rearrange("(p j) w -> p j w", j=4)[:, js, :])
+                nc.sync.dma_start(out=g_t[s][:, js, :], in_=grad_out[s].rearrange("(p j) w -> p j w", j=4)[:, js, :])
+
+        def row_pieces(s):
+            return [slice(0, 2), slice(2, 4)] if s == 0 else [slice(0, 4)]
+
+        def load_h(s):
+            h_t[s] = loads.tile([P, 4, D1], BF16, name="h")
+            nc.sync.dma_start(out=h_t[s][:], in_=h0[s].rearrange("(p j) w -> p j w", j=4))
+
+        def quantize(s, src, dtype, store, nm):
+            c = codes.tile([P, 512], U32, name=nm + "c", align_bytes=256)
+            q = codes.tile([P, 512], U8, name=nm + "s", align_bytes=256)
+            nc.vector.quantize_mx(out=c[:].bitcast(dtype), scales=q[:], in_=src)
+            store[s] = (c, q)
+
+        def q_h(s):
+            quantize(s, hi_t[s][:].rearrange("p w j -> p (w j)"), E4M3, hq_t, "h")
+
+        def q_d(s):
+            quantize(s, di_t[s][:].rearrange("p w j -> p (w j)"), E5M2, dq_t, "d")
+
+        def q_w(s):
+            quantize(s, wt_t[s][:].rearrange("p j x t -> p (j x t)"), E4M3, wq_t, "w")
+
+        def q_t(s):
+            quantize(s, dt_t[s][:].rearrange("p j x u -> p (j x u)").bitcast(BF16), E5M2, tq_t, "t")
+
+        def mask(s):
+            dz_t[s] = mid.tile([P, 4, D2], BF16, name="dz", align_bytes=256, bufs=3)
+            for js in row_pieces(s):
+                nc.vector.scalar_tensor_tensor(
+                    out=dz_t[s][:, js, :], in0=z_t[s][:, js, :], scalar=0.0, in1=g_t[s][:, js, :], op0=ALU.is_gt, op1=ALU.mult
+                )
+
+        def interleave(copy, out, in_, lo, hi):
+            copy(
+                out=out[:, lo:hi, :].rearrange("p (c i) t -> p c t i", i=4),
+                in_=in_[:, :, lo:hi].rearrange("p t (c i) -> p c t i", i=4),
+            )
+
+        def d_interleave(s):
+            di_t[s] = mid.tile([P, D2, 4], BF16, name="di", align_bytes=256)
+            interleave(nc.vector.tensor_copy, di_t[s], dz_t[s], 0, D2)
+
+        def h_interleave(s):
+            hi_t[s] = mid.tile([P, D1, 4], BF16, name="hi", align_bytes=256, bufs=3)
+            cut = D1 if s < 5 else H_SPLIT
+            interleave(nc.scalar.copy, hi_t[s], h_t[s], 0, cut)
+            if cut < D1:
+                interleave(nc.vector.tensor_copy, hi_t[s], h_t[s], cut, D1)
+
+        def product(s):
+            p_t[s] = mid.tile([P, 4, 4, P], F32, name="p", bufs=3)
+            pieces = [slice(j, j + 1) for j in range(4)] if s == 0 else [slice(0, 4)]
+            for js in pieces:
+                nc.vector.tensor_tensor(
+                    out=p_t[s][:, js, :, :],
+                    in0=we_t[s][:, js, :].rearrange("p j (m t) -> p j t m", t=4),
+                    in1=e_s[:, js, :, :],
+                    op=ALU.mult,
+                )
+
+        def w_transposes(s, j):
+            if j == 0:
+                wt_t[s] = mid.tile([P, 4, P, 4], BF16, name="wt", align_bytes=256)
+            bank = psum.tile([P, 4, P], F32, name="bank")
+            for t in range(4):
+                nc.tensor.matmul(bank[:, t, :], lhsT=wm_s[:, j, t, :], rhs=ident_f[:], is_transpose=True, start=True, stop=False)
+                nc.tensor.matmul(bank[:, t, :], lhsT=p_t[s][:, j, t, :], rhs=ident_f[:], is_transpose=True, start=False, stop=True)
+            nc.scalar.copy(out=wt_t[s][:, j, :, :], in_=bank[:].rearrange("p t x -> p x t"))
+
+        def dz_transposes(s, half):
+            if half == 0:
+                dt_t[s] = mid.tile([P, 4, P, 2], F32, name="dt", align_bytes=256)
+            bank = psum.tile([P, 2, 2, P], F32, name="bank")
+            for k in range(2):
+                words = dz_t[s][:, 2 * half + k, :].bitcast(F32)
+                for u in range(2):
+                    nc.tensor.transpose(bank[:, k, u, :], words[:, u::2], ident_f[:])
+            nc.scalar.copy(out=dt_t[s][:, 2 * half : 2 * half + 2, :, :], in_=bank[:].rearrange("p k u x -> p k x u"))
+
+        def weight_grad(s, b):
+            hc, hs = hq_t[s]
+            dc, ds = dq_t[s]
+            cols = slice(P * b, P * (b + 1))
+            nc.tensor.matmul_mx(
+                out=acc[b][:],
+                lhsT=hc[:, cols].bitcast(E4M3),
+                lhsT_scale=hs[:, cols],
+                rhs=dc[:].bitcast(E5M2),
+                rhs_scale=ds[:],
+                start=(s == 0),
+                stop=(s == S - 1),
+            )
+            if s == S - 1:
+                r = outs.tile([P, D2], F32, name="r%d" % b, bufs=1)
+                copy = nc.vector.tensor_copy if b in (1, 2) else nc.scalar.copy
+                copy(out=r[:], in_=acc[b][:])
+                nc.sync.dma_start(out=out_1[P * b : P * (b + 1), :], in_=r[:])
+
+        def input_grad(s, j):
+            tcod, tsc = tq_t[s]
+            wc, ws = wq_t[s]
+            if j == 0:
+                o_t[s] = outs.tile([P, 4, P, 4], F32, name="o")
+            cols = slice(P * j, P * (j + 1))
+            bank = psum.tile([P, 4, P], F32, name="bank")
+            nc.tensor.matmul_mx(
+                out=bank[:].rearrange("p t x -> p (t x)"),
+                lhsT=tcod[:, cols].bitcast(E5M2),
+                lhsT_scale=tsc[:, cols],
+                rhs=wc[:].bitcast(E4M3),
+                rhs_scale=ws[:],
+                start=True,
+                stop=True,
+            )
+            copy = nc.vector.tensor_copy if s == S - 2 and j == 2 else nc.scalar.copy
+            copy(out=o_t[s][:, j, :, :], in_=bank[:].rearrange("p t x -> p x t"))
+            if s == S - 1:
+                store_rows(s, j, j + 1)
+
+        def store_rows(s, j0, j1):
+            nc.sync.dma_start(
+                out=out_0[s].rearrange("(p j) d -> p j d", j=4)[:, j0:j1, :],
+                in_=o_t[s][:, j0:j1, :, :].rearrange("p j x t -> p j (x t)"),
+            )
+
+        def store(s):
+            if s < S - 1:
+                store_rows(s, 0, 4)
+
+        def sub(fn, k):
+            return lambda s: fn(s, k)
+
+        STEP = [
+            (sub(input_grad, 0), 0),
+            (sub(input_grad, 1), 0),
+            (sub(dz_transposes, 0), -1),
+            (sub(dz_transposes, 1), -1),
+            (sub(input_grad, 2), 0),
+            (sub(input_grad, 3), 0),
+            (product, -4),
+            (q_w, -1),
+            (sub(weight_grad, 1), 1),
+            (mask, -2),
+            (q_t, -1),
+            (load_we, -6),
+            (h_interleave, -2),
+            (sub(w_transposes, 0), -2),
+            (q_d, 0),
+            (q_h, 0),
+            (load_h, -4),
+            (sub(w_transposes, 1), -2),
+            (load_zg, -4),
+            (sub(weight_grad, 0), 1),
+            (sub(weight_grad, 3), 1),
+            (sub(w_transposes, 2), -2),
+            (sub(w_transposes, 3), -2),
+            (store, 0),
+            (sub(weight_grad, 2), 1),
+            (d_interleave, -2),
+        ]
+
+        with tc.manual_schedule():
+            warm = const.tile([P, 1], F32, name="warm")
+            nc.vector.memset(warm[:], 0.0)
+            nc.scalar.activation(out=warm[:], in_=warm[:], func=ACT.Exp)
+            wv_t = const.tile([P, 4, D2], BF16, name="wv_t")
+            wv_view = wv1.rearrange("(p j) w -> p j w", j=4)
+            we_t[0] = loads.tile([P, 4, D2], BF16, name="we")
+            we_view = we1[0].rearrange("(p j) w -> p j w", j=4)
+            for js in (slice(0, 2), slice(2, 4)):
+                nc.sync.dma_start(out=wv_t[:, js, :], in_=wv_view[:, js, :])
+                nc.sync.dma_start(out=we_t[0][:, js, :], in_=we_view[:, js, :])
+            wm_t = const.tile([P, 4, D2], BF16, name="wm_t")
+            nc.sync.dma_start(out=wm_t[:], in_=wm1.rearrange("(p j) w -> p j w", j=4))
+
+            e_s = const.tile([P, 4, 4, P], F32, name="e_s")
+            wm_s = const.tile([P, 4, 4, P], F32, name="wm_s")
+            for j in range(4):
+                nc.scalar.activation(
+                    out=e_s[:, j, :, :],
+                    in_=wv_t[:, j, :].rearrange("p (m t) -> p t m", t=4),
+                    func=ACT.Exp,
+                    scale=0.5,
+                )
+            for j in range(4):
+                nc.gpsimd.tensor_scalar(
+                    out=wm_s[:, j, :, :],
+                    in0=wm_t[:, j, :].rearrange("p (m t) -> p t m", t=4),
+                    scalar1=1.0,
+                    scalar2=0.0,
+                    op0=ALU.mult,
+                    op1=ALU.add,
+                )
+
+            for step in range(-6, S + 1):
+                for what, lag in STEP:
+                    s = step - lag
+                    if 0 <= s < S and not (what is load_we and s == 0):
+                        what(s)

@@ -17,55 +17,63 @@ ALU = mybir.AluOpType
 ACT = mybir.ActivationFunctionType
 
 P = 128
-H_SPLIT = 192
+AHEAD = 4
+OUT_BUFS = 4
+H_CUTS = (0, 176, 344, 512)
+HALVES = (slice(0, 2), slice(2, 4))
 
 
 def tile_bnn_pb_v_kernel(tc, h0, wm1, wv1, bm1, bv1, we1, be1, z, grad_out, out_0, out_1):
     nc = tc.nc
     with ExitStack() as ctx:
         const = ctx.enter_context(tc.tile_pool(name="const", bufs=1))
-        loads = ctx.enter_context(tc.tile_pool(name="loads", bufs=4))
+        loads = ctx.enter_context(tc.tile_pool(name="loads", bufs=AHEAD))
         mid = ctx.enter_context(tc.tile_pool(name="mid", bufs=2))
         codes = ctx.enter_context(tc.tile_pool(name="codes", bufs=2))
-        outs = ctx.enter_context(tc.tile_pool(name="outs", bufs=3))
+        outs = ctx.enter_context(tc.tile_pool(name="outs", bufs=OUT_BUFS))
         acc_pool = ctx.enter_context(tc.psum_pool(name="acc", bufs=1))
         psum = ctx.enter_context(tc.psum_pool(name="psum", bufs=4))
+        ctx.enter_context(tc.manual_schedule())
 
         ident_f = const.tile([P, P], F32, name="ident_f")
         make_identity(nc, ident_f[:])
-
+        ident_b = const.tile([P, P], BF16, name="ident_b")
+        make_identity(nc, ident_b[:])
         acc = [acc_pool.tile([P, D2], F32, name="acc%d" % b) for b in range(4)]
 
         we_t, z_t, g_t, h_t = {}, {}, {}, {}
         hi_t, di_t, p_t, wt_t, dz_t, dt_t = {}, {}, {}, {}, {}, {}
         wq_t, dq_t, hq_t, tq_t, o_t = {}, {}, {}, {}, {}
 
+        def rows(ap):
+            return ap.rearrange("(p j) w -> p j w", j=4)
+
+        def row_pieces(s):
+            return HALVES if s == 0 else (slice(0, 4),)
+
         def load_we(s):
             we_t[s] = loads.tile([P, 4, D2], BF16, name="we")
-            nc.sync.dma_start(out=we_t[s][:], in_=we1[s].rearrange("(p j) w -> p j w", j=4))
+            nc.sync.dma_start(out=we_t[s][:], in_=rows(we1[s]))
 
         def load_zg(s):
             z_t[s] = loads.tile([P, 4, D2], F32, name="z")
             g_t[s] = loads.tile([P, 4, D2], BF16, name="g")
             for js in row_pieces(s):
-                nc.sync.dma_start(out=z_t[s][:, js, :], in_=z[s].rearrange("(p j) w -> p j w", j=4)[:, js, :])
-                nc.sync.dma_start(out=g_t[s][:, js, :], in_=grad_out[s].rearrange("(p j) w -> p j w", j=4)[:, js, :])
-
-        def row_pieces(s):
-            return [slice(0, 2), slice(2, 4)] if s == 0 else [slice(0, 4)]
+                nc.sync.dma_start(out=z_t[s][:, js, :], in_=rows(z[s])[:, js, :])
+                nc.sync.dma_start(out=g_t[s][:, js, :], in_=rows(grad_out[s])[:, js, :])
 
         def load_h(s):
             h_t[s] = loads.tile([P, 4, D1], BF16, name="h")
-            nc.sync.dma_start(out=h_t[s][:], in_=h0[s].rearrange("(p j) w -> p j w", j=4))
+            nc.sync.dma_start(out=h_t[s][:], in_=rows(h0[s]))
 
-        def quantize(s, src, dtype, store, nm):
-            c = codes.tile([P, 512], U32, name=nm + "c", align_bytes=256)
-            q = codes.tile([P, 512], U8, name=nm + "s", align_bytes=256)
+        def quantize(s, src, dtype, store, nm, bufs=2):
+            c = codes.tile([P, 512], U32, name=nm + "c", align_bytes=256, bufs=bufs)
+            q = codes.tile([P, 512], U8, name=nm + "s", align_bytes=256, bufs=bufs)
             nc.vector.quantize_mx(out=c[:].bitcast(dtype), scales=q[:], in_=src)
             store[s] = (c, q)
 
         def q_h(s):
-            quantize(s, hi_t[s][:].rearrange("p w j -> p (w j)"), E4M3, hq_t, "h")
+            quantize(s, hi_t[s][:].rearrange("p w j -> p (w j)"), E4M3, hq_t, "h", 3)
 
         def q_d(s):
             quantize(s, di_t[s][:].rearrange("p w j -> p (w j)"), E5M2, dq_t, "d")
@@ -76,59 +84,89 @@ def tile_bnn_pb_v_kernel(tc, h0, wm1, wv1, bm1, bv1, we1, be1, z, grad_out, out_
         def q_t(s):
             quantize(s, dt_t[s][:].rearrange("p j x u -> p (j x u)").bitcast(BF16), E5M2, tq_t, "t")
 
-        def mask(s):
-            dz_t[s] = mid.tile([P, 4, D2], BF16, name="dz", align_bytes=256, bufs=3)
-            for js in row_pieces(s):
-                nc.vector.scalar_tensor_tensor(
-                    out=dz_t[s][:, js, :], in0=z_t[s][:, js, :], scalar=0.0, in1=g_t[s][:, js, :], op0=ALU.is_gt, op1=ALU.mult
-                )
+        def by_half_block(tile, js, u):
+            return tile[:, js, :].rearrange("p j (b u c) -> p u (j b) c", u=2, c=16)[:, u, :, :]
 
-        def interleave(copy, out, in_, lo, hi):
-            copy(
-                out=out[:, lo:hi, :].rearrange("p (c i) t -> p c t i", i=4),
-                in_=in_[:, :, lo:hi].rearrange("p t (c i) -> p c t i", i=4),
-            )
+        def by_slot(tile, js, u):
+            return tile[:, js, :].rearrange("p j (b u i e) -> p u e (j b) i", u=2, i=8, e=2)[:, u, :, :, :]
+
+        def slot_major(tile, js, u):
+            return tile[:, u, :, js, :].rearrange("p e j (b i) -> p e (j b) i", i=8)
+
+        def mask(s):
+            dz_t[s] = mid.tile([P, 2, 4, 256], BF16, name="dz", align_bytes=256)
+            for js in row_pieces(s):
+                for u in range(2):
+                    nc.vector.scalar_tensor_tensor(
+                        out=dz_t[s][:, u, js, :].rearrange("p j (b c) -> p (j b) c", c=16),
+                        in0=by_half_block(z_t[s], js, u),
+                        scalar=0.0,
+                        in1=by_half_block(g_t[s], js, u),
+                        op0=ALU.is_gt,
+                        op1=ALU.mult,
+                    )
 
         def d_interleave(s):
             di_t[s] = mid.tile([P, D2, 4], BF16, name="di", align_bytes=256)
-            interleave(nc.vector.tensor_copy, di_t[s], dz_t[s], 0, D2)
+            nc.vector.tensor_copy(
+                out=di_t[s][:].rearrange("p (u c i) j -> p u c j i", u=2, i=4),
+                in_=dz_t[s][:].rearrange("p u j (c i) -> p u c j i", i=4),
+            )
 
-        def h_interleave(s):
-            hi_t[s] = mid.tile([P, D1, 4], BF16, name="hi", align_bytes=256, bufs=3)
-            cut = D1 if s < 5 else H_SPLIT
-            interleave(nc.scalar.copy, hi_t[s], h_t[s], 0, cut)
-            if cut < D1:
-                interleave(nc.vector.tensor_copy, hi_t[s], h_t[s], cut, D1)
+        def h_interleave(s, k):
+            if k == 0:
+                hi_t[s] = mid.tile([P, D1, 4], BF16, name="hi", align_bytes=256)
+            cols = slice(H_CUTS[k], H_CUTS[k + 1])
+            nc.scalar.copy(
+                out=hi_t[s][:, cols, :].rearrange("p (c i) j -> p c j i", i=4),
+                in_=h_t[s][:, :, cols].rearrange("p j (c i) -> p c j i", i=4),
+            )
 
-        def product(s):
-            p_t[s] = mid.tile([P, 4, 4, P], F32, name="p", bufs=3)
-            pieces = [slice(j, j + 1) for j in range(4)] if s == 0 else [slice(0, 4)]
-            for js in pieces:
+        def product(s, js=slice(0, 4)):
+            if js.start == 0:
+                p_t[s] = mid.tile([P, 2, 2, 4, P], F32, name="p")
+            for u in range(2):
                 nc.vector.tensor_tensor(
-                    out=p_t[s][:, js, :, :],
-                    in0=we_t[s][:, js, :].rearrange("p j (m t) -> p j t m", t=4),
-                    in1=e_s[:, js, :, :],
-                    op=ALU.mult,
+                    out=slot_major(p_t[s], js, u), in0=by_slot(we_t[s], js, u), in1=slot_major(e_s, js, u), op=ALU.mult
                 )
 
-        def w_transposes(s, j):
+        def w_open(s, j):
             if j == 0:
                 wt_t[s] = mid.tile([P, 4, P, 4], BF16, name="wt", align_bytes=256)
             bank = psum.tile([P, 4, P], F32, name="bank")
-            for t in range(4):
-                nc.tensor.matmul(bank[:, t, :], lhsT=wm_s[:, j, t, :], rhs=ident_f[:], is_transpose=True, start=True, stop=False)
-                nc.tensor.matmul(bank[:, t, :], lhsT=p_t[s][:, j, t, :], rhs=ident_f[:], is_transpose=True, start=False, stop=True)
-            nc.scalar.copy(out=wt_t[s][:, j, :, :], in_=bank[:].rearrange("p t x -> p x t"))
+            if j > 0:
+                nc.tensor.matmul(
+                    bank[:].rearrange("p t x -> p (t x)"), lhsT=ident_b[:], rhs=wm_tr[:, j - 1, :], start=True, stop=False
+                )
+            return bank
 
-        def dz_transposes(s, half):
+        def w_close(s, j, bank):
+            for t in range(4):
+                if j == 0:
+                    nc.tensor.matmul(
+                        bank[:, t, :], lhsT=wm_f[:, t, :], rhs=ident_f[:], is_transpose=True, start=True, stop=False
+                    )
+                nc.tensor.matmul(
+                    bank[:, t, :],
+                    lhsT=p_t[s][:, t // 2, t % 2, j, :],
+                    rhs=ident_f[:],
+                    is_transpose=True,
+                    start=False,
+                    stop=(j == 0 or t == 3),
+                )
+            return lambda: nc.scalar.copy(out=wt_t[s][:, j, :, :], in_=bank[:].rearrange("p t x -> p x t"))
+
+        def w_bank(s, j):
+            return w_close(s, j, w_open(s, j))
+
+        def dz_bank(s, half):
             if half == 0:
                 dt_t[s] = mid.tile([P, 4, P, 2], F32, name="dt", align_bytes=256)
             bank = psum.tile([P, 2, 2, P], F32, name="bank")
             for k in range(2):
-                words = dz_t[s][:, 2 * half + k, :].bitcast(F32)
                 for u in range(2):
-                    nc.tensor.transpose(bank[:, k, u, :], words[:, u::2], ident_f[:])
-            nc.scalar.copy(out=dt_t[s][:, 2 * half : 2 * half + 2, :, :], in_=bank[:].rearrange("p k u x -> p k x u"))
+                    nc.tensor.transpose(bank[:, k, u, :], dz_t[s][:, u, 2 * half + k, :].bitcast(F32), ident_f[:])
+            return lambda: nc.scalar.copy(out=dt_t[s][:, HALVES[half], :, :], in_=bank[:].rearrange("p k u x -> p k x u"))
 
         def weight_grad(s, b):
             hc, hs = hq_t[s]
@@ -143,13 +181,16 @@ def tile_bnn_pb_v_kernel(tc, h0, wm1, wv1, bm1, bv1, we1, be1, z, grad_out, out_
                 start=(s == 0),
                 stop=(s == S - 1),
             )
-            if s == S - 1:
-                r = outs.tile([P, D2], F32, name="r%d" % b, bufs=1)
-                copy = nc.vector.tensor_copy if b in (1, 2) else nc.scalar.copy
-                copy(out=r[:], in_=acc[b][:])
-                nc.sync.dma_start(out=out_1[P * b : P * (b + 1), :], in_=r[:])
 
-        def input_grad(s, j):
+        def finish_weight_grad(b, copy):
+            r = const.tile([P, D2], F32, name="r%d" % b)
+            copy(
+                out=r[:].rearrange("p (b u c) -> p b u c", u=2, c=16),
+                in_=acc[b][:].rearrange("p (u b c) -> p b u c", u=2, c=16),
+            )
+            nc.sync.dma_start(out=out_1[P * b : P * (b + 1), :], in_=r[:])
+
+        def input_grad(s, j, copy):
             tcod, tsc = tq_t[s]
             wc, ws = wq_t[s]
             if j == 0:
@@ -165,88 +206,140 @@ def tile_bnn_pb_v_kernel(tc, h0, wm1, wv1, bm1, bv1, we1, be1, z, grad_out, out_
                 start=True,
                 stop=True,
             )
-            copy = nc.vector.tensor_copy if s == S - 2 and j == 2 else nc.scalar.copy
             copy(out=o_t[s][:, j, :, :], in_=bank[:].rearrange("p t x -> p x t"))
-            if s == S - 1:
-                store_rows(s, j, j + 1)
+            store_rows(s, slice(j, j + 1))
 
-        def store_rows(s, j0, j1):
-            nc.sync.dma_start(
-                out=out_0[s].rearrange("(p j) d -> p j d", j=4)[:, j0:j1, :],
-                in_=o_t[s][:, j0:j1, :, :].rearrange("p j x t -> p j (x t)"),
-            )
+        def store_rows(s, js):
+            nc.sync.dma_start(out=rows(out_0[s])[:, js, :], in_=o_t[s][:, js, :, :].rearrange("p j x t -> p j (x t)"))
 
-        def store(s):
-            if s < S - 1:
-                store_rows(s, 0, 4)
+        wv_t = const.tile([P, 4, D2], BF16, name="wv_t")
+        for js in HALVES:
+            nc.sync.dma_start(out=wv_t[:, js, :], in_=rows(wv1)[:, js, :])
+        load_h(0)
+        we_t[0] = loads.tile([P, 4, D2], BF16, name="we")
+        wm_t = const.tile([P, 4, D2], BF16, name="wm_t")
+        nc.sync.dma_start(out=we_t[0][:, HALVES[0], :], in_=rows(we1[0])[:, HALVES[0], :])
+        nc.sync.dma_start(out=wm_t[:], in_=rows(wm1))
+        nc.sync.dma_start(out=we_t[0][:, HALVES[1], :], in_=rows(we1[0])[:, HALVES[1], :])
+        load_h(1)
+        load_we(1)
+        load_zg(0)
+        load_h(2)
+        for s in range(1, AHEAD):
+            load_zg(s)
+            if s + 1 < AHEAD:
+                load_we(s + 1)
+            if s + 2 < AHEAD:
+                load_h(s + 2)
 
-        def sub(fn, k):
-            return lambda s: fn(s, k)
+        e_s = const.tile([P, 2, 2, 4, P], F32, name="e_s")
+        for js in HALVES:
+            for u in range(2):
+                nc.scalar.activation(out=slot_major(e_s, js, u), in_=by_slot(wv_t, js, u), func=ACT.Exp, scale=0.5)
+        for k in range(3):
+            h_interleave(0, k)
+        load_h(AHEAD)
+        product(0, HALVES[0])
+        wm_f = const.tile([P, 4, P], F32, name="wm_f")
+        wm_u = const.tile([P, 2, 3, 256], BF16, name="wm_u")
+        nc.vector.tensor_copy(
+            out=wm_u[:].rearrange("p u j (b c) -> p u (j b) c", c=16),
+            in_=wm_t[:, 1:4, :].rearrange("p j (b u c) -> p u (j b) c", u=2, c=16),
+        )
+        nc.vector.tensor_copy(
+            out=wm_f[:].rearrange("p (u e) (b i) -> p u e b i", e=2, i=8),
+            in_=wm_t[:, 0, :].rearrange("p (b u i e) -> p u e b i", u=2, i=8, e=2),
+        )
+        product(0, HALVES[1])
+        load_we(AHEAD)
+        q_h(0)
+        product(1)
+        load_we(AHEAD + 1)
+        wm_tr = const.tile([P, 3, D1], BF16, name="wm_tr")
+        h_interleave(1, 0)
+        for j0, j1 in ((0, 2), (2, 3)):
+            bank = psum.tile([P, j1 - j0, 4, P], BF16, name="bank")
+            for j in range(j0, j1):
+                for t in range(4):
+                    nc.tensor.transpose(bank[:, j - j0, t, :], wm_u[:, t // 2, j, t % 2 :: 2], ident_b[:])
+            nc.scalar.copy(out=wm_tr[:, j0:j1, :], in_=bank[:].rearrange("p j t x -> p j (t x)"))
+        first = w_bank(0, 0)
+        h_interleave(1, 1)
+        first()
+        h_interleave(1, 2)
+        load_h(AHEAD + 1)
+        banks = [w_open(0, j) for j in range(1, 4)]
+        for j in range(1, 4):
+            w_close(0, j, banks[j - 1])()
+        mask(0)
+        load_zg(AHEAD)
+        q_h(1)
+        d_interleave(0)
+        h_interleave(2, 0)
+        for copy_out in [dz_bank(0, 0), dz_bank(0, 1)]:
+            copy_out()
+        q_w(0)
+        q_d(0)
+        q_t(0)
+        w_bank(1, 0)()
+        h_interleave(2, 1)
+        w_bank(1, 1)()
+        h_interleave(2, 2)
+        load_h(AHEAD + 2)
 
-        STEP = [
-            (sub(input_grad, 0), 0),
-            (sub(input_grad, 1), 0),
-            (sub(dz_transposes, 0), -1),
-            (sub(dz_transposes, 1), -1),
-            (sub(input_grad, 2), 0),
-            (sub(input_grad, 3), 0),
-            (product, -4),
-            (q_w, -1),
-            (sub(weight_grad, 1), 1),
-            (mask, -2),
-            (q_t, -1),
-            (load_we, -6),
-            (h_interleave, -2),
-            (sub(w_transposes, 0), -2),
-            (q_d, 0),
-            (q_h, 0),
-            (load_h, -4),
-            (sub(w_transposes, 1), -2),
-            (load_zg, -4),
-            (sub(weight_grad, 0), 1),
-            (sub(weight_grad, 3), 1),
-            (sub(w_transposes, 2), -2),
-            (sub(w_transposes, 3), -2),
-            (store, 0),
-            (sub(weight_grad, 2), 1),
-            (d_interleave, -2),
-        ]
+        for n in range(4, 4 * (S - 1)):
+            s, q = divmod(n, 4)
+            late = s == S - 2
+            if q == 0:
+                mask(s)
+                if s + AHEAD < S:
+                    load_zg(s + AHEAD)
+            if q == 1:
+                product(s + 1)
+                if s + 1 + AHEAD < S:
+                    load_we(s + 1 + AHEAD)
+            if q == 2:
+                if not late:
+                    d_interleave(s)
+                q_h(s + 1)
+            if q == 3:
+                if not late:
+                    q_d(s)
+                q_w(s)
+                q_t(s)
+            sw, j = divmod(n + 2, 4)
+            copies = [w_bank(sw, j)]
+            if q == 1:
+                copies.extend([dz_bank(s, 0), dz_bank(s, 1)])
+            for copy_out in copies:
+                copy_out()
+            input_grad(s - 1, q, nc.scalar.copy)
+            weight_grad(s - 1, q)
+            sh, k = divmod(n + 7, 4)
+            if k < 3 and 2 < sh < S:
+                h_interleave(sh, k)
+                if k == 2 and sh + AHEAD < S:
+                    load_h(sh + AHEAD)
 
-        with tc.manual_schedule():
-            warm = const.tile([P, 1], F32, name="warm")
-            nc.vector.memset(warm[:], 0.0)
-            nc.scalar.activation(out=warm[:], in_=warm[:], func=ACT.Exp)
-            wv_t = const.tile([P, 4, D2], BF16, name="wv_t")
-            wv_view = wv1.rearrange("(p j) w -> p j w", j=4)
-            we_t[0] = loads.tile([P, 4, D2], BF16, name="we")
-            we_view = we1[0].rearrange("(p j) w -> p j w", j=4)
-            for js in (slice(0, 2), slice(2, 4)):
-                nc.sync.dma_start(out=wv_t[:, js, :], in_=wv_view[:, js, :])
-                nc.sync.dma_start(out=we_t[0][:, js, :], in_=we_view[:, js, :])
-            wm_t = const.tile([P, 4, D2], BF16, name="wm_t")
-            nc.sync.dma_start(out=wm_t[:], in_=wm1.rearrange("(p j) w -> p j w", j=4))
-
-            e_s = const.tile([P, 4, 4, P], F32, name="e_s")
-            wm_s = const.tile([P, 4, 4, P], F32, name="wm_s")
-            for j in range(4):
-                nc.scalar.activation(
-                    out=e_s[:, j, :, :],
-                    in_=wv_t[:, j, :].rearrange("p (m t) -> p t m", t=4),
-                    func=ACT.Exp,
-                    scale=0.5,
-                )
-            for j in range(4):
-                nc.gpsimd.tensor_scalar(
-                    out=wm_s[:, j, :, :],
-                    in0=wm_t[:, j, :].rearrange("p (m t) -> p t m", t=4),
-                    scalar1=1.0,
-                    scalar2=0.0,
-                    op0=ALU.mult,
-                    op1=ALU.add,
-                )
-
-            for step in range(-6, S + 1):
-                for what, lag in STEP:
-                    s = step - lag
-                    if 0 <= s < S and not (what is load_we and s == 0):
-                        what(s)
+        last = S - 1
+        mask(last)
+        for j in (2, 3):
+            w_bank(last, j)()
+        input_grad(last - 1, 0, nc.scalar.copy)
+        d_interleave(last - 1)
+        for copy_out in [dz_bank(last, 0), dz_bank(last, 1)]:
+            copy_out()
+        q_w(last)
+        q_d(last - 1)
+        input_grad(last - 1, 1, nc.vector.tensor_copy)
+        q_t(last)
+        for j in (2, 3):
+            input_grad(last - 1, j, nc.scalar.copy)
+        d_interleave(last)
+        for j in range(4):
+            input_grad(last, j, nc.scalar.copy)
+            weight_grad(last - 1, j)
+        q_d(last)
+        for b in range(4):
+            weight_grad(last, b)
+            finish_weight_grad(b, (nc.vector.tensor_copy, nc.scalar.copy)[b % 2])

@@ -21,6 +21,9 @@ AHEAD = 4
 OUT_BUFS = 4
 H_CUTS = (0, 176, 344, 512)
 HALVES = (slice(0, 2), slice(2, 4))
+D_CUT = 208
+HALF = 2048
+FIRST, SECOND, BOTH = slice(0, 1), slice(1, 2), slice(0, 2)
 
 
 def tile_bnn_pb_v_kernel(tc, h0, wm1, wv1, bm1, bv1, we1, be1, z, grad_out, out_0, out_1):
@@ -42,8 +45,7 @@ def tile_bnn_pb_v_kernel(tc, h0, wm1, wv1, bm1, bv1, we1, be1, z, grad_out, out_
         acc = [acc_pool.tile([P, D2], F32, name="acc%d" % b) for b in range(4)]
 
         we_t, z_t, g_t, h_t = {}, {}, {}, {}
-        hi_t, di_t, p_t, wt_t, dz_t, dt_t = {}, {}, {}, {}, {}, {}
-        wq_t, dq_t, hq_t, tq_t, o_t = {}, {}, {}, {}, {}
+        p_t, dz_t, e4_t, e5_t, e4q_t, e5q_t, o_t = {}, {}, {}, {}, {}, {}, {}
 
         def rows(ap):
             return ap.rearrange("(p j) w -> p j w", j=4)
@@ -66,23 +68,32 @@ def tile_bnn_pb_v_kernel(tc, h0, wm1, wv1, bm1, bv1, we1, be1, z, grad_out, out_
             h_t[s] = loads.tile([P, 4, D1], BF16, name="h")
             nc.sync.dma_start(out=h_t[s][:], in_=rows(h0[s]))
 
-        def quantize(s, src, dtype, store, nm, bufs=2):
-            c = codes.tile([P, 512], U32, name=nm + "c", align_bytes=256, bufs=bufs)
-            q = codes.tile([P, 512], U8, name=nm + "s", align_bytes=256, bufs=bufs)
-            nc.vector.quantize_mx(out=c[:].bitcast(dtype), scales=q[:], in_=src)
-            store[s] = (c, q)
+        def e4_tile(s):
+            if s not in e4_t:
+                e4_t[s] = mid.tile([P, 2 * HALF], BF16, name="e4", align_bytes=256)
+            return e4_t[s]
 
-        def q_h(s):
-            quantize(s, hi_t[s][:].rearrange("p w j -> p (w j)"), E4M3, hq_t, "h", 3)
+        def e5_tile(s):
+            if s not in e5_t:
+                e5_t[s] = mid.tile([P, 2 * HALF], BF16, name="e5", align_bytes=256)
+            return e5_t[s]
 
-        def q_d(s):
-            quantize(s, di_t[s][:].rearrange("p w j -> p (w j)"), E5M2, dq_t, "d")
+        def quantize(src, parts, dtype, store, key, nm, bufs):
+            if key not in store:
+                c = codes.tile([P, 2 * 512], U32, name=nm + "c", align_bytes=256, bufs=bufs)
+                q = codes.tile([P, 2 * 512], U8, name=nm + "s", align_bytes=256, bufs=bufs)
+                store[key] = (c, q)
+            c, q = store[key]
+            words = slice(512 * parts.start, 512 * parts.stop)
+            nc.vector.quantize_mx(
+                out=c[:, words].bitcast(dtype), scales=q[:, words], in_=src[:, HALF * parts.start : HALF * parts.stop]
+            )
 
-        def q_w(s):
-            quantize(s, wt_t[s][:].rearrange("p j x t -> p (j x t)"), E4M3, wq_t, "w")
+        def q_e4(s, parts=BOTH):
+            quantize(e4_t[s], parts, E4M3, e4q_t, s, "e4", 3)
 
-        def q_t(s):
-            quantize(s, dt_t[s][:].rearrange("p j x u -> p (j x u)").bitcast(BF16), E5M2, tq_t, "t")
+        def q_e5(s, parts=BOTH):
+            quantize(e5_t[s], parts, E5M2, e5q_t, s, "e5", 2)
 
         def by_half_block(tile, js, u):
             return tile[:, js, :].rearrange("p j (b u c) -> p u (j b) c", u=2, c=16)[:, u, :, :]
@@ -106,19 +117,18 @@ def tile_bnn_pb_v_kernel(tc, h0, wm1, wv1, bm1, bv1, we1, be1, z, grad_out, out_
                         op1=ALU.mult,
                     )
 
-        def d_interleave(s):
-            di_t[s] = mid.tile([P, D2, 4], BF16, name="di", align_bytes=256)
-            nc.vector.tensor_copy(
-                out=di_t[s][:].rearrange("p (u c i) j -> p u c j i", u=2, i=4),
-                in_=dz_t[s][:].rearrange("p u j (c i) -> p u c j i", i=4),
+        def d_interleave(s, copy, lo, hi):
+            di = e5_tile(s)[:, HALF:].rearrange("p (u w j) -> p u w j", u=2, j=4)
+            copy(
+                out=di[:, :, lo:hi, :].rearrange("p u (c i) j -> p u c j i", i=4),
+                in_=dz_t[s][:, :, :, lo:hi].rearrange("p u j (c i) -> p u c j i", i=4),
             )
 
         def h_interleave(s, k):
-            if k == 0:
-                hi_t[s] = mid.tile([P, D1, 4], BF16, name="hi", align_bytes=256)
             cols = slice(H_CUTS[k], H_CUTS[k + 1])
+            hi = e4_tile(s - 1)[:, HALF + 4 * cols.start : HALF + 4 * cols.stop]
             nc.scalar.copy(
-                out=hi_t[s][:, cols, :].rearrange("p (c i) j -> p c j i", i=4),
+                out=hi.rearrange("p (c i j) -> p c j i", i=4, j=4),
                 in_=h_t[s][:, :, cols].rearrange("p j (c i) -> p c j i", i=4),
             )
 
@@ -131,8 +141,6 @@ def tile_bnn_pb_v_kernel(tc, h0, wm1, wv1, bm1, bv1, we1, be1, z, grad_out, out_
                 )
 
         def w_open(s, j):
-            if j == 0:
-                wt_t[s] = mid.tile([P, 4, P, 4], BF16, name="wt", align_bytes=256)
             bank = psum.tile([P, 4, P], F32, name="bank")
             if j > 0:
                 nc.tensor.matmul(
@@ -154,30 +162,30 @@ def tile_bnn_pb_v_kernel(tc, h0, wm1, wv1, bm1, bv1, we1, be1, z, grad_out, out_
                     start=False,
                     stop=(j == 0 or t == 3),
                 )
-            return lambda: nc.scalar.copy(out=wt_t[s][:, j, :, :], in_=bank[:].rearrange("p t x -> p x t"))
+            wt = e4_tile(s)[:, 512 * j : 512 * (j + 1)].rearrange("p (x t) -> p x t", t=4)
+            return lambda: nc.scalar.copy(out=wt, in_=bank[:].rearrange("p t x -> p x t"))
 
         def w_bank(s, j):
             return w_close(s, j, w_open(s, j))
 
         def dz_bank(s, half):
-            if half == 0:
-                dt_t[s] = mid.tile([P, 4, P, 2], F32, name="dt", align_bytes=256)
             bank = psum.tile([P, 2, 2, P], F32, name="bank")
             for k in range(2):
                 for u in range(2):
                     nc.tensor.transpose(bank[:, k, u, :], dz_t[s][:, u, 2 * half + k, :].bitcast(F32), ident_f[:])
-            return lambda: nc.scalar.copy(out=dt_t[s][:, HALVES[half], :, :], in_=bank[:].rearrange("p k u x -> p k x u"))
+            dt = e5_tile(s)[:, 1024 * half : 1024 * (half + 1)].bitcast(F32).rearrange("p (k x u) -> p k x u", k=2, u=2)
+            return lambda: nc.scalar.copy(out=dt, in_=bank[:].rearrange("p k u x -> p k x u"))
 
         def weight_grad(s, b):
-            hc, hs = hq_t[s]
-            dc, ds = dq_t[s]
-            cols = slice(P * b, P * (b + 1))
+            hc, hs = e4q_t[s - 1]
+            dc, ds = e5q_t[s]
+            cols = slice(512 + P * b, 512 + P * (b + 1))
             nc.tensor.matmul_mx(
                 out=acc[b][:],
                 lhsT=hc[:, cols].bitcast(E4M3),
                 lhsT_scale=hs[:, cols],
-                rhs=dc[:].bitcast(E5M2),
-                rhs_scale=ds[:],
+                rhs=dc[:, 512:].bitcast(E5M2),
+                rhs_scale=ds[:, 512:],
                 start=(s == 0),
                 stop=(s == S - 1),
             )
@@ -191,8 +199,8 @@ def tile_bnn_pb_v_kernel(tc, h0, wm1, wv1, bm1, bv1, we1, be1, z, grad_out, out_
             nc.sync.dma_start(out=out_1[P * b : P * (b + 1), :], in_=r[:])
 
         def input_grad(s, j, copy):
-            tcod, tsc = tq_t[s]
-            wc, ws = wq_t[s]
+            tcod, tsc = e5q_t[s]
+            wc, ws = e4q_t[s]
             if j == 0:
                 o_t[s] = outs.tile([P, 4, P, 4], F32, name="o")
             cols = slice(P * j, P * (j + 1))
@@ -201,8 +209,8 @@ def tile_bnn_pb_v_kernel(tc, h0, wm1, wv1, bm1, bv1, we1, be1, z, grad_out, out_
                 out=bank[:].rearrange("p t x -> p (t x)"),
                 lhsT=tcod[:, cols].bitcast(E5M2),
                 lhsT_scale=tsc[:, cols],
-                rhs=wc[:].bitcast(E4M3),
-                rhs_scale=ws[:],
+                rhs=wc[:, :512].bitcast(E4M3),
+                rhs_scale=ws[:, :512],
                 start=True,
                 stop=True,
             )
@@ -252,7 +260,7 @@ def tile_bnn_pb_v_kernel(tc, h0, wm1, wv1, bm1, bv1, we1, be1, z, grad_out, out_
         )
         product(0, HALVES[1])
         load_we(AHEAD)
-        q_h(0)
+        q_e4(-1, SECOND)
         product(1)
         load_we(AHEAD + 1)
         wm_tr = const.tile([P, 3, D1], BF16, name="wm_tr")
@@ -273,14 +281,13 @@ def tile_bnn_pb_v_kernel(tc, h0, wm1, wv1, bm1, bv1, we1, be1, z, grad_out, out_
             w_close(0, j, banks[j - 1])()
         mask(0)
         load_zg(AHEAD)
-        q_h(1)
-        d_interleave(0)
+        q_e4(0, SECOND)
+        d_interleave(0, nc.vector.tensor_copy, 0, 256)
         h_interleave(2, 0)
         for copy_out in [dz_bank(0, 0), dz_bank(0, 1)]:
             copy_out()
-        q_w(0)
-        q_d(0)
-        q_t(0)
+        q_e4(0, FIRST)
+        q_e5(0)
         w_bank(1, 0)()
         h_interleave(2, 1)
         w_bank(1, 1)()
@@ -298,15 +305,12 @@ def tile_bnn_pb_v_kernel(tc, h0, wm1, wv1, bm1, bv1, we1, be1, z, grad_out, out_
                 product(s + 1)
                 if s + 1 + AHEAD < S:
                     load_we(s + 1 + AHEAD)
-            if q == 2:
-                if not late:
-                    d_interleave(s)
-                q_h(s + 1)
+            if q == 2 and not late:
+                d_interleave(s, nc.vector.tensor_copy, 0, D_CUT)
+                d_interleave(s, nc.scalar.copy, D_CUT, 256)
             if q == 3:
-                if not late:
-                    q_d(s)
-                q_w(s)
-                q_t(s)
+                q_e4(s)
+                q_e5(s, FIRST if late else BOTH)
             sw, j = divmod(n + 2, 4)
             copies = [w_bank(sw, j)]
             if q == 1:
@@ -326,20 +330,20 @@ def tile_bnn_pb_v_kernel(tc, h0, wm1, wv1, bm1, bv1, we1, be1, z, grad_out, out_
         for j in (2, 3):
             w_bank(last, j)()
         input_grad(last - 1, 0, nc.scalar.copy)
-        d_interleave(last - 1)
+        d_interleave(last - 1, nc.vector.tensor_copy, 0, 256)
         for copy_out in [dz_bank(last, 0), dz_bank(last, 1)]:
             copy_out()
-        q_w(last)
-        q_d(last - 1)
+        q_e4(last, FIRST)
+        q_e5(last - 1, SECOND)
         input_grad(last - 1, 1, nc.vector.tensor_copy)
-        q_t(last)
+        q_e5(last, FIRST)
         for j in (2, 3):
             input_grad(last - 1, j, nc.scalar.copy)
-        d_interleave(last)
+        d_interleave(last, nc.vector.tensor_copy, 0, 256)
         for j in range(4):
             input_grad(last, j, nc.scalar.copy)
             weight_grad(last - 1, j)
-        q_d(last)
+        q_e5(last, SECOND)
         for b in range(4):
             weight_grad(last, b)
             finish_weight_grad(b, (nc.vector.tensor_copy, nc.scalar.copy)[b % 2])

@@ -20,14 +20,16 @@ P = 128
 AHEAD = 4
 OUT_BUFS = 4
 H_CUTS = (0, 176, 344, 512)
+W_ORDER = (1, 0, 2, 3)
+D_CUT = 448
+ROWS = slice(0, 4)
 HALVES = (slice(0, 2), slice(2, 4))
-D_CUT = 208
-HALF = 2048
-FIRST, SECOND, BOTH = slice(0, 1), slice(1, 2), slice(0, 2)
+COLS = 512
 
 
 def tile_bnn_pb_v_kernel(tc, h0, wm1, wv1, bm1, bv1, we1, be1, z, grad_out, out_0, out_1):
     nc = tc.nc
+    on_vector, on_scalar = nc.vector.tensor_copy, nc.scalar.copy
     with ExitStack() as ctx:
         const = ctx.enter_context(tc.tile_pool(name="const", bufs=1))
         loads = ctx.enter_context(tc.tile_pool(name="loads", bufs=AHEAD))
@@ -38,11 +40,11 @@ def tile_bnn_pb_v_kernel(tc, h0, wm1, wv1, bm1, bv1, we1, be1, z, grad_out, out_
         psum = ctx.enter_context(tc.psum_pool(name="psum", bufs=4))
         ctx.enter_context(tc.manual_schedule())
 
-        ident_f = const.tile([P, P], F32, name="ident_f")
-        make_identity(nc, ident_f[:])
         ident_b = const.tile([P, P], BF16, name="ident_b")
         make_identity(nc, ident_b[:])
-        acc = [acc_pool.tile([P, D2], F32, name="acc%d" % b) for b in range(4)]
+        ident_f = const.tile([P, P], F32, name="ident_f")
+        make_identity(nc, ident_f[:])
+        acc = [[acc_pool.tile([P, 2, 256], F32, name="acc%d%d" % (c, k)) for k in range(2)] for c in range(2)]
 
         we_t, z_t, g_t, h_t = {}, {}, {}, {}
         p_t, dz_t, e4_t, e5_t, e4q_t, e5q_t, o_t = {}, {}, {}, {}, {}, {}, {}
@@ -50,97 +52,71 @@ def tile_bnn_pb_v_kernel(tc, h0, wm1, wv1, bm1, bv1, we1, be1, z, grad_out, out_
         def rows(ap):
             return ap.rearrange("(p j) w -> p j w", j=4)
 
-        def row_pieces(s):
-            return HALVES if s == 0 else (slice(0, 4),)
+        def load(store, s, src, dtype, name, js=ROWS):
+            if js.start == 0:
+                store[s] = loads.tile([P, 4, COLS], dtype, name=name)
+            nc.sync.dma_start(out=store[s][:, js, :], in_=rows(src[s])[:, js, :])
 
-        def load_we(s):
-            we_t[s] = loads.tile([P, 4, D2], BF16, name="we")
-            nc.sync.dma_start(out=we_t[s][:], in_=rows(we1[s]))
-
-        def load_zg(s):
-            z_t[s] = loads.tile([P, 4, D2], F32, name="z")
-            g_t[s] = loads.tile([P, 4, D2], BF16, name="g")
-            for js in row_pieces(s):
-                nc.sync.dma_start(out=z_t[s][:, js, :], in_=rows(z[s])[:, js, :])
-                nc.sync.dma_start(out=g_t[s][:, js, :], in_=rows(grad_out[s])[:, js, :])
+        def load_we(s, js=ROWS):
+            if s < S:
+                load(we_t, s, we1, BF16, "we", js)
 
         def load_h(s):
-            h_t[s] = loads.tile([P, 4, D1], BF16, name="h")
-            nc.sync.dma_start(out=h_t[s][:], in_=rows(h0[s]))
+            if s < S:
+                load(h_t, s, h0, BF16, "h")
 
-        def e4_tile(s):
-            if s not in e4_t:
-                e4_t[s] = mid.tile([P, 2 * HALF], BF16, name="e4", align_bytes=256)
-            return e4_t[s]
+        def load_zg(s, js=ROWS):
+            if s < S:
+                load(z_t, s, z, F32, "z", js)
+                load(g_t, s, grad_out, BF16, "g", js)
 
-        def e5_tile(s):
-            if s not in e5_t:
-                e5_t[s] = mid.tile([P, 2 * HALF], BF16, name="e5", align_bytes=256)
-            return e5_t[s]
+        def pair_tile(store, s, name):
+            if s not in store:
+                store[s] = mid.tile([P, 2 * COLS * 4], BF16, name=name, align_bytes=256)
+            return store[s]
 
-        def quantize(src, parts, dtype, store, key, nm, bufs):
-            if key not in store:
-                c = codes.tile([P, 2 * 512], U32, name=nm + "c", align_bytes=256, bufs=bufs)
-                q = codes.tile([P, 2 * 512], U8, name=nm + "s", align_bytes=256, bufs=bufs)
-                store[key] = (c, q)
-            c, q = store[key]
-            words = slice(512 * parts.start, 512 * parts.stop)
-            nc.vector.quantize_mx(
-                out=c[:, words].bitcast(dtype), scales=q[:, words], in_=src[:, HALF * parts.start : HALF * parts.stop]
+        def quantize(src, lo, hi, dtype, store, s, name, bufs):
+            if s not in store:
+                c = codes.tile([P, 2 * COLS], U32, name=name + "c", align_bytes=256, bufs=bufs)
+                q = codes.tile([P, 2 * COLS], U8, name=name + "s", align_bytes=256, bufs=bufs)
+                store[s] = (c, q)
+            c, q = store[s]
+            nc.vector.quantize_mx(out=c[:, lo:hi].bitcast(dtype), scales=q[:, lo:hi], in_=src[:, 4 * lo : 4 * hi])
+
+        def q_e4(s, lo=0, hi=2 * COLS):
+            quantize(e4_t[s], lo, hi, E4M3, e4q_t, s, "e4", 3)
+
+        def q_e5(s, lo=0, hi=2 * COLS):
+            quantize(e5_t[s], lo, hi, E5M2, e5q_t, s, "e5", 2)
+
+        def by_slot(tile, js):
+            return tile[:, js, :].rearrange("p j (m t) -> p j t m", t=4)
+
+        def mask(s, js=ROWS):
+            if js.start == 0:
+                dz_t[s] = mid.tile([P, 4, D2], BF16, name="dz", align_bytes=256)
+            nc.vector.scalar_tensor_tensor(
+                out=dz_t[s][:, js, :], in0=z_t[s][:, js, :], scalar=0.0, in1=g_t[s][:, js, :], op0=ALU.is_gt, op1=ALU.mult
             )
 
-        def q_e4(s, parts=BOTH):
-            quantize(e4_t[s], parts, E4M3, e4q_t, s, "e4", 3)
-
-        def q_e5(s, parts=BOTH):
-            quantize(e5_t[s], parts, E5M2, e5q_t, s, "e5", 2)
-
-        def by_half_block(tile, js, u):
-            return tile[:, js, :].rearrange("p j (b u c) -> p u (j b) c", u=2, c=16)[:, u, :, :]
-
-        def by_slot(tile, js, u):
-            return tile[:, js, :].rearrange("p j (b u i e) -> p u e (j b) i", u=2, i=8, e=2)[:, u, :, :, :]
-
-        def slot_major(tile, js, u):
-            return tile[:, u, :, js, :].rearrange("p e j (b i) -> p e (j b) i", i=8)
-
-        def mask(s):
-            dz_t[s] = mid.tile([P, 2, 4, 256], BF16, name="dz", align_bytes=256)
-            for js in row_pieces(s):
-                for u in range(2):
-                    nc.vector.scalar_tensor_tensor(
-                        out=dz_t[s][:, u, js, :].rearrange("p j (b c) -> p (j b) c", c=16),
-                        in0=by_half_block(z_t[s], js, u),
-                        scalar=0.0,
-                        in1=by_half_block(g_t[s], js, u),
-                        op0=ALU.is_gt,
-                        op1=ALU.mult,
-                    )
+        def interleave(copy, pair, src, lo, hi):
+            copy(
+                out=pair[:, 4 * (COLS + lo) : 4 * (COLS + hi)].rearrange("p (c i j) -> p c j i", i=4, j=4),
+                in_=src[:, :, lo:hi].rearrange("p j (c i) -> p c j i", i=4),
+            )
 
         def d_interleave(s, copy, lo, hi):
-            di = e5_tile(s)[:, HALF:].rearrange("p (u w j) -> p u w j", u=2, j=4)
-            copy(
-                out=di[:, :, lo:hi, :].rearrange("p u (c i) j -> p u c j i", i=4),
-                in_=dz_t[s][:, :, :, lo:hi].rearrange("p u j (c i) -> p u c j i", i=4),
-            )
+            interleave(copy, pair_tile(e5_t, s, "e5"), dz_t[s], lo, hi)
 
-        def h_interleave(s, k):
-            cols = slice(H_CUTS[k], H_CUTS[k + 1])
-            hi = e4_tile(s - 1)[:, HALF + 4 * cols.start : HALF + 4 * cols.stop]
-            nc.scalar.copy(
-                out=hi.rearrange("p (c i j) -> p c j i", i=4, j=4),
-                in_=h_t[s][:, :, cols].rearrange("p j (c i) -> p c j i", i=4),
-            )
+        def h_interleave(s, copy, lo, hi):
+            interleave(copy, pair_tile(e4_t, s - 1, "e4"), h_t[s], lo, hi)
 
-        def product(s, js=slice(0, 4)):
+        def product(s, js=ROWS):
             if js.start == 0:
-                p_t[s] = mid.tile([P, 2, 2, 4, P], F32, name="p")
-            for u in range(2):
-                nc.vector.tensor_tensor(
-                    out=slot_major(p_t[s], js, u), in0=by_slot(we_t[s], js, u), in1=slot_major(e_s, js, u), op=ALU.mult
-                )
+                p_t[s] = mid.tile([P, 4, 4, P], F32, name="p")
+            nc.vector.tensor_tensor(out=p_t[s][:, js, :, :], in0=by_slot(we_t[s], js), in1=e_s[:, js, :, :], op=ALU.mult)
 
-        def w_open(s, j):
+        def w_open(j):
             bank = psum.tile([P, 4, P], F32, name="bank")
             if j > 0:
                 nc.tensor.matmul(
@@ -156,49 +132,51 @@ def tile_bnn_pb_v_kernel(tc, h0, wm1, wv1, bm1, bv1, we1, be1, z, grad_out, out_
                     )
                 nc.tensor.matmul(
                     bank[:, t, :],
-                    lhsT=p_t[s][:, t // 2, t % 2, j, :],
+                    lhsT=p_t[s][:, j, t, :],
                     rhs=ident_f[:],
                     is_transpose=True,
                     start=False,
                     stop=(j == 0 or t == 3),
                 )
-            wt = e4_tile(s)[:, 512 * j : 512 * (j + 1)].rearrange("p (x t) -> p x t", t=4)
-            return lambda: nc.scalar.copy(out=wt, in_=bank[:].rearrange("p t x -> p x t"))
+            wt = pair_tile(e4_t, s, "e4")[:, 512 * j : 512 * (j + 1)].rearrange("p (x t) -> p x t", t=4)
+            return lambda: on_scalar(out=wt, in_=bank[:].rearrange("p t x -> p x t"))
 
         def w_bank(s, j):
-            return w_close(s, j, w_open(s, j))
+            return w_close(s, j, w_open(j))
 
         def dz_bank(s, half):
             bank = psum.tile([P, 2, 2, P], F32, name="bank")
             for k in range(2):
+                words = dz_t[s][:, 2 * half + k, :].bitcast(F32)
                 for u in range(2):
-                    nc.tensor.transpose(bank[:, k, u, :], dz_t[s][:, u, 2 * half + k, :].bitcast(F32), ident_f[:])
-            dt = e5_tile(s)[:, 1024 * half : 1024 * (half + 1)].bitcast(F32).rearrange("p (k x u) -> p k x u", k=2, u=2)
-            return lambda: nc.scalar.copy(out=dt, in_=bank[:].rearrange("p k u x -> p k x u"))
+                    nc.tensor.transpose(bank[:, k, u, :], words[:, u::2], ident_f[:])
+            dt = pair_tile(e5_t, s, "e5")[:, 1024 * half : 1024 * (half + 1)].bitcast(F32)
+            return lambda: on_scalar(
+                out=dt.rearrange("p (k x u) -> p k x u", k=2, u=2), in_=bank[:].rearrange("p k u x -> p k x u")
+            )
 
-        def weight_grad(s, b):
+        def weight_grad(s, b, c):
             hc, hs = e4q_t[s - 1]
             dc, ds = e5q_t[s]
-            cols = slice(512 + P * b, 512 + P * (b + 1))
+            hcols = slice(COLS + P * b, COLS + P * (b + 1))
+            dcols = slice(COLS + 256 * c, COLS + 256 * (c + 1))
             nc.tensor.matmul_mx(
-                out=acc[b][:],
-                lhsT=hc[:, cols].bitcast(E4M3),
-                lhsT_scale=hs[:, cols],
-                rhs=dc[:, 512:].bitcast(E5M2),
-                rhs_scale=ds[:, 512:],
-                start=(s == 0),
-                stop=(s == S - 1),
+                out=acc[c][b // 2][:, b % 2, :],
+                lhsT=hc[:, hcols].bitcast(E4M3),
+                lhsT_scale=hs[:, hcols],
+                rhs=dc[:, dcols].bitcast(E5M2),
+                rhs_scale=ds[:, dcols],
+                start=(s == 0 and b % 2 == 0),
+                stop=(s == S - 1 and b % 2 == 1),
             )
 
-        def finish_weight_grad(b, copy):
-            r = const.tile([P, D2], F32, name="r%d" % b)
-            copy(
-                out=r[:].rearrange("p (b u c) -> p b u c", u=2, c=16),
-                in_=acc[b][:].rearrange("p (u b c) -> p b u c", u=2, c=16),
-            )
-            nc.sync.dma_start(out=out_1[P * b : P * (b + 1), :], in_=r[:])
+        def finish_weight_grad(c, k, copy):
+            r = const.tile([P, 2, 256], F32, name="r%d%d" % (c, k))
+            copy(out=r[:], in_=acc[c][k][:])
+            dst = out_1[256 * k : 256 * (k + 1), 256 * c : 256 * (c + 1)]
+            nc.sync.dma_start(out=dst.rearrange("(b p) w -> p b w", p=P), in_=r[:])
 
-        def input_grad(s, j, copy):
+        def input_grad(s, j, copy=on_scalar):
             tcod, tsc = e5q_t[s]
             wc, ws = e4q_t[s]
             if j == 0:
@@ -209,29 +187,26 @@ def tile_bnn_pb_v_kernel(tc, h0, wm1, wv1, bm1, bv1, we1, be1, z, grad_out, out_
                 out=bank[:].rearrange("p t x -> p (t x)"),
                 lhsT=tcod[:, cols].bitcast(E5M2),
                 lhsT_scale=tsc[:, cols],
-                rhs=wc[:, :512].bitcast(E4M3),
-                rhs_scale=ws[:, :512],
+                rhs=wc[:, :COLS].bitcast(E4M3),
+                rhs_scale=ws[:, :COLS],
                 start=True,
                 stop=True,
             )
             copy(out=o_t[s][:, j, :, :], in_=bank[:].rearrange("p t x -> p x t"))
-            store_rows(s, slice(j, j + 1))
-
-        def store_rows(s, js):
-            nc.sync.dma_start(out=rows(out_0[s])[:, js, :], in_=o_t[s][:, js, :, :].rearrange("p j x t -> p j (x t)"))
+            nc.sync.dma_start(out=rows(out_0[s])[:, j, :], in_=o_t[s][:, j, :, :].rearrange("p x t -> p (x t)"))
 
         wv_t = const.tile([P, 4, D2], BF16, name="wv_t")
-        for js in HALVES:
-            nc.sync.dma_start(out=wv_t[:, js, :], in_=rows(wv1)[:, js, :])
-        load_h(0)
-        we_t[0] = loads.tile([P, 4, D2], BF16, name="we")
         wm_t = const.tile([P, 4, D2], BF16, name="wm_t")
-        nc.sync.dma_start(out=we_t[0][:, HALVES[0], :], in_=rows(we1[0])[:, HALVES[0], :])
+        nc.sync.dma_start(out=wv_t[:, HALVES[0], :], in_=rows(wv1)[:, HALVES[0], :])
         nc.sync.dma_start(out=wm_t[:], in_=rows(wm1))
-        nc.sync.dma_start(out=we_t[0][:, HALVES[1], :], in_=rows(we1[0])[:, HALVES[1], :])
+        nc.sync.dma_start(out=wv_t[:, HALVES[1], :], in_=rows(wv1)[:, HALVES[1], :])
+        load_h(0)
+        for js in HALVES:
+            load_we(0, js)
         load_h(1)
         load_we(1)
-        load_zg(0)
+        for js in HALVES:
+            load_zg(0, js)
         load_h(2)
         for s in range(1, AHEAD):
             load_zg(s)
@@ -240,110 +215,112 @@ def tile_bnn_pb_v_kernel(tc, h0, wm1, wv1, bm1, bv1, we1, be1, z, grad_out, out_
             if s + 2 < AHEAD:
                 load_h(s + 2)
 
-        e_s = const.tile([P, 2, 2, 4, P], F32, name="e_s")
+        e_s = const.tile([P, 4, 4, P], F32, name="e_s")
         for js in HALVES:
-            for u in range(2):
-                nc.scalar.activation(out=slot_major(e_s, js, u), in_=by_slot(wv_t, js, u), func=ACT.Exp, scale=0.5)
-        for k in range(3):
-            h_interleave(0, k)
-        load_h(AHEAD)
-        product(0, HALVES[0])
+            nc.scalar.activation(out=e_s[:, js, :, :], in_=by_slot(wv_t, js), func=ACT.Exp, scale=0.5)
         wm_f = const.tile([P, 4, P], F32, name="wm_f")
-        wm_u = const.tile([P, 2, 3, 256], BF16, name="wm_u")
-        nc.vector.tensor_copy(
-            out=wm_u[:].rearrange("p u j (b c) -> p u (j b) c", c=16),
-            in_=wm_t[:, 1:4, :].rearrange("p j (b u c) -> p u (j b) c", u=2, c=16),
-        )
-        nc.vector.tensor_copy(
-            out=wm_f[:].rearrange("p (u e) (b i) -> p u e b i", e=2, i=8),
-            in_=wm_t[:, 0, :].rearrange("p (b u i e) -> p u e b i", u=2, i=8, e=2),
-        )
-        product(0, HALVES[1])
-        load_we(AHEAD)
-        q_e4(-1, SECOND)
-        product(1)
-        load_we(AHEAD + 1)
+        on_vector(out=wm_f[:], in_=wm_t[:, 0, :].rearrange("p (m t) -> p t m", t=4))
+        h_interleave(0, on_vector, 0, 256)
+        h_interleave(0, on_scalar, 256, 512)
+        load_h(AHEAD)
         wm_tr = const.tile([P, 3, D1], BF16, name="wm_tr")
-        h_interleave(1, 0)
-        for j0, j1 in ((0, 2), (2, 3)):
+        for j0, j1 in ((1, 3), (3, 4)):
             bank = psum.tile([P, j1 - j0, 4, P], BF16, name="bank")
             for j in range(j0, j1):
                 for t in range(4):
-                    nc.tensor.transpose(bank[:, j - j0, t, :], wm_u[:, t // 2, j, t % 2 :: 2], ident_b[:])
-            nc.scalar.copy(out=wm_tr[:, j0:j1, :], in_=bank[:].rearrange("p j t x -> p j (t x)"))
+                    nc.tensor.transpose(bank[:, j - j0, t, :], wm_t[:, j, t::4], ident_b[:])
+            on_scalar(out=wm_tr[:, j0 - 1 : j1 - 1, :], in_=bank[:].rearrange("p j t x -> p j (t x)"))
+        for js in HALVES:
+            product(0, js)
+        load_we(AHEAD)
+        q_e4(-1, COLS)
+        product(1)
+        load_we(AHEAD + 1)
         first = w_bank(0, 0)
-        h_interleave(1, 1)
+        h_interleave(1, on_scalar, H_CUTS[0], H_CUTS[1])
         first()
-        h_interleave(1, 2)
+        h_interleave(1, on_scalar, H_CUTS[1], H_CUTS[3])
         load_h(AHEAD + 1)
-        banks = [w_open(0, j) for j in range(1, 4)]
+        banks = [w_open(j) for j in range(1, 4)]
         for j in range(1, 4):
             w_close(0, j, banks[j - 1])()
-        mask(0)
+        for js in HALVES:
+            mask(0, js)
         load_zg(AHEAD)
-        q_e4(0, SECOND)
-        d_interleave(0, nc.vector.tensor_copy, 0, 256)
-        h_interleave(2, 0)
+        q_e4(0)
+        d_interleave(0, on_vector, 0, D_CUT)
+        w_bank(1, W_ORDER[0])()
+        h_interleave(2, on_scalar, H_CUTS[0], H_CUTS[1])
         for copy_out in [dz_bank(0, 0), dz_bank(0, 1)]:
             copy_out()
-        q_e4(0, FIRST)
+        d_interleave(0, on_scalar, D_CUT, D2)
         q_e5(0)
-        w_bank(1, 0)()
-        h_interleave(2, 1)
-        w_bank(1, 1)()
-        h_interleave(2, 2)
+        h_interleave(2, on_scalar, H_CUTS[1], H_CUTS[2])
+        w_bank(1, W_ORDER[1])()
+        h_interleave(2, on_scalar, H_CUTS[2], H_CUTS[3])
         load_h(AHEAD + 2)
+
+        def products(s, q):
+            input_grad(s, q)
+            for c in range(2):
+                weight_grad(s, q, c)
 
         for n in range(4, 4 * (S - 1)):
             s, q = divmod(n, 4)
             late = s == S - 2
             if q == 0:
                 mask(s)
-                if s + AHEAD < S:
-                    load_zg(s + AHEAD)
+                load_zg(s + AHEAD)
             if q == 1:
                 product(s + 1)
-                if s + 1 + AHEAD < S:
-                    load_we(s + 1 + AHEAD)
+                load_we(s + 1 + AHEAD)
+                if not late:
+                    d_interleave(s, on_scalar, D_CUT, D2)
             if q == 2 and not late:
-                d_interleave(s, nc.vector.tensor_copy, 0, D_CUT)
-                d_interleave(s, nc.scalar.copy, D_CUT, 256)
+                d_interleave(s, on_vector, 0, D_CUT)
             if q == 3:
                 q_e4(s)
-                q_e5(s, FIRST if late else BOTH)
-            sw, j = divmod(n + 2, 4)
-            copies = [w_bank(sw, j)]
+                q_e5(s, 0, COLS if late else 2 * COLS)
+            sw, k = divmod(n + 2, 4)
+            w_bank(sw, W_ORDER[k])()
+            products(s - 1, q)
             if q == 1:
-                copies.extend([dz_bank(s, 0), dz_bank(s, 1)])
-            for copy_out in copies:
-                copy_out()
-            input_grad(s - 1, q, nc.scalar.copy)
-            weight_grad(s - 1, q)
+                for copy_out in [dz_bank(s, 0), dz_bank(s, 1)]:
+                    copy_out()
             sh, k = divmod(n + 7, 4)
             if k < 3 and 2 < sh < S:
-                h_interleave(sh, k)
-                if k == 2 and sh + AHEAD < S:
+                h_interleave(sh, on_scalar, H_CUTS[k], H_CUTS[k + 1])
+                if k == 2:
                     load_h(sh + AHEAD)
 
         last = S - 1
         mask(last)
-        for j in (2, 3):
-            w_bank(last, j)()
-        input_grad(last - 1, 0, nc.scalar.copy)
-        d_interleave(last - 1, nc.vector.tensor_copy, 0, 256)
+        for k in (2, 3):
+            w_bank(last, W_ORDER[k])()
+            input_grad(last - 1, k - 2)
+        d_interleave(last - 1, on_vector, 0, 256)
         for copy_out in [dz_bank(last, 0), dz_bank(last, 1)]:
             copy_out()
-        q_e4(last, FIRST)
-        q_e5(last - 1, SECOND)
-        input_grad(last - 1, 1, nc.vector.tensor_copy)
-        q_e5(last, FIRST)
+        d_interleave(last, on_vector, 0, 256)
+        q_e5(last - 1, COLS, COLS + 256)
+        q_e4(last, 0, COLS)
+        q_e5(last, COLS, COLS + 256)
+        q_e5(last, 0, COLS)
         for j in (2, 3):
-            input_grad(last - 1, j, nc.scalar.copy)
-        d_interleave(last, nc.vector.tensor_copy, 0, 256)
-        for j in range(4):
-            input_grad(last, j, nc.scalar.copy)
-            weight_grad(last - 1, j)
-        q_e5(last, SECOND)
+            input_grad(last - 1, j)
         for b in range(4):
-            weight_grad(last, b)
-            finish_weight_grad(b, (nc.vector.tensor_copy, nc.scalar.copy)[b % 2])
+            for s in (last - 1, last):
+                weight_grad(s, b, 0)
+        d_interleave(last - 1, on_vector, 256, D2)
+        d_interleave(last, on_vector, 256, D2)
+        for k in range(2):
+            finish_weight_grad(0, k, on_scalar)
+        for s in (last - 1, last):
+            q_e5(s, COLS + 256)
+        for j in range(4):
+            input_grad(last, j, on_vector if j == 2 else on_scalar)
+        for b in range(4):
+            for s in (last - 1, last):
+                weight_grad(s, b, 1)
+        finish_weight_grad(1, 0, on_vector)
+        finish_weight_grad(1, 1, on_vector)

@@ -21,7 +21,8 @@ AHEAD = 4
 OUT_BUFS = 4
 H_CUTS = (0, 176, 344, 512)
 W_ORDER = (1, 0, 2, 3)
-D_CUT = 448
+RUN = 4
+D_CUT = 80
 ROWS = slice(0, 4)
 HALVES = (slice(0, 2), slice(2, 4))
 COLS = 512
@@ -89,32 +90,49 @@ def tile_bnn_pb_v_kernel(tc, h0, wm1, wv1, bm1, bv1, we1, be1, z, grad_out, out_
         def q_e5(s, lo=0, hi=2 * COLS):
             quantize(e5_t[s], lo, hi, E5M2, e5q_t, s, "e5", 2)
 
-        def by_slot(tile, js):
-            return tile[:, js, :].rearrange("p j (m t) -> p j t m", t=4)
+        def by_half_block(tile, js, u):
+            return tile[:, js, :].rearrange("p j (b u c) -> p u (j b) c", u=2, c=16)[:, u, :, :]
+
+        def by_slot(tile, js, u):
+            return tile[:, js, :].rearrange("p j (b u i e) -> p u e (j b) i", u=2, i=8, e=2)[:, u, :, :, :]
+
+        def slot_major(tile, js, u):
+            return tile[:, u, :, js, :].rearrange("p e j (b i) -> p e (j b) i", i=8)
 
         def mask(s, js=ROWS):
             if js.start == 0:
-                dz_t[s] = mid.tile([P, 4, D2], BF16, name="dz", align_bytes=256)
-            nc.vector.scalar_tensor_tensor(
-                out=dz_t[s][:, js, :], in0=z_t[s][:, js, :], scalar=0.0, in1=g_t[s][:, js, :], op0=ALU.is_gt, op1=ALU.mult
-            )
+                dz_t[s] = mid.tile([P, 2, 4, 256], BF16, name="dz", align_bytes=256)
+            for u in range(2):
+                nc.vector.scalar_tensor_tensor(
+                    out=dz_t[s][:, u, js, :].rearrange("p j (b c) -> p (j b) c", c=16),
+                    in0=by_half_block(z_t[s], js, u),
+                    scalar=0.0,
+                    in1=by_half_block(g_t[s], js, u),
+                    op0=ALU.is_gt,
+                    op1=ALU.mult,
+                )
 
-        def interleave(copy, pair, src, lo, hi):
+        def d_interleave(s, copy, c, lo=0, hi=P):
+            di = pair_tile(e5_t, s, "e5")[:, 4 * COLS :].rearrange("p (c u w j) -> p c u w j", c=2, u=2, j=4)
             copy(
-                out=pair[:, 4 * (COLS + lo) : 4 * (COLS + hi)].rearrange("p (c i j) -> p c j i", i=4, j=4),
-                in_=src[:, :, lo:hi].rearrange("p j (c i) -> p c j i", i=4),
+                out=di[:, c, :, lo:hi, :].rearrange("p u (n i) j -> p u n j i", i=RUN),
+                in_=dz_t[s][:, :, :, P * c + lo : P * c + hi].rearrange("p u j (n i) -> p u n j i", i=RUN),
             )
-
-        def d_interleave(s, copy, lo, hi):
-            interleave(copy, pair_tile(e5_t, s, "e5"), dz_t[s], lo, hi)
 
         def h_interleave(s, copy, lo, hi):
-            interleave(copy, pair_tile(e4_t, s - 1, "e4"), h_t[s], lo, hi)
+            pair = pair_tile(e4_t, s - 1, "e4")
+            copy(
+                out=pair[:, 4 * (COLS + lo) : 4 * (COLS + hi)].rearrange("p (n i j) -> p n j i", i=RUN, j=4),
+                in_=h_t[s][:, :, lo:hi].rearrange("p j (n i) -> p n j i", i=RUN),
+            )
 
         def product(s, js=ROWS):
             if js.start == 0:
-                p_t[s] = mid.tile([P, 4, 4, P], F32, name="p")
-            nc.vector.tensor_tensor(out=p_t[s][:, js, :, :], in0=by_slot(we_t[s], js), in1=e_s[:, js, :, :], op=ALU.mult)
+                p_t[s] = mid.tile([P, 2, 2, 4, P], F32, name="p")
+            for u in range(2):
+                nc.vector.tensor_tensor(
+                    out=slot_major(p_t[s], js, u), in0=by_slot(we_t[s], js, u), in1=slot_major(e_s, js, u), op=ALU.mult
+                )
 
         def w_open(j):
             bank = psum.tile([P, 4, P], F32, name="bank")
@@ -132,7 +150,7 @@ def tile_bnn_pb_v_kernel(tc, h0, wm1, wv1, bm1, bv1, we1, be1, z, grad_out, out_
                     )
                 nc.tensor.matmul(
                     bank[:, t, :],
-                    lhsT=p_t[s][:, j, t, :],
+                    lhsT=p_t[s][:, t // 2, t % 2, j, :],
                     rhs=ident_f[:],
                     is_transpose=True,
                     start=False,
@@ -147,9 +165,8 @@ def tile_bnn_pb_v_kernel(tc, h0, wm1, wv1, bm1, bv1, we1, be1, z, grad_out, out_
         def dz_bank(s, half):
             bank = psum.tile([P, 2, 2, P], F32, name="bank")
             for k in range(2):
-                words = dz_t[s][:, 2 * half + k, :].bitcast(F32)
                 for u in range(2):
-                    nc.tensor.transpose(bank[:, k, u, :], words[:, u::2], ident_f[:])
+                    nc.tensor.transpose(bank[:, k, u, :], dz_t[s][:, u, 2 * half + k, :].bitcast(F32), ident_f[:])
             dt = pair_tile(e5_t, s, "e5")[:, 1024 * half : 1024 * (half + 1)].bitcast(F32)
             return lambda: on_scalar(
                 out=dt.rearrange("p (k x u) -> p k x u", k=2, u=2), in_=bank[:].rearrange("p k u x -> p k x u")
@@ -172,7 +189,10 @@ def tile_bnn_pb_v_kernel(tc, h0, wm1, wv1, bm1, bv1, we1, be1, z, grad_out, out_
 
         def finish_weight_grad(c, k, copy):
             r = const.tile([P, 2, 256], F32, name="r%d%d" % (c, k))
-            copy(out=r[:], in_=acc[c][k][:])
+            copy(
+                out=r[:].rearrange("p k (b u i) -> p k b u i", u=2, i=16),
+                in_=acc[c][k][:].rearrange("p k (u b i) -> p k b u i", u=2, i=16),
+            )
             dst = out_1[256 * k : 256 * (k + 1), 256 * c : 256 * (c + 1)]
             nc.sync.dma_start(out=dst.rearrange("(b p) w -> p b w", p=P), in_=r[:])
 
@@ -215,21 +235,30 @@ def tile_bnn_pb_v_kernel(tc, h0, wm1, wv1, bm1, bv1, we1, be1, z, grad_out, out_
             if s + 2 < AHEAD:
                 load_h(s + 2)
 
-        e_s = const.tile([P, 4, 4, P], F32, name="e_s")
+        e_s = const.tile([P, 2, 2, 4, P], F32, name="e_s")
         for js in HALVES:
-            nc.scalar.activation(out=e_s[:, js, :, :], in_=by_slot(wv_t, js), func=ACT.Exp, scale=0.5)
+            for u in range(2):
+                nc.scalar.activation(out=slot_major(e_s, js, u), in_=by_slot(wv_t, js, u), func=ACT.Exp, scale=0.5)
+        wm_u = const.tile([P, 2, 3, 256], BF16, name="wm_u")
+        on_vector(
+            out=wm_u[:].rearrange("p u j (b c) -> p u (j b) c", c=16),
+            in_=wm_t[:, 1:4, :].rearrange("p j (b u c) -> p u (j b) c", u=2, c=16),
+        )
         wm_f = const.tile([P, 4, P], F32, name="wm_f")
-        on_vector(out=wm_f[:], in_=wm_t[:, 0, :].rearrange("p (m t) -> p t m", t=4))
+        on_vector(
+            out=wm_f[:].rearrange("p (u e) (b i) -> p u e b i", e=2, i=8),
+            in_=wm_t[:, 0, :].rearrange("p (b u i e) -> p u e b i", u=2, i=8, e=2),
+        )
         h_interleave(0, on_vector, 0, 256)
         h_interleave(0, on_scalar, 256, 512)
         load_h(AHEAD)
         wm_tr = const.tile([P, 3, D1], BF16, name="wm_tr")
-        for j0, j1 in ((1, 3), (3, 4)):
+        for j0, j1 in ((0, 2), (2, 3)):
             bank = psum.tile([P, j1 - j0, 4, P], BF16, name="bank")
             for j in range(j0, j1):
                 for t in range(4):
-                    nc.tensor.transpose(bank[:, j - j0, t, :], wm_t[:, j, t::4], ident_b[:])
-            on_scalar(out=wm_tr[:, j0 - 1 : j1 - 1, :], in_=bank[:].rearrange("p j t x -> p j (t x)"))
+                    nc.tensor.transpose(bank[:, j - j0, t, :], wm_u[:, t // 2, j, t % 2 :: 2], ident_b[:])
+            on_scalar(out=wm_tr[:, j0:j1, :], in_=bank[:].rearrange("p j t x -> p j (t x)"))
         for js in HALVES:
             product(0, js)
         load_we(AHEAD)
@@ -248,12 +277,13 @@ def tile_bnn_pb_v_kernel(tc, h0, wm1, wv1, bm1, bv1, we1, be1, z, grad_out, out_
             mask(0, js)
         load_zg(AHEAD)
         q_e4(0)
-        d_interleave(0, on_vector, 0, D_CUT)
+        d_interleave(0, on_vector, 0)
+        d_interleave(0, on_vector, 1, 0, D_CUT)
         w_bank(1, W_ORDER[0])()
         h_interleave(2, on_scalar, H_CUTS[0], H_CUTS[1])
         for copy_out in [dz_bank(0, 0), dz_bank(0, 1)]:
             copy_out()
-        d_interleave(0, on_scalar, D_CUT, D2)
+        d_interleave(0, on_scalar, 1, D_CUT)
         q_e5(0)
         h_interleave(2, on_scalar, H_CUTS[1], H_CUTS[2])
         w_bank(1, W_ORDER[1])()
@@ -275,9 +305,10 @@ def tile_bnn_pb_v_kernel(tc, h0, wm1, wv1, bm1, bv1, we1, be1, z, grad_out, out_
                 product(s + 1)
                 load_we(s + 1 + AHEAD)
                 if not late:
-                    d_interleave(s, on_scalar, D_CUT, D2)
+                    d_interleave(s, on_scalar, 1, D_CUT)
             if q == 2 and not late:
-                d_interleave(s, on_vector, 0, D_CUT)
+                d_interleave(s, on_vector, 0)
+                d_interleave(s, on_vector, 1, 0, D_CUT)
             if q == 3:
                 q_e4(s)
                 q_e5(s, 0, COLS if late else 2 * COLS)
@@ -298,10 +329,10 @@ def tile_bnn_pb_v_kernel(tc, h0, wm1, wv1, bm1, bv1, we1, be1, z, grad_out, out_
         for k in (2, 3):
             w_bank(last, W_ORDER[k])()
             input_grad(last - 1, k - 2)
-        d_interleave(last - 1, on_vector, 0, 256)
+        d_interleave(last - 1, on_vector, 0)
         for copy_out in [dz_bank(last, 0), dz_bank(last, 1)]:
             copy_out()
-        d_interleave(last, on_vector, 0, 256)
+        d_interleave(last, on_vector, 0)
         q_e5(last - 1, COLS, COLS + 256)
         q_e4(last, 0, COLS)
         q_e5(last, COLS, COLS + 256)
@@ -311,8 +342,8 @@ def tile_bnn_pb_v_kernel(tc, h0, wm1, wv1, bm1, bv1, we1, be1, z, grad_out, out_
         for b in range(4):
             for s in (last - 1, last):
                 weight_grad(s, b, 0)
-        d_interleave(last - 1, on_vector, 256, D2)
-        d_interleave(last, on_vector, 256, D2)
+        d_interleave(last - 1, on_vector, 1)
+        d_interleave(last, on_vector, 1)
         for k in range(2):
             finish_weight_grad(0, k, on_scalar)
         for s in (last - 1, last):
@@ -322,5 +353,5 @@ def tile_bnn_pb_v_kernel(tc, h0, wm1, wv1, bm1, bv1, we1, be1, z, grad_out, out_
         for b in range(4):
             for s in (last - 1, last):
                 weight_grad(s, b, 1)
-        finish_weight_grad(1, 0, on_vector)
+        finish_weight_grad(1, 0, on_scalar)
         finish_weight_grad(1, 1, on_vector)

@@ -22,6 +22,8 @@ OUT_BUFS = 4
 H_CUTS = (0, 176, 344, 512)
 W_ORDER = (1, 0, 2, 3)
 RUN = 4
+LATE = 5
+H7_CUT = 256
 D_CUT = 80
 ROWS = slice(0, 4)
 HALVES = (slice(0, 2), slice(2, 4))
@@ -73,7 +75,8 @@ def tile_bnn_pb_v_kernel(tc, h0, wm1, wv1, bm1, bv1, we1, be1, z, grad_out, out_
 
         def pair_tile(store, s, name):
             if s not in store:
-                store[s] = mid.tile([P, 2 * COLS * 4], BF16, name=name, align_bytes=256)
+                bufs = 3 if name == "e5" else 2
+                store[s] = mid.tile([P, 2 * COLS * 4], BF16, name=name, align_bytes=256, bufs=bufs)
             return store[s]
 
         def quantize(src, lo, hi, dtype, store, s, name, bufs):
@@ -85,10 +88,10 @@ def tile_bnn_pb_v_kernel(tc, h0, wm1, wv1, bm1, bv1, we1, be1, z, grad_out, out_
             nc.vector.quantize_mx(out=c[:, lo:hi].bitcast(dtype), scales=q[:, lo:hi], in_=src[:, 4 * lo : 4 * hi])
 
         def q_e4(s, lo=0, hi=2 * COLS):
-            quantize(e4_t[s], lo, hi, E4M3, e4q_t, s, "e4", 3)
+            quantize(e4_t[s], lo, hi, E4M3, e4q_t, s, "e4", 4)
 
         def q_e5(s, lo=0, hi=2 * COLS):
-            quantize(e5_t[s], lo, hi, E5M2, e5q_t, s, "e5", 2)
+            quantize(e5_t[s], lo, hi, E5M2, e5q_t, s, "e5", 4)
 
         def by_half_block(tile, js, u):
             return tile[:, js, :].rearrange("p j (b u c) -> p u (j b) c", u=2, c=16)[:, u, :, :]
@@ -101,7 +104,7 @@ def tile_bnn_pb_v_kernel(tc, h0, wm1, wv1, bm1, bv1, we1, be1, z, grad_out, out_
 
         def mask(s, js=ROWS):
             if js.start == 0:
-                dz_t[s] = mid.tile([P, 2, 4, 256], BF16, name="dz", align_bytes=256)
+                dz_t[s] = mid.tile([P, 2, 4, 256], BF16, name="dz", align_bytes=256, bufs=3)
             for u in range(2):
                 nc.vector.scalar_tensor_tensor(
                     out=dz_t[s][:, u, js, :].rearrange("p j (b c) -> p (j b) c", c=16),
@@ -188,7 +191,7 @@ def tile_bnn_pb_v_kernel(tc, h0, wm1, wv1, bm1, bv1, we1, be1, z, grad_out, out_
             )
 
         def finish_weight_grad(c, k, copy):
-            r = const.tile([P, 2, 256], F32, name="r%d%d" % (c, k))
+            r = loads.tile([P, 2, 256], F32, name="we")
             copy(
                 out=r[:].rearrange("p k (b u i) -> p k b u i", u=2, i=16),
                 in_=acc[c][k][:].rearrange("p k (u b i) -> p k b u i", u=2, i=16),
@@ -213,10 +216,13 @@ def tile_bnn_pb_v_kernel(tc, h0, wm1, wv1, bm1, bv1, we1, be1, z, grad_out, out_
                 stop=True,
             )
             copy(out=o_t[s][:, j, :, :], in_=bank[:].rearrange("p t x -> p x t"))
-            nc.sync.dma_start(out=rows(out_0[s])[:, j, :], in_=o_t[s][:, j, :, :].rearrange("p x t -> p (x t)"))
+            n = 2 if s < LATE else 1
+            if (j + 1) % n == 0:
+                js = slice(j + 1 - n, j + 1)
+                nc.sync.dma_start(out=rows(out_0[s])[:, js, :], in_=o_t[s][:, js, :, :].rearrange("p j x t -> p j (x t)"))
 
-        wv_t = const.tile([P, 4, D2], BF16, name="wv_t")
-        wm_t = const.tile([P, 4, D2], BF16, name="wm_t")
+        wv_t = mid.tile([P, 4, D2], BF16, name="dz", align_bytes=256, bufs=3)
+        wm_t = mid.tile([P, 4, D2], BF16, name="dz", align_bytes=256, bufs=3)
         nc.sync.dma_start(out=wv_t[:, HALVES[0], :], in_=rows(wv1)[:, HALVES[0], :])
         nc.sync.dma_start(out=wm_t[:], in_=rows(wm1))
         nc.sync.dma_start(out=wv_t[:, HALVES[1], :], in_=rows(wv1)[:, HALVES[1], :])
@@ -297,7 +303,7 @@ def tile_bnn_pb_v_kernel(tc, h0, wm1, wv1, bm1, bv1, we1, be1, z, grad_out, out_
 
         for n in range(4, 4 * (S - 1)):
             s, q = divmod(n, 4)
-            late = s == S - 2
+            late = s >= LATE
             if q == 0:
                 mask(s)
                 load_zg(s + AHEAD)
@@ -310,48 +316,62 @@ def tile_bnn_pb_v_kernel(tc, h0, wm1, wv1, bm1, bv1, we1, be1, z, grad_out, out_
                 d_interleave(s, on_vector, 0)
                 d_interleave(s, on_vector, 1, 0, D_CUT)
             if q == 3:
-                q_e4(s)
+                q_e4(s, 0, COLS if s == S - 2 else 2 * COLS)
+                if s == S - 2:
+                    h_interleave(s + 1, on_vector, 0, H7_CUT)
                 q_e5(s, 0, COLS if late else 2 * COLS)
             sw, k = divmod(n + 2, 4)
             w_bank(sw, W_ORDER[k])()
-            products(s - 1, q)
+            if s - 1 < LATE:
+                products(s - 1, q)
+            else:
+                input_grad(s - 1, q)
             if q == 1:
                 for copy_out in [dz_bank(s, 0), dz_bank(s, 1)]:
                     copy_out()
             sh, k = divmod(n + 7, 4)
-            if k < 3 and 2 < sh < S:
+            if k < 3 and 2 < sh < S - 1:
                 h_interleave(sh, on_scalar, H_CUTS[k], H_CUTS[k + 1])
                 if k == 2:
                     load_h(sh + AHEAD)
 
         last = S - 1
+        late_samples = range(LATE, S)
         mask(last)
         for k in (2, 3):
             w_bank(last, W_ORDER[k])()
             input_grad(last - 1, k - 2)
-        d_interleave(last - 1, on_vector, 0)
+        for s in late_samples[:-1]:
+            d_interleave(s, on_vector, 0)
         for copy_out in [dz_bank(last, 0), dz_bank(last, 1)]:
             copy_out()
-        d_interleave(last, on_vector, 0)
-        q_e5(last - 1, COLS, COLS + 256)
+        q_e5(LATE, COLS, COLS + 256)
         q_e4(last, 0, COLS)
-        q_e5(last, COLS, COLS + 256)
+        q_e5(last - 1, COLS, COLS + 256)
+        d_interleave(last, on_vector, 0)
         q_e5(last, 0, COLS)
         for j in (2, 3):
             input_grad(last - 1, j)
-        for b in range(4):
-            for s in (last - 1, last):
+        for s in late_samples[:-1]:
+            for b in range(4):
                 weight_grad(s, b, 0)
-        d_interleave(last - 1, on_vector, 1)
-        d_interleave(last, on_vector, 1)
-        for k in range(2):
-            finish_weight_grad(0, k, on_scalar)
-        for s in (last - 1, last):
-            q_e5(s, COLS + 256)
+        h_interleave(last, on_scalar, H7_CUT, D1)
+        q_e5(last, COLS, COLS + 256)
         for j in range(4):
-            input_grad(last, j, on_vector if j == 2 else on_scalar)
+            input_grad(last, j)
+        d_interleave(LATE, on_vector, 1)
+        q_e4(last - 1, COLS)
         for b in range(4):
-            for s in (last - 1, last):
-                weight_grad(s, b, 1)
+            weight_grad(last, b, 0)
+        for s in late_samples[1:]:
+            d_interleave(s, on_vector, 1)
+            q_e5(s - 1, COLS + 256)
+            for b in range(4):
+                weight_grad(s - 1, b, 1)
+        finish_weight_grad(0, 0, on_scalar)
+        q_e5(last, COLS + 256)
+        finish_weight_grad(0, 1, on_vector)
+        for b in range(4):
+            weight_grad(last, b, 1)
         finish_weight_grad(1, 0, on_scalar)
         finish_weight_grad(1, 1, on_vector)

@@ -17,17 +17,17 @@ ALU = mybir.AluOpType
 ACT = mybir.ActivationFunctionType
 
 P = 128
+COLS = 512
+HALF = 256
+ROWS = slice(0, 4)
+ROW_HALVES = (slice(0, 2), slice(2, 4))
 AHEAD = 4
 OUT_BUFS = 4
-H_CUTS = (0, 176, 344, 512)
-W_ORDER = (1, 0, 2, 3)
 RUN = 4
-LATE = 5
-H7_CUT = 256
+H_CUTS = (0, 176, 344, 512)
 D_CUT = 80
-ROWS = slice(0, 4)
-HALVES = (slice(0, 2), slice(2, 4))
-COLS = 512
+LATE = 5
+W_ORDER = (1, 0, 2, 3)
 
 
 def tile_bnn_pb_v_kernel(tc, h0, wm1, wv1, bm1, bv1, we1, be1, z, grad_out, out_0, out_1):
@@ -47,7 +47,7 @@ def tile_bnn_pb_v_kernel(tc, h0, wm1, wv1, bm1, bv1, we1, be1, z, grad_out, out_
         make_identity(nc, ident_b[:])
         ident_f = const.tile([P, P], F32, name="ident_f")
         make_identity(nc, ident_f[:])
-        acc = [[acc_pool.tile([P, 2, 256], F32, name="acc%d%d" % (c, k)) for k in range(2)] for c in range(2)]
+        acc = [[acc_pool.tile([P, 2, HALF], F32, name="acc%d%d" % (c, k)) for k in range(2)] for c in range(2)]
 
         we_t, z_t, g_t, h_t = {}, {}, {}, {}
         p_t, dz_t, e4_t, e5_t, e4q_t, e5q_t, o_t = {}, {}, {}, {}, {}, {}, {}
@@ -73,41 +73,47 @@ def tile_bnn_pb_v_kernel(tc, h0, wm1, wv1, bm1, bv1, we1, be1, z, grad_out, out_
                 load(z_t, s, z, F32, "z", js)
                 load(g_t, s, grad_out, BF16, "g", js)
 
-        def pair_tile(store, s, name):
-            if s not in store:
-                bufs = 3 if name == "e5" else 2
-                store[s] = mid.tile([P, 2 * COLS * 4], BF16, name=name, align_bytes=256, bufs=bufs)
-            return store[s]
+        def e4_tile(s):
+            if s not in e4_t:
+                e4_t[s] = mid.tile([P, 2 * COLS * 4], BF16, name="e4", align_bytes=256, bufs=2)
+            return e4_t[s]
 
-        def quantize(src, lo, hi, dtype, store, s, name, bufs):
+        def e5_tile(s):
+            if s not in e5_t:
+                e5_t[s] = mid.tile([P, 2 * COLS * 4], BF16, name="e5", align_bytes=256, bufs=S - LATE)
+            return e5_t[s]
+
+        def quantize(src, lo, hi, dtype, store, s, name):
             if s not in store:
-                c = codes.tile([P, 2 * COLS], U32, name=name + "c", align_bytes=256, bufs=bufs)
-                q = codes.tile([P, 2 * COLS], U8, name=name + "s", align_bytes=256, bufs=bufs)
-                store[s] = (c, q)
-            c, q = store[s]
-            nc.vector.quantize_mx(out=c[:, lo:hi].bitcast(dtype), scales=q[:, lo:hi], in_=src[:, 4 * lo : 4 * hi])
+                words = codes.tile([P, 2 * COLS], U32, name=name + "c", align_bytes=256, bufs=S - LATE + 1)
+                scales = codes.tile([P, 2 * COLS], U8, name=name + "s", align_bytes=256, bufs=S - LATE + 1)
+                store[s] = (words, scales)
+            words, scales = store[s]
+            nc.vector.quantize_mx(
+                out=words[:, lo:hi].bitcast(dtype), scales=scales[:, lo:hi], in_=src[:, 4 * lo : 4 * hi]
+            )
 
         def q_e4(s, lo=0, hi=2 * COLS):
-            quantize(e4_t[s], lo, hi, E4M3, e4q_t, s, "e4", 4)
+            quantize(e4_t[s], lo, hi, E4M3, e4q_t, s, "e4")
 
         def q_e5(s, lo=0, hi=2 * COLS):
-            quantize(e5_t[s], lo, hi, E5M2, e5q_t, s, "e5", 4)
+            quantize(e5_t[s], lo, hi, E5M2, e5q_t, s, "e5")
 
         def by_half_block(tile, js, u):
-            return tile[:, js, :].rearrange("p j (b u c) -> p u (j b) c", u=2, c=16)[:, u, :, :]
+            return tile[:, js, :].rearrange("p j (b u f) -> p u (j b) f", u=2, f=16)[:, u, :, :]
 
-        def by_slot(tile, js, u):
+        def by_position(tile, js, u):
             return tile[:, js, :].rearrange("p j (b u i e) -> p u e (j b) i", u=2, i=8, e=2)[:, u, :, :, :]
 
-        def slot_major(tile, js, u):
+        def position_major(tile, js, u):
             return tile[:, u, :, js, :].rearrange("p e j (b i) -> p e (j b) i", i=8)
 
         def mask(s, js=ROWS):
             if js.start == 0:
-                dz_t[s] = mid.tile([P, 2, 4, 256], BF16, name="dz", align_bytes=256, bufs=3)
+                dz_t[s] = mid.tile([P, 2, 4, 256], BF16, name="dz", align_bytes=256, bufs=S - LATE)
             for u in range(2):
                 nc.vector.scalar_tensor_tensor(
-                    out=dz_t[s][:, u, js, :].rearrange("p j (b c) -> p (j b) c", c=16),
+                    out=dz_t[s][:, u, js, :].rearrange("p j (b f) -> p (j b) f", f=16),
                     in0=by_half_block(z_t[s], js, u),
                     scalar=0.0,
                     in1=by_half_block(g_t[s], js, u),
@@ -116,17 +122,17 @@ def tile_bnn_pb_v_kernel(tc, h0, wm1, wv1, bm1, bv1, we1, be1, z, grad_out, out_
                 )
 
         def d_interleave(s, copy, c, lo=0, hi=P):
-            di = pair_tile(e5_t, s, "e5")[:, 4 * COLS :].rearrange("p (c u w j) -> p c u w j", c=2, u=2, j=4)
+            di = e5_tile(s)[:, 4 * COLS :].rearrange("p (c u w j) -> p c u w j", c=2, u=2, j=4)
             copy(
-                out=di[:, c, :, lo:hi, :].rearrange("p u (n i) j -> p u n j i", i=RUN),
-                in_=dz_t[s][:, :, :, P * c + lo : P * c + hi].rearrange("p u j (n i) -> p u n j i", i=RUN),
+                out=di[:, c, :, lo:hi, :].rearrange("p u (n r) j -> p u n j r", r=RUN),
+                in_=dz_t[s][:, :, :, P * c + lo : P * c + hi].rearrange("p u j (n r) -> p u n j r", r=RUN),
             )
 
         def h_interleave(s, copy, lo, hi):
-            pair = pair_tile(e4_t, s - 1, "e4")
+            pair = e4_tile(s - 1)
             copy(
-                out=pair[:, 4 * (COLS + lo) : 4 * (COLS + hi)].rearrange("p (n i j) -> p n j i", i=RUN, j=4),
-                in_=h_t[s][:, :, lo:hi].rearrange("p j (n i) -> p n j i", i=RUN),
+                out=pair[:, 4 * (COLS + lo) : 4 * (COLS + hi)].rearrange("p (n r j) -> p n j r", r=RUN, j=4),
+                in_=h_t[s][:, :, lo:hi].rearrange("p j (n r) -> p n j r", r=RUN),
             )
 
         def product(s, js=ROWS):
@@ -134,15 +140,17 @@ def tile_bnn_pb_v_kernel(tc, h0, wm1, wv1, bm1, bv1, we1, be1, z, grad_out, out_
                 p_t[s] = mid.tile([P, 2, 2, 4, P], F32, name="p")
             for u in range(2):
                 nc.vector.tensor_tensor(
-                    out=slot_major(p_t[s], js, u), in0=by_slot(we_t[s], js, u), in1=slot_major(e_s, js, u), op=ALU.mult
+                    out=position_major(p_t[s], js, u),
+                    in0=by_position(we_t[s], js, u),
+                    in1=position_major(e_s, js, u),
+                    op=ALU.mult,
                 )
 
         def w_open(j):
             bank = psum.tile([P, 4, P], F32, name="bank")
             if j > 0:
-                nc.tensor.matmul(
-                    bank[:].rearrange("p t x -> p (t x)"), lhsT=ident_b[:], rhs=wm_tr[:, j - 1, :], start=True, stop=False
-                )
+                whole = bank[:].rearrange("p t x -> p (t x)")
+                nc.tensor.matmul(whole, lhsT=ident_b[:], rhs=wm_tr[:, j - 1, :], start=True, stop=False)
             return bank
 
         def w_close(s, j, bank):
@@ -159,7 +167,7 @@ def tile_bnn_pb_v_kernel(tc, h0, wm1, wv1, bm1, bv1, we1, be1, z, grad_out, out_
                     start=False,
                     stop=(j == 0 or t == 3),
                 )
-            wt = pair_tile(e4_t, s, "e4")[:, 512 * j : 512 * (j + 1)].rearrange("p (x t) -> p x t", t=4)
+            wt = e4_tile(s)[:, COLS * j : COLS * (j + 1)].rearrange("p (x t) -> p x t", t=4)
             return lambda: on_scalar(out=wt, in_=bank[:].rearrange("p t x -> p x t"))
 
         def w_bank(s, j):
@@ -170,68 +178,74 @@ def tile_bnn_pb_v_kernel(tc, h0, wm1, wv1, bm1, bv1, we1, be1, z, grad_out, out_
             for k in range(2):
                 for u in range(2):
                     nc.tensor.transpose(bank[:, k, u, :], dz_t[s][:, u, 2 * half + k, :].bitcast(F32), ident_f[:])
-            dt = pair_tile(e5_t, s, "e5")[:, 1024 * half : 1024 * (half + 1)].bitcast(F32)
+            dt = e5_tile(s)[:, 2 * COLS * half : 2 * COLS * (half + 1)].bitcast(F32)
             return lambda: on_scalar(
                 out=dt.rearrange("p (k x u) -> p k x u", k=2, u=2), in_=bank[:].rearrange("p k u x -> p k x u")
             )
 
-        def weight_grad(s, b, c):
+        def weight_grad(s, blk, c):
             hc, hs = e4q_t[s - 1]
             dc, ds = e5q_t[s]
-            hcols = slice(COLS + P * b, COLS + P * (b + 1))
-            dcols = slice(COLS + 256 * c, COLS + 256 * (c + 1))
+            hcols = slice(COLS + P * blk, COLS + P * (blk + 1))
+            dcols = slice(COLS + HALF * c, COLS + HALF * (c + 1))
             nc.tensor.matmul_mx(
-                out=acc[c][b // 2][:, b % 2, :],
+                out=acc[c][blk // 2][:, blk % 2, :],
                 lhsT=hc[:, hcols].bitcast(E4M3),
                 lhsT_scale=hs[:, hcols],
                 rhs=dc[:, dcols].bitcast(E5M2),
                 rhs_scale=ds[:, dcols],
-                start=(s == 0 and b % 2 == 0),
-                stop=(s == S - 1 and b % 2 == 1),
+                start=(s == 0 and blk % 2 == 0),
+                stop=(s == S - 1 and blk % 2 == 1),
             )
 
-        def finish_weight_grad(c, k, copy):
-            r = loads.tile([P, 2, 256], F32, name="we")
+        def finish_weight_grad(c, k, copy, queue):
+            result = loads.tile([P, 2, HALF], F32, name="we")
             copy(
-                out=r[:].rearrange("p k (b u i) -> p k b u i", u=2, i=16),
-                in_=acc[c][k][:].rearrange("p k (u b i) -> p k b u i", u=2, i=16),
+                out=result[:].rearrange("p k (b u f) -> p k b u f", u=2, f=16),
+                in_=acc[c][k][:].rearrange("p k (u b f) -> p k b u f", u=2, f=16),
             )
-            dst = out_1[256 * k : 256 * (k + 1), 256 * c : 256 * (c + 1)]
-            nc.sync.dma_start(out=dst.rearrange("(b p) w -> p b w", p=P), in_=r[:])
+            dst = out_1[2 * P * k : 2 * P * (k + 1), HALF * c : HALF * (c + 1)]
+            queue.dma_start(out=dst.rearrange("(k p) w -> p k w", p=P), in_=result[:])
 
-        def input_grad(s, j, copy=on_scalar):
-            tcod, tsc = e5q_t[s]
+        def input_grad(s, j):
+            dc, ds = e5q_t[s]
             wc, ws = e4q_t[s]
             if j == 0:
                 o_t[s] = outs.tile([P, 4, P, 4], F32, name="o")
             cols = slice(P * j, P * (j + 1))
             bank = psum.tile([P, 4, P], F32, name="bank")
             nc.tensor.matmul_mx(
-                out=bank[:].rearrange("p t x -> p (t x)"),
-                lhsT=tcod[:, cols].bitcast(E5M2),
-                lhsT_scale=tsc[:, cols],
+                out=bank[:].rearrange("p w x -> p (w x)"),
+                lhsT=dc[:, cols].bitcast(E5M2),
+                lhsT_scale=ds[:, cols],
                 rhs=wc[:, :COLS].bitcast(E4M3),
                 rhs_scale=ws[:, :COLS],
                 start=True,
                 stop=True,
             )
-            copy(out=o_t[s][:, j, :, :], in_=bank[:].rearrange("p t x -> p x t"))
-            n = 2 if s < LATE else 1
-            if (j + 1) % n == 0:
-                js = slice(j + 1 - n, j + 1)
-                nc.sync.dma_start(out=rows(out_0[s])[:, js, :], in_=o_t[s][:, js, :, :].rearrange("p j x t -> p j (x t)"))
+            on_scalar(out=o_t[s][:, j, :, :], in_=bank[:].rearrange("p w x -> p x w"))
+            rows_a_store = 2 if s < LATE else 1
+            if (j + 1) % rows_a_store == 0:
+                js = slice(j + 1 - rows_a_store, j + 1)
+                src = o_t[s][:, js, :, :].rearrange("p j x w -> p j (x w)")
+                nc.sync.dma_start(out=rows(out_0[s])[:, js, :], in_=src)
 
-        wv_t = mid.tile([P, 4, D2], BF16, name="dz", align_bytes=256, bufs=3)
-        wm_t = mid.tile([P, 4, D2], BF16, name="dz", align_bytes=256, bufs=3)
-        nc.sync.dma_start(out=wv_t[:, HALVES[0], :], in_=rows(wv1)[:, HALVES[0], :])
+        def both_grads(s, q):
+            input_grad(s, q)
+            for c in range(2):
+                weight_grad(s, q, c)
+
+        wv_t = mid.tile([P, 4, D2], BF16, name="dz", align_bytes=256, bufs=S - LATE)
+        wm_t = mid.tile([P, 4, D2], BF16, name="dz", align_bytes=256, bufs=S - LATE)
+        nc.sync.dma_start(out=wv_t[:, ROW_HALVES[0], :], in_=rows(wv1)[:, ROW_HALVES[0], :])
         nc.sync.dma_start(out=wm_t[:], in_=rows(wm1))
-        nc.sync.dma_start(out=wv_t[:, HALVES[1], :], in_=rows(wv1)[:, HALVES[1], :])
+        nc.sync.dma_start(out=wv_t[:, ROW_HALVES[1], :], in_=rows(wv1)[:, ROW_HALVES[1], :])
         load_h(0)
-        for js in HALVES:
+        for js in ROW_HALVES:
             load_we(0, js)
         load_h(1)
         load_we(1)
-        for js in HALVES:
+        for js in ROW_HALVES:
             load_zg(0, js)
         load_h(2)
         for s in range(1, AHEAD):
@@ -242,21 +256,23 @@ def tile_bnn_pb_v_kernel(tc, h0, wm1, wv1, bm1, bv1, we1, be1, z, grad_out, out_
                 load_h(s + 2)
 
         e_s = const.tile([P, 2, 2, 4, P], F32, name="e_s")
-        for js in HALVES:
+        for js in ROW_HALVES:
             for u in range(2):
-                nc.scalar.activation(out=slot_major(e_s, js, u), in_=by_slot(wv_t, js, u), func=ACT.Exp, scale=0.5)
+                nc.scalar.activation(
+                    out=position_major(e_s, js, u), in_=by_position(wv_t, js, u), func=ACT.Exp, scale=0.5
+                )
         wm_u = const.tile([P, 2, 3, 256], BF16, name="wm_u")
         on_vector(
-            out=wm_u[:].rearrange("p u j (b c) -> p u (j b) c", c=16),
-            in_=wm_t[:, 1:4, :].rearrange("p j (b u c) -> p u (j b) c", u=2, c=16),
+            out=wm_u[:].rearrange("p u j (b f) -> p u (j b) f", f=16),
+            in_=wm_t[:, 1:4, :].rearrange("p j (b u f) -> p u (j b) f", u=2, f=16),
         )
         wm_f = const.tile([P, 4, P], F32, name="wm_f")
         on_vector(
             out=wm_f[:].rearrange("p (u e) (b i) -> p u e b i", e=2, i=8),
             in_=wm_t[:, 0, :].rearrange("p (b u i e) -> p u e b i", u=2, i=8, e=2),
         )
-        h_interleave(0, on_vector, 0, 256)
-        h_interleave(0, on_scalar, 256, 512)
+        h_interleave(0, on_vector, 0, D1 // 2)
+        h_interleave(0, on_scalar, D1 // 2, D1)
         load_h(AHEAD)
         wm_tr = const.tile([P, 3, D1], BF16, name="wm_tr")
         for j0, j1 in ((0, 2), (2, 3)):
@@ -265,7 +281,7 @@ def tile_bnn_pb_v_kernel(tc, h0, wm1, wv1, bm1, bv1, we1, be1, z, grad_out, out_
                 for t in range(4):
                     nc.tensor.transpose(bank[:, j - j0, t, :], wm_u[:, t // 2, j, t % 2 :: 2], ident_b[:])
             on_scalar(out=wm_tr[:, j0:j1, :], in_=bank[:].rearrange("p j t x -> p j (t x)"))
-        for js in HALVES:
+        for js in ROW_HALVES:
             product(0, js)
         load_we(AHEAD)
         q_e4(-1, COLS)
@@ -279,7 +295,7 @@ def tile_bnn_pb_v_kernel(tc, h0, wm1, wv1, bm1, bv1, we1, be1, z, grad_out, out_
         banks = [w_open(j) for j in range(1, 4)]
         for j in range(1, 4):
             w_close(0, j, banks[j - 1])()
-        for js in HALVES:
+        for js in ROW_HALVES:
             mask(0, js)
         load_zg(AHEAD)
         q_e4(0)
@@ -296,11 +312,6 @@ def tile_bnn_pb_v_kernel(tc, h0, wm1, wv1, bm1, bv1, we1, be1, z, grad_out, out_
         h_interleave(2, on_scalar, H_CUTS[2], H_CUTS[3])
         load_h(AHEAD + 2)
 
-        def products(s, q):
-            input_grad(s, q)
-            for c in range(2):
-                weight_grad(s, q, c)
-
         for n in range(4, 4 * (S - 1)):
             s, q = divmod(n, 4)
             late = s >= LATE
@@ -316,62 +327,62 @@ def tile_bnn_pb_v_kernel(tc, h0, wm1, wv1, bm1, bv1, we1, be1, z, grad_out, out_
                 d_interleave(s, on_vector, 0)
                 d_interleave(s, on_vector, 1, 0, D_CUT)
             if q == 3:
-                q_e4(s, 0, COLS if s == S - 2 else 2 * COLS)
-                if s == S - 2:
-                    h_interleave(s + 1, on_vector, 0, H7_CUT)
+                before_last = s == S - 2
+                q_e4(s, 0, COLS if before_last else 2 * COLS)
+                if before_last:
+                    h_interleave(s + 1, on_vector, 0, D1 // 2)
                 q_e5(s, 0, COLS if late else 2 * COLS)
-            sw, k = divmod(n + 2, 4)
-            w_bank(sw, W_ORDER[k])()
+            w_sample, w_step = divmod(n + 2, 4)
+            w_bank(w_sample, W_ORDER[w_step])()
             if s - 1 < LATE:
-                products(s - 1, q)
+                both_grads(s - 1, q)
             else:
                 input_grad(s - 1, q)
             if q == 1:
                 for copy_out in [dz_bank(s, 0), dz_bank(s, 1)]:
                     copy_out()
-            sh, k = divmod(n + 7, 4)
-            if k < 3 and 2 < sh < S - 1:
-                h_interleave(sh, on_scalar, H_CUTS[k], H_CUTS[k + 1])
-                if k == 2:
-                    load_h(sh + AHEAD)
+            if q > 0 and s + 2 < S - 1:
+                h_interleave(s + 2, on_scalar, H_CUTS[q - 1], H_CUTS[q])
+                if q == 3:
+                    load_h(s + 2 + AHEAD)
 
         last = S - 1
         late_samples = range(LATE, S)
         mask(last)
-        for k in (2, 3):
-            w_bank(last, W_ORDER[k])()
-            input_grad(last - 1, k - 2)
+        for j in range(2):
+            w_bank(last, W_ORDER[j + 2])()
+            input_grad(last - 1, j)
         for s in late_samples[:-1]:
             d_interleave(s, on_vector, 0)
         for copy_out in [dz_bank(last, 0), dz_bank(last, 1)]:
             copy_out()
-        q_e5(LATE, COLS, COLS + 256)
+        q_e5(LATE, COLS, COLS + HALF)
         q_e4(last, 0, COLS)
-        q_e5(last - 1, COLS, COLS + 256)
+        q_e5(last - 1, COLS, COLS + HALF)
         d_interleave(last, on_vector, 0)
         q_e5(last, 0, COLS)
         for j in (2, 3):
             input_grad(last - 1, j)
         for s in late_samples[:-1]:
-            for b in range(4):
-                weight_grad(s, b, 0)
-        h_interleave(last, on_scalar, H7_CUT, D1)
-        q_e5(last, COLS, COLS + 256)
+            for blk in range(4):
+                weight_grad(s, blk, 0)
+        h_interleave(last, on_scalar, D1 // 2, D1)
+        q_e5(last, COLS, COLS + HALF)
         for j in range(4):
             input_grad(last, j)
         d_interleave(LATE, on_vector, 1)
         q_e4(last - 1, COLS)
-        for b in range(4):
-            weight_grad(last, b, 0)
+        for blk in range(4):
+            weight_grad(last, blk, 0)
         for s in late_samples[1:]:
             d_interleave(s, on_vector, 1)
-            q_e5(s - 1, COLS + 256)
-            for b in range(4):
-                weight_grad(s - 1, b, 1)
-        finish_weight_grad(0, 0, on_scalar)
-        q_e5(last, COLS + 256)
-        finish_weight_grad(0, 1, on_vector)
-        for b in range(4):
-            weight_grad(last, b, 1)
-        finish_weight_grad(1, 0, on_scalar)
-        finish_weight_grad(1, 1, on_vector)
+            q_e5(s - 1, COLS + HALF)
+            for blk in range(4):
+                weight_grad(s - 1, blk, 1)
+        finish_weight_grad(0, 0, on_scalar, nc.scalar)
+        q_e5(last, COLS + HALF)
+        finish_weight_grad(0, 1, on_vector, nc.sync)
+        for blk in range(4):
+            weight_grad(last, blk, 1)
+        finish_weight_grad(1, 0, on_scalar, nc.scalar)
+        finish_weight_grad(1, 1, on_vector, nc.sync)

@@ -24,10 +24,18 @@ ROW_HALVES = (slice(0, 2), slice(2, 4))
 AHEAD = 4
 OUT_BUFS = 4
 RUN = 4
-H_CUTS = (0, 176, 344, 512)
-D_CUT = 80
-LATE = 5
-W_ORDER = (1, 0, 2, 3)
+D_CUT = 288
+H_CUT = 256
+PLAIN = 3
+STD_FLOOR = 2.0**-63
+FORMAT = {"w": E4M3, "h": E4M3, "df": E5M2, "dt": E5M2}
+EARLY = 1
+DZ_BUFS = 3
+STAGE_BUFS = {"w": 2, "h": 2, "df": 2, "dt": 2}
+CODE_BUFS = {"w": 2, "h": 3, "df": 2, "dt": 2}
+STORE_ROWS = (4, 4, 4, 4, 4, 2, 1, 1)
+T_CUT = 384
+H0_CUT = 384
 
 
 def tile_bnn_pb_v_kernel(tc, h0, wm1, wv1, bm1, bv1, we1, be1, z, grad_out, out_0, out_1):
@@ -40,349 +48,333 @@ def tile_bnn_pb_v_kernel(tc, h0, wm1, wv1, bm1, bv1, we1, be1, z, grad_out, out_
         codes = ctx.enter_context(tc.tile_pool(name="codes", bufs=2))
         outs = ctx.enter_context(tc.tile_pool(name="outs", bufs=OUT_BUFS))
         acc_pool = ctx.enter_context(tc.psum_pool(name="acc", bufs=1))
-        psum = ctx.enter_context(tc.psum_pool(name="psum", bufs=4))
+        psum = ctx.enter_context(tc.psum_pool(name="psum", bufs=2))
         ctx.enter_context(tc.manual_schedule())
 
         ident_b = const.tile([P, P], BF16, name="ident_b")
         make_identity(nc, ident_b[:])
         ident_f = const.tile([P, P], F32, name="ident_f")
         make_identity(nc, ident_f[:])
-        acc = [[acc_pool.tile([P, 2, HALF], F32, name="acc%d%d" % (c, k)) for k in range(2)] for c in range(2)]
+        acc = [acc_pool.tile([P, COLS], F32, name="acc%d" % blk) for blk in range(4)]
 
         we_t, z_t, g_t, h_t = {}, {}, {}, {}
-        p_t, dz_t, e4_t, e5_t, e4q_t, e5q_t, o_t = {}, {}, {}, {}, {}, {}, {}
+        wf_t, dz_t, staged, coded, o_t, w_banks = {}, {}, {}, {}, {}, {}
 
         def rows(ap):
             return ap.rearrange("(p j) w -> p j w", j=4)
 
         def load(store, s, src, dtype, name, js=ROWS):
-            if js.start == 0:
-                store[s] = loads.tile([P, 4, COLS], dtype, name=name)
-            nc.sync.dma_start(out=store[s][:, js, :], in_=rows(src[s])[:, js, :])
+            if s < S:
+                if js.start == 0:
+                    store[s] = loads.tile([P, 4, COLS], dtype, name=name)
+                nc.sync.dma_start(out=store[s][:, js, :], in_=rows(src[s])[:, js, :])
 
         def load_we(s, js=ROWS):
-            if s < S:
-                load(we_t, s, we1, BF16, "we", js)
+            load(we_t, s, we1, BF16, "we", js)
 
         def load_h(s):
-            if s < S:
-                load(h_t, s, h0, BF16, "h")
+            load(h_t, s, h0, BF16, "h")
 
         def load_zg(s, js=ROWS):
-            if s < S:
-                load(z_t, s, z, F32, "z", js)
-                load(g_t, s, grad_out, BF16, "g", js)
+            load(z_t, s, z, F32, "z", js)
+            load(g_t, s, grad_out, BF16, "g", js)
 
-        def e4_tile(s):
-            if s not in e4_t:
-                e4_t[s] = mid.tile([P, 2 * COLS * 4], BF16, name="e4", align_bytes=256, bufs=2)
-            return e4_t[s]
+        def stage(kind, s):
+            if (kind, s) not in staged:
+                staged[kind, s] = mid.tile([P, 4 * COLS], BF16, name=kind, align_bytes=256, bufs=STAGE_BUFS[kind])
+            return staged[kind, s]
 
-        def e5_tile(s):
-            if s not in e5_t:
-                e5_t[s] = mid.tile([P, 2 * COLS * 4], BF16, name="e5", align_bytes=256, bufs=S - LATE)
-            return e5_t[s]
-
-        def quantize(src, lo, hi, dtype, store, s, name):
-            if s not in store:
-                words = codes.tile([P, 2 * COLS], U32, name=name + "c", align_bytes=256, bufs=S - LATE + 1)
-                scales = codes.tile([P, 2 * COLS], U8, name=name + "s", align_bytes=256, bufs=S - LATE + 1)
-                store[s] = (words, scales)
-            words, scales = store[s]
+        def quantize(kind, s, lo=0, hi=COLS):
+            if (kind, s) not in coded:
+                words = codes.tile([P, COLS], U32, name=kind + "c", align_bytes=256, bufs=CODE_BUFS[kind])
+                scales = codes.tile([P, COLS], U8, name=kind + "s", align_bytes=256, bufs=CODE_BUFS[kind])
+                coded[kind, s] = (words, scales)
+            words, scales = coded[kind, s]
             nc.vector.quantize_mx(
-                out=words[:, lo:hi].bitcast(dtype), scales=scales[:, lo:hi], in_=src[:, 4 * lo : 4 * hi]
+                out=words[:, lo:hi].bitcast(FORMAT[kind]),
+                scales=scales[:, lo:hi],
+                in_=staged[kind, s][:, 4 * lo : 4 * hi],
             )
-
-        def q_e4(s, lo=0, hi=2 * COLS):
-            quantize(e4_t[s], lo, hi, E4M3, e4q_t, s, "e4")
-
-        def q_e5(s, lo=0, hi=2 * COLS):
-            quantize(e5_t[s], lo, hi, E5M2, e5q_t, s, "e5")
-
-        def by_half_block(tile, js, u):
-            return tile[:, js, :].rearrange("p j (b u f) -> p u (j b) f", u=2, f=16)[:, u, :, :]
-
-        def by_position(tile, js, u):
-            return tile[:, js, :].rearrange("p j (b u i e) -> p u e (j b) i", u=2, i=8, e=2)[:, u, :, :, :]
-
-        def position_major(tile, js, u):
-            return tile[:, u, :, js, :].rearrange("p e j (b i) -> p e (j b) i", i=8)
 
         def mask(s, js=ROWS):
             if js.start == 0:
-                dz_t[s] = mid.tile([P, 2, 4, 256], BF16, name="dz", align_bytes=256, bufs=S - LATE)
-            for u in range(2):
-                nc.vector.scalar_tensor_tensor(
-                    out=dz_t[s][:, u, js, :].rearrange("p j (b f) -> p (j b) f", f=16),
-                    in0=by_half_block(z_t[s], js, u),
-                    scalar=0.0,
-                    in1=by_half_block(g_t[s], js, u),
-                    op0=ALU.is_gt,
-                    op1=ALU.mult,
-                )
-
-        def d_interleave(s, copy, c, lo=0, hi=P):
-            di = e5_tile(s)[:, 4 * COLS :].rearrange("p (c u w j) -> p c u w j", c=2, u=2, j=4)
-            copy(
-                out=di[:, c, :, lo:hi, :].rearrange("p u (n r) j -> p u n j r", r=RUN),
-                in_=dz_t[s][:, :, :, P * c + lo : P * c + hi].rearrange("p u j (n r) -> p u n j r", r=RUN),
+                dz_t[s] = mid.tile([P, 4, COLS], BF16, name="dz", align_bytes=256, bufs=DZ_BUFS)
+            nc.vector.scalar_tensor_tensor(
+                out=dz_t[s][:, js, :],
+                in0=z_t[s][:, js, :],
+                scalar=0.0,
+                in1=g_t[s][:, js, :],
+                op0=ALU.is_gt,
+                op1=ALU.mult,
             )
+
+        def interleave(copy, src, dst, lo, hi):
+            copy(
+                out=dst[:, 4 * lo : 4 * hi].rearrange("p (n r j) -> p n j r", r=RUN, j=4),
+                in_=src[:, :, lo:hi].rearrange("p j (n r) -> p n j r", r=RUN),
+            )
+
+        def d_interleave(s, copy, lo, hi):
+            interleave(copy, dz_t[s], stage("dt", s), lo, hi)
 
         def h_interleave(s, copy, lo, hi):
-            pair = e4_tile(s - 1)
-            copy(
-                out=pair[:, 4 * (COLS + lo) : 4 * (COLS + hi)].rearrange("p (n r j) -> p n j r", r=RUN, j=4),
-                in_=h_t[s][:, :, lo:hi].rearrange("p j (n r) -> p n j r", r=RUN),
+            interleave(copy, h_t[s], stage("h", s), lo, hi)
+
+        def we_cast(s, copy=on_scalar):
+            wf_t[s] = mid.tile([P, 4, P], F32, name="wf")
+            copy(out=wf_t[s][:], in_=we_t[s][:, :, PLAIN::4])
+
+        def w_matmul(s, j, t):
+            if t == 0:
+                w_banks[s, j] = psum.tile([P, 4, P], F32, name="w_bank")
+            nc.tensor.matmul(
+                w_banks[s, j][:, t, :], lhsT=we_t[s][:, j, t::4], rhs=ident_b[:], start=(t == 0), stop=False
             )
 
-        def product(s, js=ROWS):
-            if js.start == 0:
-                p_t[s] = mid.tile([P, 2, 2, 4, P], F32, name="p")
-            for u in range(2):
-                nc.vector.tensor_tensor(
-                    out=position_major(p_t[s], js, u),
-                    in0=by_position(we_t[s], js, u),
-                    in1=position_major(e_s, js, u),
-                    op=ALU.mult,
-                )
-
-        def w_open(j):
-            bank = psum.tile([P, 4, P], F32, name="bank")
-            if j > 0:
-                whole = bank[:].rearrange("p t x -> p (t x)")
-                nc.tensor.matmul(whole, lhsT=ident_b[:], rhs=wm_tr[:, j - 1, :], start=True, stop=False)
-            return bank
-
-        def w_close(s, j, bank):
-            for t in range(4):
-                if j == 0:
-                    nc.tensor.matmul(
-                        bank[:, t, :], lhsT=wm_f[:, t, :], rhs=ident_f[:], is_transpose=True, start=True, stop=False
-                    )
+        def w_transposes(s, j):
+            bank = w_banks[s, j]
+            if s > 0:
                 nc.tensor.matmul(
-                    bank[:, t, :],
-                    lhsT=p_t[s][:, t // 2, t % 2, j, :],
-                    rhs=ident_f[:],
-                    is_transpose=True,
-                    start=False,
-                    stop=(j == 0 or t == 3),
+                    bank[:, PLAIN, :], lhsT=wf_t[s][:, j, :], rhs=ident_f[:], is_transpose=True, start=False, stop=False
                 )
-            wt = e4_tile(s)[:, COLS * j : COLS * (j + 1)].rearrange("p (x t) -> p x t", t=4)
-            return lambda: on_scalar(out=wt, in_=bank[:].rearrange("p t x -> p x t"))
+            for t in range(4):
+                nc.tensor.matmul(
+                    bank[:, t, :], lhsT=ratio[:, j, t, :], rhs=ident_f[:], is_transpose=True, start=False, stop=(t == 3)
+                )
 
-        def w_bank(s, j):
-            return w_close(s, j, w_open(j))
+        def w_out(s, j):
+            nc.vector.scalar_tensor_tensor(
+                out=stage("w", s)[:, COLS * j : COLS * (j + 1)].rearrange("p (x t) -> p x t", t=4),
+                in0=std_t[:, j, :, :],
+                scalar=STD_FLOOR,
+                in1=w_banks[s, j][:].rearrange("p t x -> p x t"),
+                op0=ALU.max,
+                op1=ALU.mult,
+            )
 
-        def dz_bank(s, half):
+        def word_bank(src, half):
             bank = psum.tile([P, 2, 2, P], F32, name="bank")
             for k in range(2):
+                words = src[:, 2 * half + k, :].bitcast(F32)
                 for u in range(2):
-                    nc.tensor.transpose(bank[:, k, u, :], dz_t[s][:, u, 2 * half + k, :].bitcast(F32), ident_f[:])
-            dt = e5_tile(s)[:, 2 * COLS * half : 2 * COLS * (half + 1)].bitcast(F32)
-            return lambda: on_scalar(
-                out=dt.rearrange("p (k x u) -> p k x u", k=2, u=2), in_=bank[:].rearrange("p k u x -> p k x u")
-            )
+                    nc.tensor.transpose(bank[:, k, u, :], words[:, u::2], ident_f[:])
+            return bank
 
-        def weight_grad(s, blk, c):
-            hc, hs = e4q_t[s - 1]
-            dc, ds = e5q_t[s]
-            hcols = slice(COLS + P * blk, COLS + P * (blk + 1))
-            dcols = slice(COLS + HALF * c, COLS + HALF * (c + 1))
+        def dz_bank(s, half):
+            bank = word_bank(dz_t[s], half)
+            dt = stage("df", s)[:, 2 * COLS * half : 2 * COLS * (half + 1)].bitcast(F32)
+            on_scalar(out=dt.rearrange("p (k x u) -> p k x u", k=2, u=2), in_=bank[:].rearrange("p k u x -> p k x u"))
+
+        def weight_grad(s, blk, lo=0, hi=D2):
+            hc, hs = coded["h", s]
+            dc, ds = coded["dt", s]
+            hcols = slice(P * blk, P * (blk + 1))
+            dcols = slice(lo, hi)
             nc.tensor.matmul_mx(
-                out=acc[c][blk // 2][:, blk % 2, :],
+                out=acc[blk][:, dcols],
                 lhsT=hc[:, hcols].bitcast(E4M3),
                 lhsT_scale=hs[:, hcols],
                 rhs=dc[:, dcols].bitcast(E5M2),
                 rhs_scale=ds[:, dcols],
-                start=(s == 0 and blk % 2 == 0),
-                stop=(s == S - 1 and blk % 2 == 1),
+                start=(s == 0 and lo == 0),
+                stop=(s == S - 1 and hi == D2),
             )
 
-        def finish_weight_grad(c, k, copy, queue):
-            result = loads.tile([P, 2, HALF], F32, name="we")
-            copy(
-                out=result[:].rearrange("p k (b u f) -> p k b u f", u=2, f=16),
-                in_=acc[c][k][:].rearrange("p k (u b f) -> p k b u f", u=2, f=16),
-            )
-            dst = out_1[2 * P * k : 2 * P * (k + 1), HALF * c : HALF * (c + 1)]
-            queue.dma_start(out=dst.rearrange("(k p) w -> p k w", p=P), in_=result[:])
+        def finish_weight_grad(blk, copy):
+            result = loads.tile([P, COLS], F32, name="we")
+            copy(out=result[:], in_=acc[blk][:])
+            nc.sync.dma_start(out=out_1[P * blk : P * (blk + 1), :], in_=result[:])
 
-        def input_grad(s, j):
-            dc, ds = e5q_t[s]
-            wc, ws = e4q_t[s]
+        def input_grad(s, j, copy=on_scalar, tag="bank"):
+            dc, ds = coded["df", s]
+            wc, ws = coded["w", s]
             if j == 0:
                 o_t[s] = outs.tile([P, 4, P, 4], F32, name="o")
             cols = slice(P * j, P * (j + 1))
-            bank = psum.tile([P, 4, P], F32, name="bank")
+            bank = psum.tile([P, 4, P], F32, name=tag)
             nc.tensor.matmul_mx(
                 out=bank[:].rearrange("p w x -> p (w x)"),
                 lhsT=dc[:, cols].bitcast(E5M2),
                 lhsT_scale=ds[:, cols],
-                rhs=wc[:, :COLS].bitcast(E4M3),
-                rhs_scale=ws[:, :COLS],
+                rhs=wc[:].bitcast(E4M3),
+                rhs_scale=ws[:],
                 start=True,
                 stop=True,
             )
-            on_scalar(out=o_t[s][:, j, :, :], in_=bank[:].rearrange("p w x -> p x w"))
-            rows_a_store = 2 if s < LATE else 1
+            copy(out=o_t[s][:, j, :, :], in_=bank[:].rearrange("p w x -> p x w"))
+            rows_a_store = STORE_ROWS[s]
             if (j + 1) % rows_a_store == 0:
                 js = slice(j + 1 - rows_a_store, j + 1)
                 src = o_t[s][:, js, :, :].rearrange("p j x w -> p j (x w)")
                 nc.sync.dma_start(out=rows(out_0[s])[:, js, :], in_=src)
 
-        def both_grads(s, q):
-            input_grad(s, q)
-            for c in range(2):
-                weight_grad(s, q, c)
+        def weave(passes, matmuls, lead=0):
+            for n in range(max(len(passes), lead + len(matmuls))):
+                if n < len(passes):
+                    passes[n]()
+                if lead <= n < lead + len(matmuls):
+                    matmuls[n - lead]()
 
-        wv_t = mid.tile([P, 4, D2], BF16, name="dz", align_bytes=256, bufs=S - LATE)
-        wm_t = mid.tile([P, 4, D2], BF16, name="dz", align_bytes=256, bufs=S - LATE)
-        nc.sync.dma_start(out=wv_t[:, ROW_HALVES[0], :], in_=rows(wv1)[:, ROW_HALVES[0], :])
-        nc.sync.dma_start(out=wm_t[:], in_=rows(wm1))
-        nc.sync.dma_start(out=wv_t[:, ROW_HALVES[1], :], in_=rows(wv1)[:, ROW_HALVES[1], :])
-        load_h(0)
-        for js in ROW_HALVES:
-            load_we(0, js)
-        load_h(1)
-        load_we(1)
+        def out_pass(s, q):
+            return [lambda: input_grad(s, q)] if 0 <= s < S else []
+
+        def acc_passes(s, blk):
+            return [lambda: weight_grad(s, blk, 0, HALF), lambda: weight_grad(s, blk, HALF, D2)] if 0 <= s < S - 2 else []
+
+        def w_matmuls(s, j):
+            return [lambda t=t: w_matmul(s, j, t) for t in range(PLAIN if s > 0 else 4)] if s < S else []
+
+        wv_t = mid.tile([P, 4, D2], BF16, name="dz", align_bytes=256, bufs=DZ_BUFS)
+        wm_t = mid.tile([P, 4, D2], BF16, name="dz", align_bytes=256, bufs=DZ_BUFS)
+
+        def load_moments(js):
+            nc.sync.dma_start(out=wv_t[:, js, :], in_=rows(wv1)[:, js, :])
+            nc.sync.dma_start(out=wm_t[:, js, :], in_=rows(wm1)[:, js, :])
+
+        load_moments(ROW_HALVES[0])
+        load_we(0)
+        load_moments(ROW_HALVES[1])
         for js in ROW_HALVES:
             load_zg(0, js)
+        load_h(0)
+        load_we(1)
+        load_zg(1, ROW_HALVES[0])
+        load_h(1)
+        load_zg(1, ROW_HALVES[1])
+        load_we(2)
+        load_zg(2, ROW_HALVES[0])
         load_h(2)
-        for s in range(1, AHEAD):
+        load_zg(2, ROW_HALVES[1])
+        for s in range(3, AHEAD):
+            load_we(s)
+            load_h(s)
             load_zg(s)
-            if s + 1 < AHEAD:
-                load_we(s + 1)
-            if s + 2 < AHEAD:
-                load_h(s + 2)
 
-        e_s = const.tile([P, 2, 2, 4, P], F32, name="e_s")
-        for js in ROW_HALVES:
-            for u in range(2):
+        ratio = const.tile([P, 4, 4, P], F32, name="ratio")
+        std_t = const.tile([P, 4, P, 4], F32, name="std_t")
+
+        def inverse_std(j):
+            nc.scalar.activation(
+                out=ratio[:, j, :, :], in_=wv_t[:, j, :].rearrange("p (m t) -> p t m", t=4), func=ACT.Exp, scale=-0.5
+            )
+
+        def std_rows(half):
+            bank = word_bank(wv_t, half)
+            for k in range(2):
                 nc.scalar.activation(
-                    out=position_major(e_s, js, u), in_=by_position(wv_t, js, u), func=ACT.Exp, scale=0.5
+                    out=std_t[:, 2 * half + k, :, :].rearrange("p x (u e) -> p x u e", e=2),
+                    in_=bank[:, k, :, :].bitcast(BF16).rearrange("p u (x e) -> p x u e", e=2),
+                    func=ACT.Exp,
+                    scale=0.5,
                 )
-        wm_u = const.tile([P, 2, 3, 256], BF16, name="wm_u")
-        on_vector(
-            out=wm_u[:].rearrange("p u j (b f) -> p u (j b) f", f=16),
-            in_=wm_t[:, 1:4, :].rearrange("p j (b u f) -> p u (j b) f", u=2, f=16),
-        )
-        wm_f = const.tile([P, 4, P], F32, name="wm_f")
-        on_vector(
-            out=wm_f[:].rearrange("p (u e) (b i) -> p u e b i", e=2, i=8),
-            in_=wm_t[:, 0, :].rearrange("p (b u i e) -> p u e b i", u=2, i=8, e=2),
-        )
-        h_interleave(0, on_vector, 0, D1 // 2)
-        h_interleave(0, on_scalar, D1 // 2, D1)
-        load_h(AHEAD)
-        wm_tr = const.tile([P, 3, D1], BF16, name="wm_tr")
-        for j0, j1 in ((0, 2), (2, 3)):
-            bank = psum.tile([P, j1 - j0, 4, P], BF16, name="bank")
-            for j in range(j0, j1):
-                for t in range(4):
-                    nc.tensor.transpose(bank[:, j - j0, t, :], wm_u[:, t // 2, j, t % 2 :: 2], ident_b[:])
-            on_scalar(out=wm_tr[:, j0:j1, :], in_=bank[:].rearrange("p j t x -> p j (t x)"))
-        for js in ROW_HALVES:
-            product(0, js)
-        load_we(AHEAD)
-        q_e4(-1, COLS)
-        product(1)
-        load_we(AHEAD + 1)
-        first = w_bank(0, 0)
-        h_interleave(1, on_scalar, H_CUTS[0], H_CUTS[1])
-        first()
-        h_interleave(1, on_scalar, H_CUTS[1], H_CUTS[3])
-        load_h(AHEAD + 1)
-        banks = [w_open(j) for j in range(1, 4)]
-        for j in range(1, 4):
-            w_close(0, j, banks[j - 1])()
-        for js in ROW_HALVES:
-            mask(0, js)
-        load_zg(AHEAD)
-        q_e4(0)
-        d_interleave(0, on_vector, 0)
-        d_interleave(0, on_vector, 1, 0, D_CUT)
-        w_bank(1, W_ORDER[0])()
-        h_interleave(2, on_scalar, H_CUTS[0], H_CUTS[1])
-        for copy_out in [dz_bank(0, 0), dz_bank(0, 1)]:
-            copy_out()
-        d_interleave(0, on_scalar, 1, D_CUT)
-        q_e5(0)
-        h_interleave(2, on_scalar, H_CUTS[1], H_CUTS[2])
-        w_bank(1, W_ORDER[1])()
-        h_interleave(2, on_scalar, H_CUTS[2], H_CUTS[3])
-        load_h(AHEAD + 2)
 
-        for n in range(4, 4 * (S - 1)):
-            s, q = divmod(n, 4)
-            late = s >= LATE
-            if q == 0:
-                mask(s)
-                load_zg(s + AHEAD)
-            if q == 1:
-                product(s + 1)
-                load_we(s + 1 + AHEAD)
-                if not late:
-                    d_interleave(s, on_scalar, 1, D_CUT)
-            if q == 2 and not late:
-                d_interleave(s, on_vector, 0)
-                d_interleave(s, on_vector, 1, 0, D_CUT)
-            if q == 3:
-                before_last = s == S - 2
-                q_e4(s, 0, COLS if before_last else 2 * COLS)
-                if before_last:
-                    h_interleave(s + 1, on_vector, 0, D1 // 2)
-                q_e5(s, 0, COLS if late else 2 * COLS)
-            w_sample, w_step = divmod(n + 2, 4)
-            w_bank(w_sample, W_ORDER[w_step])()
-            if s - 1 < LATE:
-                both_grads(s - 1, q)
-            else:
-                input_grad(s - 1, q)
-            if q == 1:
-                for copy_out in [dz_bank(s, 0), dz_bank(s, 1)]:
-                    copy_out()
-            if q > 0 and s + 2 < S - 1:
-                h_interleave(s + 2, on_scalar, H_CUTS[q - 1], H_CUTS[q])
-                if q == 3:
-                    load_h(s + 2 + AHEAD)
+        def ratio_row(j):
+            nc.vector.scalar_tensor_tensor(
+                out=ratio[:, j, :, :],
+                in0=ratio[:, j, :, :],
+                scalar=1.0 / STD_FLOOR,
+                in1=wm_t[:, j, :].rearrange("p (m t) -> p t m", t=4),
+                op0=ALU.min,
+                op1=ALU.mult,
+            )
+
+        def w_fill(s, j):
+            weave([], w_matmuls(s, j))
+            w_transposes(s, j)
+
+        for j in (0, 1):
+            inverse_std(j)
+            ratio_row(j)
+        std_rows(0)
+        w_fill(0, 0)
+        for j in (2, 3):
+            inverse_std(j)
+        std_rows(1)
+        w_fill(0, 1)
+        w_out(0, 0)
+        for j in (2, 3):
+            ratio_row(j)
+        w_fill(0, 2)
+        mask(0, ROW_HALVES[0])
+        dz_bank(0, 0)
+        w_out(0, 1)
+        w_fill(0, 3)
+        mask(0, ROW_HALVES[1])
+        load_we(AHEAD)
+        load_zg(AHEAD)
+        dz_bank(0, 1)
+        h_interleave(0, on_scalar, 0, H_CUT)
+        we_cast(1)
+        h_interleave(0, on_scalar, H_CUT, D1)
+        load_h(AHEAD)
+        w_out(0, 2)
+        w_fill(1, 0)
+        w_out(0, 3)
+        w_fill(1, 1)
+        d_interleave(0, on_vector, 0, D2)
+        h_interleave(1, on_scalar, 0, H_CUT)
+        quantize("w", 0)
+        quantize("df", 0)
 
         last = S - 1
-        late_samples = range(LATE, S)
-        mask(last)
-        for j in range(2):
-            w_bank(last, W_ORDER[j + 2])()
-            input_grad(last - 1, j)
-        for s in late_samples[:-1]:
-            d_interleave(s, on_vector, 0)
-        for copy_out in [dz_bank(last, 0), dz_bank(last, 1)]:
-            copy_out()
-        q_e5(LATE, COLS, COLS + HALF)
-        q_e4(last, 0, COLS)
-        q_e5(last - 1, COLS, COLS + HALF)
-        d_interleave(last, on_vector, 0)
-        q_e5(last, 0, COLS)
-        for j in (2, 3):
-            input_grad(last - 1, j)
-        for s in late_samples[:-1]:
-            for blk in range(4):
-                weight_grad(s, blk, 0)
-        h_interleave(last, on_scalar, D1 // 2, D1)
-        q_e5(last, COLS, COLS + HALF)
-        for j in range(4):
-            input_grad(last, j)
-        d_interleave(LATE, on_vector, 1)
-        q_e4(last - 1, COLS)
+        for m in range(4, 4 * S):
+            s, j = divmod(m, 4)
+            shared = EARLY <= s < last - 1
+            if j in (0, 2):
+                mask(s, ROW_HALVES[j // 2])
+            if j == 2:
+                load_zg(s + AHEAD)
+            if m == 5:
+                quantize("h", 0)
+            if j == 1 and s > 1:
+                quantize("w", s - 1)
+                quantize("df", s - 1)
+            if j == 3:
+                if shared:
+                    d_interleave(s, on_vector, 0, D_CUT)
+                if 0 < s < last:
+                    quantize("h", s)
+                if 0 < s:
+                    quantize("dt", s - 1)
+            w_out(s, j)
+            w_sample, w_row = divmod(m + 2, 4)
+            out_step = m - 4 if m < 8 else (m - 5 if m > 8 else -1)
+            weave(out_pass(*divmod(out_step, 4)) + acc_passes(*divmod(m - 7, 4)), w_matmuls(w_sample, w_row))
+            if w_sample < S:
+                w_transposes(w_sample, w_row)
+            if w_row == 3:
+                load_we(w_sample + AHEAD)
+            if j == 2 and s < last:
+                d_interleave(s, on_scalar, D_CUT if shared else HALF, D2)
+            if j == 3 and not shared and s < last:
+                d_interleave(s, on_scalar, 0, HALF)
+            if j == 3 and s + 1 < last:
+                h_interleave(s + 1, on_scalar, 0, H_CUT)
+            if j == 0 and 0 < s < last:
+                h_interleave(s, on_scalar, H_CUT, D1)
+                load_h(s + AHEAD)
+            if j == 1 and s + 1 < S:
+                we_cast(s + 1)
+            if j in (0, 2):
+                dz_bank(s, j // 2)
+
+        def h_block(blk):
+            h_interleave(last, on_vector, P * blk, P * (blk + 1))
+
+        input_grad(last - 1, 3)
+        d_interleave(last, on_vector, 0, T_CUT)
+        quantize("w", last)
+        quantize("df", last)
+        d_interleave(last, on_scalar, T_CUT, D2)
         for blk in range(4):
-            weight_grad(last, blk, 0)
-        for s in late_samples[1:]:
-            d_interleave(s, on_vector, 1)
-            q_e5(s - 1, COLS + HALF)
-            for blk in range(4):
-                weight_grad(s - 1, blk, 1)
-        finish_weight_grad(0, 0, on_scalar, nc.scalar)
-        q_e5(last, COLS + HALF)
-        finish_weight_grad(0, 1, on_vector, nc.sync)
+            weight_grad(last - 1, blk)
+        for q in range(4):
+            input_grad(last, q)
+        h_block(0)
+        quantize("dt", last)
         for blk in range(4):
-            weight_grad(last, blk, 1)
-        finish_weight_grad(1, 0, on_scalar, nc.scalar)
-        finish_weight_grad(1, 1, on_vector, nc.sync)
+            if blk < 3:
+                h_block(blk + 1)
+            quantize("h", last, P * blk, P * (blk + 1))
+            weight_grad(last, blk)
+            finish_weight_grad(blk, on_scalar)

@@ -24,18 +24,18 @@ ROW_HALVES = (slice(0, 2), slice(2, 4))
 AHEAD = 4
 OUT_BUFS = 4
 RUN = 4
-D_CUT = 288
-H_CUT = 256
+D0_CUT = 256
+D_CUTS = (0, 224, 320, 512)
 PLAIN = 3
 STD_FLOOR = 2.0**-63
-FORMAT = {"w": E4M3, "h": E4M3, "df": E5M2, "dt": E5M2}
-EARLY = 1
+FORMAT = {"e4": E4M3, "e5": E5M2}
 DZ_BUFS = 3
-STAGE_BUFS = {"w": 2, "h": 2, "df": 2, "dt": 2}
-CODE_BUFS = {"w": 2, "h": 3, "df": 2, "dt": 2}
+STAGE_BUFS = {"e4": 2, "e5": 2, "e4_last": 1, "e5_last": 1}
+CODE_BUFS = 3
 STORE_ROWS = (4, 4, 4, 4, 4, 2, 1, 1)
-T_CUT = 384
-H0_CUT = 384
+G_CUTS = (0, 48, 144, 240, 336)
+L_CUTS = (0, 96, 288, 384, 512)
+H_LAST = 384
 
 
 def tile_bnn_pb_v_kernel(tc, h0, wm1, wv1, bm1, bv1, we1, be1, z, grad_out, out_0, out_1):
@@ -79,22 +79,36 @@ def tile_bnn_pb_v_kernel(tc, h0, wm1, wv1, bm1, bv1, we1, be1, z, grad_out, out_
             load(z_t, s, z, F32, "z", js)
             load(g_t, s, grad_out, BF16, "g", js)
 
+        def place(kind, s):
+            return {"w": ("e4", s, 0), "h": ("e4", s + 1, COLS), "df": ("e5", s, 0), "dt": ("e5", s + 1, COLS)}[kind]
+
         def stage(kind, s):
-            if (kind, s) not in staged:
-                staged[kind, s] = mid.tile([P, 4 * COLS], BF16, name=kind, align_bytes=256, bufs=STAGE_BUFS[kind])
-            return staged[kind, s]
+            pair, n, at = place(kind, s)
+            if (pair, n) not in staged:
+                tag = pair if n < S else pair + "_last"
+                staged[pair, n] = mid.tile([P, 8 * COLS], BF16, name=tag, align_bytes=256, bufs=STAGE_BUFS[tag])
+            return staged[pair, n][:, 4 * at : 4 * (at + COLS)]
+
+        def quantize_pair(pair, n, lo=0, hi=2 * COLS):
+            if (pair, n) not in coded:
+                words = codes.tile([P, 2 * COLS], U32, name=pair + "c", align_bytes=256, bufs=CODE_BUFS)
+                scales = codes.tile([P, 2 * COLS], U8, name=pair + "s", align_bytes=256, bufs=CODE_BUFS)
+                coded[pair, n] = (words, scales)
+            words, scales = coded[pair, n]
+            nc.vector.quantize_mx(
+                out=words[:, lo:hi].bitcast(FORMAT[pair]),
+                scales=scales[:, lo:hi],
+                in_=staged[pair, n][:, 4 * lo : 4 * hi],
+            )
 
         def quantize(kind, s, lo=0, hi=COLS):
-            if (kind, s) not in coded:
-                words = codes.tile([P, COLS], U32, name=kind + "c", align_bytes=256, bufs=CODE_BUFS[kind])
-                scales = codes.tile([P, COLS], U8, name=kind + "s", align_bytes=256, bufs=CODE_BUFS[kind])
-                coded[kind, s] = (words, scales)
-            words, scales = coded[kind, s]
-            nc.vector.quantize_mx(
-                out=words[:, lo:hi].bitcast(FORMAT[kind]),
-                scales=scales[:, lo:hi],
-                in_=staged[kind, s][:, 4 * lo : 4 * hi],
-            )
+            pair, n, at = place(kind, s)
+            quantize_pair(pair, n, at + lo, at + hi)
+
+        def operand(kind, s, lo, hi):
+            pair, n, at = place(kind, s)
+            words, scales = coded[pair, n]
+            return words[:, at + lo : at + hi].bitcast(FORMAT[pair]), scales[:, at + lo : at + hi]
 
         def mask(s, js=ROWS):
             if js.start == 0:
@@ -119,6 +133,22 @@ def tile_bnn_pb_v_kernel(tc, h0, wm1, wv1, bm1, bv1, we1, be1, z, grad_out, out_
 
         def h_interleave(s, copy, lo, hi):
             interleave(copy, h_t[s], stage("h", s), lo, hi)
+
+        def h_on_gpsimd(s, lo, hi):
+            on_gpsimd(h_t[s], stage("h", s), lo, hi)
+
+        def d_on_gpsimd(s, lo, hi):
+            on_gpsimd(dz_t[s], stage("dt", s), lo, hi)
+
+        def on_gpsimd(src, dst, lo, hi):
+            nc.gpsimd.tensor_scalar(
+                out=dst[:, 4 * lo : 4 * hi].rearrange("p (c j) -> p c j", j=4),
+                in0=src[:, :, lo:hi].rearrange("p j c -> p c j"),
+                scalar1=1.0,
+                scalar2=0.0,
+                op0=ALU.mult,
+                op1=ALU.add,
+            )
 
         def we_cast(s, copy=on_scalar):
             wf_t[s] = mid.tile([P, 4, P], F32, name="wf")
@@ -166,16 +196,14 @@ def tile_bnn_pb_v_kernel(tc, h0, wm1, wv1, bm1, bv1, we1, be1, z, grad_out, out_
             on_scalar(out=dt.rearrange("p (k x u) -> p k x u", k=2, u=2), in_=bank[:].rearrange("p k u x -> p k x u"))
 
         def weight_grad(s, blk, lo=0, hi=D2):
-            hc, hs = coded["h", s]
-            dc, ds = coded["dt", s]
-            hcols = slice(P * blk, P * (blk + 1))
-            dcols = slice(lo, hi)
+            hc, hs = operand("h", s, P * blk, P * (blk + 1))
+            dc, ds = operand("dt", s, lo, hi)
             nc.tensor.matmul_mx(
-                out=acc[blk][:, dcols],
-                lhsT=hc[:, hcols].bitcast(E4M3),
-                lhsT_scale=hs[:, hcols],
-                rhs=dc[:, dcols].bitcast(E5M2),
-                rhs_scale=ds[:, dcols],
+                out=acc[blk][:, lo:hi],
+                lhsT=hc,
+                lhsT_scale=hs,
+                rhs=dc,
+                rhs_scale=ds,
                 start=(s == 0 and lo == 0),
                 stop=(s == S - 1 and hi == D2),
             )
@@ -186,18 +214,17 @@ def tile_bnn_pb_v_kernel(tc, h0, wm1, wv1, bm1, bv1, we1, be1, z, grad_out, out_
             nc.sync.dma_start(out=out_1[P * blk : P * (blk + 1), :], in_=result[:])
 
         def input_grad(s, j, copy=on_scalar, tag="bank"):
-            dc, ds = coded["df", s]
-            wc, ws = coded["w", s]
+            dc, ds = operand("df", s, P * j, P * (j + 1))
+            wc, ws = operand("w", s, 0, COLS)
             if j == 0:
                 o_t[s] = outs.tile([P, 4, P, 4], F32, name="o")
-            cols = slice(P * j, P * (j + 1))
             bank = psum.tile([P, 4, P], F32, name=tag)
             nc.tensor.matmul_mx(
                 out=bank[:].rearrange("p w x -> p (w x)"),
-                lhsT=dc[:, cols].bitcast(E5M2),
-                lhsT_scale=ds[:, cols],
-                rhs=wc[:].bitcast(E4M3),
-                rhs_scale=ws[:],
+                lhsT=dc,
+                lhsT_scale=ds,
+                rhs=wc,
+                rhs_scale=ws,
                 start=True,
                 stop=True,
             )
@@ -219,7 +246,7 @@ def tile_bnn_pb_v_kernel(tc, h0, wm1, wv1, bm1, bv1, we1, be1, z, grad_out, out_
             return [lambda: input_grad(s, q)] if 0 <= s < S else []
 
         def acc_passes(s, blk):
-            return [lambda: weight_grad(s, blk, 0, HALF), lambda: weight_grad(s, blk, HALF, D2)] if 0 <= s < S - 2 else []
+            return [lambda: weight_grad(s, blk, 0, HALF), lambda: weight_grad(s, blk, HALF, D2)] if 0 <= s < S else []
 
         def w_matmuls(s, j):
             return [lambda t=t: w_matmul(s, j, t) for t in range(PLAIN if s > 0 else 4)] if s < S else []
@@ -236,8 +263,8 @@ def tile_bnn_pb_v_kernel(tc, h0, wm1, wv1, bm1, bv1, we1, be1, z, grad_out, out_
         load_moments(ROW_HALVES[1])
         for js in ROW_HALVES:
             load_zg(0, js)
-        load_h(0)
         load_we(1)
+        load_h(0)
         load_zg(1, ROW_HALVES[0])
         load_h(1)
         load_zg(1, ROW_HALVES[1])
@@ -303,78 +330,89 @@ def tile_bnn_pb_v_kernel(tc, h0, wm1, wv1, bm1, bv1, we1, be1, z, grad_out, out_
         load_we(AHEAD)
         load_zg(AHEAD)
         dz_bank(0, 1)
-        h_interleave(0, on_scalar, 0, H_CUT)
         we_cast(1)
-        h_interleave(0, on_scalar, H_CUT, D1)
-        load_h(AHEAD)
         w_out(0, 2)
         w_fill(1, 0)
         w_out(0, 3)
         w_fill(1, 1)
-        d_interleave(0, on_vector, 0, D2)
-        h_interleave(1, on_scalar, 0, H_CUT)
-        quantize("w", 0)
-        quantize("df", 0)
+        d_interleave(0, on_vector, 0, D0_CUT)
+        h_interleave(0, on_scalar, 0, D1)
+        load_h(AHEAD)
+        d_interleave(0, on_scalar, D0_CUT, D2)
 
         last = S - 1
-        for m in range(4, 4 * S):
-            s, j = divmod(m, 4)
-            shared = EARLY <= s < last - 1
-            if j in (0, 2):
-                mask(s, ROW_HALVES[j // 2])
-            if j == 2:
-                load_zg(s + AHEAD)
-            if m == 5:
-                quantize("h", 0)
-            if j == 1 and s > 1:
-                quantize("w", s - 1)
-                quantize("df", s - 1)
-            if j == 3:
-                if shared:
-                    d_interleave(s, on_vector, 0, D_CUT)
-                if 0 < s < last:
-                    quantize("h", s)
-                if 0 < s:
-                    quantize("dt", s - 1)
-            w_out(s, j)
-            w_sample, w_row = divmod(m + 2, 4)
-            out_step = m - 4 if m < 8 else (m - 5 if m > 8 else -1)
-            weave(out_pass(*divmod(out_step, 4)) + acc_passes(*divmod(m - 7, 4)), w_matmuls(w_sample, w_row))
-            if w_sample < S:
-                w_transposes(w_sample, w_row)
+
+        def fill(m, passes):
+            w_sample, w_row = divmod(m, 4)
+            weave(passes, w_matmuls(w_sample, w_row))
+            w_transposes(w_sample, w_row)
             if w_row == 3:
                 load_we(w_sample + AHEAD)
-            if j == 2 and s < last:
-                d_interleave(s, on_scalar, D_CUT if shared else HALF, D2)
-            if j == 3 and not shared and s < last:
-                d_interleave(s, on_scalar, 0, HALF)
-            if j == 3 and s + 1 < last:
-                h_interleave(s + 1, on_scalar, 0, H_CUT)
-            if j == 0 and 0 < s < last:
-                h_interleave(s, on_scalar, H_CUT, D1)
-                load_h(s + AHEAD)
-            if j == 1 and s + 1 < S:
+
+        def gpsimd_piece(m):
+            g_sample, piece = divmod(m - 1, 4)
+            if g_sample > 0:
+                h_on_gpsimd(g_sample, G_CUTS[piece], G_CUTS[piece + 1])
+
+        for m in range(4, 4 * last):
+            s, j = divmod(m, 4)
+            if j in (0, 3):
+                mask(s, ROW_HALVES[j // 3])
+            if j == 3:
+                load_zg(s + AHEAD)
+            if j in (1, 2):
+                quantize_pair(("e4", "e5")[j - 1], s - 1, 0, COLS if s == 1 else 2 * COLS)
+            gpsimd_piece(m)
+            w_out(s, j)
+            fill(m + 2, out_pass(*divmod(m - 6, 4)) + acc_passes(*divmod(m - 10, 4)))
+            if j == 3:
+                h_interleave(s, on_scalar, G_CUTS[4], D1)
+            if j == 0 and s > 1:
+                load_h(s - 1 + AHEAD)
+            if j == 1:
                 we_cast(s + 1)
-            if j in (0, 2):
-                dz_bank(s, j // 2)
+            if j < 3 and s > 1:
+                d_interleave(s - 1, on_scalar, D_CUTS[j], D_CUTS[j + 1])
+            if j in (0, 3):
+                dz_bank(s, j // 3)
 
-        def h_block(blk):
-            h_interleave(last, on_vector, P * blk, P * (blk + 1))
-
-        input_grad(last - 1, 3)
-        d_interleave(last, on_vector, 0, T_CUT)
-        quantize("w", last)
+        m = 4 * last
+        for j in (0, 1):
+            mask(last, ROW_HALVES[j])
+            if j == 0:
+                gpsimd_piece(m)
+            else:
+                d_on_gpsimd(last - 1, L_CUTS[0], L_CUTS[1])
+            w_out(last, j)
+            fill(m + j + 2, out_pass(last - 2, j + 2) + acc_passes(last - 3, j + 2))
+            d_interleave(last - 1, on_scalar, L_CUTS[j + 2], L_CUTS[j + 3])
+            dz_bank(last, j)
+        quantize("w", last - 1)
+        quantize("df", last - 1)
+        w_out(last, 2)
+        w_out(last, 3)
+        for q in range(4):
+            input_grad(last - 1, q, tag="bank" if q < 2 else "w_bank")
+        d_interleave(last - 1, on_vector, L_CUTS[1], L_CUTS[2])
         quantize("df", last)
-        d_interleave(last, on_scalar, T_CUT, D2)
+        quantize("w", last)
+        for q in range(4):
+            input_grad(last, q, tag="bank" if q < 2 else "w_bank")
+        quantize("h", last - 2)
+        quantize("dt", last - 2)
+        d_interleave(last, on_vector, 0, D2)
+        for blk in range(4):
+            weight_grad(last - 2, blk)
+        quantize("h", last - 1)
+        quantize("dt", last - 1)
         for blk in range(4):
             weight_grad(last - 1, blk)
-        for q in range(4):
-            input_grad(last, q)
-        h_block(0)
+        h_interleave(last, on_vector, 0, P)
+        h_interleave(last, on_scalar, H_LAST, D1)
         quantize("dt", last)
         for blk in range(4):
-            if blk < 3:
-                h_block(blk + 1)
+            if P * (blk + 1) < H_LAST:
+                h_interleave(last, on_vector, P * (blk + 1), P * (blk + 2))
             quantize("h", last, P * blk, P * (blk + 1))
             weight_grad(last, blk)
             finish_weight_grad(blk, on_scalar)

@@ -25,16 +25,16 @@ AHEAD = 4
 OUT_BUFS = 4
 RUN = 4
 D0_CUT = 256
-D_CUTS = (0, 224, 320, 512)
 PLAIN = 3
 STD_FLOOR = 2.0**-63
 FORMAT = {"e4": E4M3, "e5": E5M2}
 DZ_BUFS = 3
-STAGE_BUFS = {"e4": 2, "e5": 2, "e4_last": 1, "e5_last": 1}
 CODE_BUFS = 3
 STORE_ROWS = (4, 4, 4, 4, 4, 2, 1, 1)
-G_CUTS = (0, 48, 144, 240, 336)
-L_CUTS = (0, 96, 288, 384, 512)
+G_D = 160
+G_H = 160
+H_MID = 320
+LEAD = 1
 H_LAST = 384
 
 
@@ -58,7 +58,7 @@ def tile_bnn_pb_v_kernel(tc, h0, wm1, wv1, bm1, bv1, we1, be1, z, grad_out, out_
         acc = [acc_pool.tile([P, COLS], F32, name="acc%d" % blk) for blk in range(4)]
 
         we_t, z_t, g_t, h_t = {}, {}, {}, {}
-        wf_t, dz_t, staged, coded, o_t, w_banks = {}, {}, {}, {}, {}, {}
+        wf_t, dz_t, staged, coded, o_t, o_banks, w_banks = {}, {}, {}, {}, {}, {}, {}
 
         def rows(ap):
             return ap.rearrange("(p j) w -> p j w", j=4)
@@ -80,13 +80,12 @@ def tile_bnn_pb_v_kernel(tc, h0, wm1, wv1, bm1, bv1, we1, be1, z, grad_out, out_
             load(g_t, s, grad_out, BF16, "g", js)
 
         def place(kind, s):
-            return {"w": ("e4", s, 0), "h": ("e4", s + 1, COLS), "df": ("e5", s, 0), "dt": ("e5", s + 1, COLS)}[kind]
+            return {"w": ("e4", s, 0), "h": ("e4", s, COLS), "df": ("e5", s, 0), "dt": ("e5", s, COLS)}[kind]
 
         def stage(kind, s):
             pair, n, at = place(kind, s)
             if (pair, n) not in staged:
-                tag = pair if n < S else pair + "_last"
-                staged[pair, n] = mid.tile([P, 8 * COLS], BF16, name=tag, align_bytes=256, bufs=STAGE_BUFS[tag])
+                staged[pair, n] = mid.tile([P, 8 * COLS], BF16, name=pair, align_bytes=256)
             return staged[pair, n][:, 4 * at : 4 * (at + COLS)]
 
         def quantize_pair(pair, n, lo=0, hi=2 * COLS):
@@ -110,14 +109,14 @@ def tile_bnn_pb_v_kernel(tc, h0, wm1, wv1, bm1, bv1, we1, be1, z, grad_out, out_
             words, scales = coded[pair, n]
             return words[:, at + lo : at + hi].bitcast(FORMAT[pair]), scales[:, at + lo : at + hi]
 
-        def mask(s, js=ROWS):
-            if js.start == 0:
+        def mask(s, js=ROWS, cols=slice(0, D2)):
+            if s not in dz_t:
                 dz_t[s] = mid.tile([P, 4, COLS], BF16, name="dz", align_bytes=256, bufs=DZ_BUFS)
             nc.vector.scalar_tensor_tensor(
-                out=dz_t[s][:, js, :],
-                in0=z_t[s][:, js, :],
+                out=dz_t[s][:, js, cols],
+                in0=z_t[s][:, js, cols],
                 scalar=0.0,
-                in1=g_t[s][:, js, :],
+                in1=g_t[s][:, js, cols],
                 op0=ALU.is_gt,
                 op1=ALU.mult,
             )
@@ -213,14 +212,16 @@ def tile_bnn_pb_v_kernel(tc, h0, wm1, wv1, bm1, bv1, we1, be1, z, grad_out, out_
             copy(out=result[:], in_=acc[blk][:])
             nc.sync.dma_start(out=out_1[P * blk : P * (blk + 1), :], in_=result[:])
 
-        def input_grad(s, j, copy=on_scalar, tag="bank"):
-            dc, ds = operand("df", s, P * j, P * (j + 1))
-            wc, ws = operand("w", s, 0, COLS)
-            if j == 0:
+        def input_grad_half(s, j, c, tag="bank"):
+            if j == 0 and c == 0:
                 o_t[s] = outs.tile([P, 4, P, 4], F32, name="o")
-            bank = psum.tile([P, 4, P], F32, name=tag)
+            if c == 0:
+                o_banks[s, j] = psum.tile([P, 4, P], F32, name=tag)
+            bank = o_banks[s, j]
+            dc, ds = operand("df", s, P * j, P * (j + 1))
+            wc, ws = operand("w", s, HALF * c, HALF * (c + 1))
             nc.tensor.matmul_mx(
-                out=bank[:].rearrange("p w x -> p (w x)"),
+                out=bank[:].rearrange("p w x -> p (w x)")[:, HALF * c : HALF * (c + 1)],
                 lhsT=dc,
                 lhsT_scale=ds,
                 rhs=wc,
@@ -228,12 +229,17 @@ def tile_bnn_pb_v_kernel(tc, h0, wm1, wv1, bm1, bv1, we1, be1, z, grad_out, out_
                 start=True,
                 stop=True,
             )
-            copy(out=o_t[s][:, j, :, :], in_=bank[:].rearrange("p w x -> p x w"))
-            rows_a_store = STORE_ROWS[s]
-            if (j + 1) % rows_a_store == 0:
-                js = slice(j + 1 - rows_a_store, j + 1)
-                src = o_t[s][:, js, :, :].rearrange("p j x w -> p j (x w)")
-                nc.sync.dma_start(out=rows(out_0[s])[:, js, :], in_=src)
+            if c == 1:
+                on_scalar(out=o_t[s][:, j, :, :], in_=bank[:].rearrange("p w x -> p x w"))
+                rows_a_store = STORE_ROWS[s]
+                if (j + 1) % rows_a_store == 0:
+                    js = slice(j + 1 - rows_a_store, j + 1)
+                    src = o_t[s][:, js, :, :].rearrange("p j x w -> p j (x w)")
+                    nc.sync.dma_start(out=rows(out_0[s])[:, js, :], in_=src)
+
+        def input_grad(s, j, tag="bank"):
+            for c in range(2):
+                input_grad_half(s, j, c, tag)
 
         def weave(passes, matmuls, lead=0):
             for n in range(max(len(passes), lead + len(matmuls))):
@@ -243,7 +249,7 @@ def tile_bnn_pb_v_kernel(tc, h0, wm1, wv1, bm1, bv1, we1, be1, z, grad_out, out_
                     matmuls[n - lead]()
 
         def out_pass(s, q):
-            return [lambda: input_grad(s, q)] if 0 <= s < S else []
+            return [lambda: input_grad_half(s, q, 0), lambda: input_grad_half(s, q, 1)] if 0 <= s < S else []
 
         def acc_passes(s, blk):
             return [lambda: weight_grad(s, blk, 0, HALF), lambda: weight_grad(s, blk, HALF, D2)] if 0 <= s < S else []
@@ -269,9 +275,8 @@ def tile_bnn_pb_v_kernel(tc, h0, wm1, wv1, bm1, bv1, we1, be1, z, grad_out, out_
         load_h(1)
         load_zg(1, ROW_HALVES[1])
         load_we(2)
-        load_zg(2, ROW_HALVES[0])
+        load_zg(2)
         load_h(2)
-        load_zg(2, ROW_HALVES[1])
         for s in range(3, AHEAD):
             load_we(s)
             load_h(s)
@@ -335,81 +340,90 @@ def tile_bnn_pb_v_kernel(tc, h0, wm1, wv1, bm1, bv1, we1, be1, z, grad_out, out_
         w_fill(1, 0)
         w_out(0, 3)
         w_fill(1, 1)
-        d_interleave(0, on_vector, 0, D0_CUT)
         h_interleave(0, on_scalar, 0, D1)
         load_h(AHEAD)
+        quantize("w", 0)
+        quantize("df", 0)
+        d_interleave(0, on_vector, 0, D0_CUT)
         d_interleave(0, on_scalar, D0_CUT, D2)
 
         last = S - 1
 
-        def fill(m, passes):
-            w_sample, w_row = divmod(m, 4)
-            weave(passes, w_matmuls(w_sample, w_row))
-            w_transposes(w_sample, w_row)
-            if w_row == 3:
-                load_we(w_sample + AHEAD)
+        def fill(s, j, outs_from, accs_from, between):
+            for k in range(2):
+                passes = out_pass(outs_from[0], outs_from[1] + k) + acc_passes(accs_from[0], accs_from[1] + k)
+                weave(passes, w_matmuls(s, j + k), LEAD if len(passes) > PLAIN else 0)
+                w_transposes(s, j + k)
+                if k == 0:
+                    between()
 
-        def gpsimd_piece(m):
-            g_sample, piece = divmod(m - 1, 4)
-            if g_sample > 0:
-                h_on_gpsimd(g_sample, G_CUTS[piece], G_CUTS[piece + 1])
+        def mask_by_columns(s):
+            mask(s, cols=slice(0, HALF))
+            d_on_gpsimd(s, 0, G_D)
+            mask(s, cols=slice(HALF, D2))
+            load_zg(s + AHEAD)
 
-        for m in range(4, 4 * last):
-            s, j = divmod(m, 4)
-            if j in (0, 3):
-                mask(s, ROW_HALVES[j // 3])
-            if j == 3:
-                load_zg(s + AHEAD)
-            if j in (1, 2):
-                quantize_pair(("e4", "e5")[j - 1], s - 1, 0, COLS if s == 1 else 2 * COLS)
-            gpsimd_piece(m)
-            w_out(s, j)
-            fill(m + 2, out_pass(*divmod(m - 6, 4)) + acc_passes(*divmod(m - 10, 4)))
-            if j == 3:
-                h_interleave(s, on_scalar, G_CUTS[4], D1)
-            if j == 0 and s > 1:
-                load_h(s - 1 + AHEAD)
-            if j == 1:
-                we_cast(s + 1)
-            if j < 3 and s > 1:
-                d_interleave(s - 1, on_scalar, D_CUTS[j], D_CUTS[j + 1])
-            if j in (0, 3):
-                dz_bank(s, j // 3)
+        mask(1, ROW_HALVES[0])
+        w_out(1, 0)
+        w_out(1, 1)
+        fill(1, 2, (0, 0), (-1, 0), lambda: we_cast(2))
+        load_we(1 + AHEAD)
+        h_interleave(1, on_scalar, 0, H_MID)
+        dz_bank(1, 0)
+        quantize("h", 0)
+        quantize("dt", 0)
+        mask(1, ROW_HALVES[1])
+        load_zg(1 + AHEAD)
+        w_out(1, 2)
+        w_out(1, 3)
+        d_interleave(1, on_vector, 0, D2)
+        fill(2, 0, (0, 2), (0, 0), lambda: h_interleave(1, on_scalar, H_MID, D1))
+        load_h(1 + AHEAD)
+        h_interleave(2, on_scalar, 0, H_MID)
+        dz_bank(1, 1)
 
-        m = 4 * last
-        for j in (0, 1):
-            mask(last, ROW_HALVES[j])
-            if j == 0:
-                gpsimd_piece(m)
-            else:
-                d_on_gpsimd(last - 1, L_CUTS[0], L_CUTS[1])
-            w_out(last, j)
-            fill(m + j + 2, out_pass(last - 2, j + 2) + acc_passes(last - 3, j + 2))
-            d_interleave(last - 1, on_scalar, L_CUTS[j + 2], L_CUTS[j + 3])
-            dz_bank(last, j)
+        for s in range(2, last):
+            mask_by_columns(s)
+            w_out(s, 0)
+            w_out(s, 1)
+            fill(s, 2, (s - 2 if s > 2 else -1, 2), (s - 2, 2), lambda: we_cast(s + 1))
+            load_we(s + AHEAD)
+            h_interleave(s, on_scalar, H_MID, D1)
+            load_h(s + AHEAD)
+            dz_bank(s, 0)
+            quantize_pair("e4", s - 1)
+            if s + 1 < last:
+                h_on_gpsimd(s + 1, 0, G_H)
+            quantize_pair("e5", s - 1)
+            w_out(s, 2)
+            w_out(s, 3)
+            cuts = (G_H, H_MID) if s + 1 < last else (H_LAST, D1)
+            fill(s + 1, 0, (s - 1, 0), (s - 1, 0), lambda: h_interleave(s + 1, on_scalar, *cuts))
+            d_interleave(s, on_scalar, G_D, D2)
+            dz_bank(s, 1)
+
+        mask_by_columns(last)
+        w_out(last, 0)
+        w_out(last, 1)
+        fill(last, 2, (last - 2, 2), (last - 2, 2), lambda: dz_bank(last, 0))
+        dz_bank(last, 1)
         quantize("w", last - 1)
         quantize("df", last - 1)
         w_out(last, 2)
+        d_interleave(last, on_vector, G_D, D2)
         w_out(last, 3)
         for q in range(4):
             input_grad(last - 1, q, tag="bank" if q < 2 else "w_bank")
-        d_interleave(last - 1, on_vector, L_CUTS[1], L_CUTS[2])
+        quantize("h", last - 1)
         quantize("df", last)
         quantize("w", last)
         for q in range(4):
             input_grad(last, q, tag="bank" if q < 2 else "w_bank")
-        quantize("h", last - 2)
-        quantize("dt", last - 2)
-        d_interleave(last, on_vector, 0, D2)
-        for blk in range(4):
-            weight_grad(last - 2, blk)
-        quantize("h", last - 1)
         quantize("dt", last - 1)
+        h_interleave(last, on_vector, 0, P)
+        quantize("dt", last)
         for blk in range(4):
             weight_grad(last - 1, blk)
-        h_interleave(last, on_vector, 0, P)
-        h_interleave(last, on_scalar, H_LAST, D1)
-        quantize("dt", last)
         for blk in range(4):
             if P * (blk + 1) < H_LAST:
                 h_interleave(last, on_vector, P * (blk + 1), P * (blk + 2))

@@ -34,7 +34,6 @@ STORE_ROWS = (4, 4, 4, 4, 4, 2, 1, 1)
 G_D = 160
 G_H = 160
 H_MID = 320
-LEAD = 1
 H_LAST = 384
 
 
@@ -58,7 +57,7 @@ def tile_bnn_pb_v_kernel(tc, h0, wm1, wv1, bm1, bv1, we1, be1, z, grad_out, out_
         acc = [acc_pool.tile([P, COLS], F32, name="acc%d" % blk) for blk in range(4)]
 
         we_t, z_t, g_t, h_t = {}, {}, {}, {}
-        wf_t, dz_t, staged, coded, o_t, o_banks, w_banks = {}, {}, {}, {}, {}, {}, {}
+        wf_t, dz_t, staged, coded, o_t, w_banks = {}, {}, {}, {}, {}, {}
 
         def rows(ap):
             return ap.rearrange("(p j) w -> p j w", j=4)
@@ -194,17 +193,17 @@ def tile_bnn_pb_v_kernel(tc, h0, wm1, wv1, bm1, bv1, we1, be1, z, grad_out, out_
             dt = stage("df", s)[:, 2 * COLS * half : 2 * COLS * (half + 1)].bitcast(F32)
             on_scalar(out=dt.rearrange("p (k x u) -> p k x u", k=2, u=2), in_=bank[:].rearrange("p k u x -> p k x u"))
 
-        def weight_grad(s, blk, lo=0, hi=D2):
+        def weight_grad(s, blk):
             hc, hs = operand("h", s, P * blk, P * (blk + 1))
-            dc, ds = operand("dt", s, lo, hi)
+            dc, ds = operand("dt", s, 0, COLS)
             nc.tensor.matmul_mx(
-                out=acc[blk][:, lo:hi],
+                out=acc[blk][:],
                 lhsT=hc,
                 lhsT_scale=hs,
                 rhs=dc,
                 rhs_scale=ds,
-                start=(s == 0 and lo == 0),
-                stop=(s == S - 1 and hi == D2),
+                start=(s == 0),
+                stop=(s == S - 1),
             )
 
         def finish_weight_grad(blk, copy):
@@ -212,16 +211,14 @@ def tile_bnn_pb_v_kernel(tc, h0, wm1, wv1, bm1, bv1, we1, be1, z, grad_out, out_
             copy(out=result[:], in_=acc[blk][:])
             nc.sync.dma_start(out=out_1[P * blk : P * (blk + 1), :], in_=result[:])
 
-        def input_grad_half(s, j, c, tag="bank"):
-            if j == 0 and c == 0:
+        def input_grad(s, j, tag="bank"):
+            if j == 0:
                 o_t[s] = outs.tile([P, 4, P, 4], F32, name="o")
-            if c == 0:
-                o_banks[s, j] = psum.tile([P, 4, P], F32, name=tag)
-            bank = o_banks[s, j]
+            bank = psum.tile([P, 4, P], F32, name=tag)
             dc, ds = operand("df", s, P * j, P * (j + 1))
-            wc, ws = operand("w", s, HALF * c, HALF * (c + 1))
+            wc, ws = operand("w", s, 0, COLS)
             nc.tensor.matmul_mx(
-                out=bank[:].rearrange("p w x -> p (w x)")[:, HALF * c : HALF * (c + 1)],
+                out=bank[:].rearrange("p w x -> p (w x)"),
                 lhsT=dc,
                 lhsT_scale=ds,
                 rhs=wc,
@@ -229,33 +226,12 @@ def tile_bnn_pb_v_kernel(tc, h0, wm1, wv1, bm1, bv1, we1, be1, z, grad_out, out_
                 start=True,
                 stop=True,
             )
-            if c == 1:
-                on_scalar(out=o_t[s][:, j, :, :], in_=bank[:].rearrange("p w x -> p x w"))
-                rows_a_store = STORE_ROWS[s]
-                if (j + 1) % rows_a_store == 0:
-                    js = slice(j + 1 - rows_a_store, j + 1)
-                    src = o_t[s][:, js, :, :].rearrange("p j x w -> p j (x w)")
-                    nc.sync.dma_start(out=rows(out_0[s])[:, js, :], in_=src)
-
-        def input_grad(s, j, tag="bank"):
-            for c in range(2):
-                input_grad_half(s, j, c, tag)
-
-        def weave(passes, matmuls, lead=0):
-            for n in range(max(len(passes), lead + len(matmuls))):
-                if n < len(passes):
-                    passes[n]()
-                if lead <= n < lead + len(matmuls):
-                    matmuls[n - lead]()
-
-        def out_pass(s, q):
-            return [lambda: input_grad_half(s, q, 0), lambda: input_grad_half(s, q, 1)] if 0 <= s < S else []
-
-        def acc_passes(s, blk):
-            return [lambda: weight_grad(s, blk, 0, HALF), lambda: weight_grad(s, blk, HALF, D2)] if 0 <= s < S else []
-
-        def w_matmuls(s, j):
-            return [lambda t=t: w_matmul(s, j, t) for t in range(PLAIN if s > 0 else 4)] if s < S else []
+            on_scalar(out=o_t[s][:, j, :, :], in_=bank[:].rearrange("p w x -> p x w"))
+            rows_a_store = STORE_ROWS[s]
+            if (j + 1) % rows_a_store == 0:
+                js = slice(j + 1 - rows_a_store, j + 1)
+                src = o_t[s][:, js, :, :].rearrange("p j x w -> p j (x w)")
+                nc.sync.dma_start(out=rows(out_0[s])[:, js, :], in_=src)
 
         wv_t = mid.tile([P, 4, D2], BF16, name="dz", align_bytes=256, bufs=DZ_BUFS)
         wm_t = mid.tile([P, 4, D2], BF16, name="dz", align_bytes=256, bufs=DZ_BUFS)
@@ -311,7 +287,8 @@ def tile_bnn_pb_v_kernel(tc, h0, wm1, wv1, bm1, bv1, we1, be1, z, grad_out, out_
             )
 
         def w_fill(s, j):
-            weave([], w_matmuls(s, j))
+            for t in range(PLAIN if s > 0 else 4):
+                w_matmul(s, j, t)
             w_transposes(s, j)
 
         for j in (0, 1):
@@ -351,9 +328,11 @@ def tile_bnn_pb_v_kernel(tc, h0, wm1, wv1, bm1, bv1, we1, be1, z, grad_out, out_
 
         def fill(s, j, outs_from, accs_from, between):
             for k in range(2):
-                passes = out_pass(outs_from[0], outs_from[1] + k) + acc_passes(accs_from[0], accs_from[1] + k)
-                weave(passes, w_matmuls(s, j + k), LEAD if len(passes) > PLAIN else 0)
-                w_transposes(s, j + k)
+                if outs_from[0] >= 0:
+                    input_grad(outs_from[0], outs_from[1] + k)
+                if accs_from[0] >= 0:
+                    weight_grad(accs_from[0], accs_from[1] + k)
+                w_fill(s, j + k)
                 if k == 0:
                     between()
 

@@ -30,9 +30,10 @@ STD_FLOOR = 2.0**-63
 FORMAT = {"e4": E4M3, "e5": E5M2}
 DZ_BUFS = 3
 CODE_BUFS = 3
-STORE_ROWS = (4, 4, 4, 4, 4, 2, 1, 1)
-G_D = 160
-G_H = 160
+STORE_ROWS = (2, 2, 2, 2, 2, 1, 1, 1)
+V_D = 160
+G_D = 112
+G_H = 112
 H_MID = 320
 H_LAST = 384
 
@@ -370,6 +371,7 @@ def tile_bnn_pb_v_kernel(tc, h0, wm1, wv1, bm1, bv1, we1, be1, z, grad_out, out_
             h_interleave(s, on_scalar, H_MID, D1)
             load_h(s + AHEAD)
             dz_bank(s, 0)
+            d_interleave(s, on_vector, G_D, G_D + V_D)
             quantize_pair("e4", s - 1)
             if s + 1 < last:
                 h_on_gpsimd(s + 1, 0, G_H)
@@ -378,7 +380,7 @@ def tile_bnn_pb_v_kernel(tc, h0, wm1, wv1, bm1, bv1, we1, be1, z, grad_out, out_
             w_out(s, 3)
             cuts = (G_H, H_MID) if s + 1 < last else (H_LAST, D1)
             fill(s + 1, 0, (s - 1, 0), (s - 1, 0), lambda: h_interleave(s + 1, on_scalar, *cuts))
-            d_interleave(s, on_scalar, G_D, D2)
+            d_interleave(s, on_scalar, G_D + V_D, D2)
             dz_bank(s, 1)
 
         mask_by_columns(last)

@@ -21,21 +21,26 @@ COLS = 512
 HALF = 256
 ROWS = slice(0, 4)
 ROW_HALVES = (slice(0, 2), slice(2, 4))
-AHEAD = 4
-OUT_BUFS = 4
 RUN = 4
-D0_CUT = 256
 PLAIN = 3
 STD_FLOOR = 2.0**-63
-FORMAT = {"e4": E4M3, "e5": E5M2}
+FORMAT = {"w": E4M3, "h": E4M3, "df": E5M2, "dt": E5M2}
+LEAD = 2
+WE_BUFS = 5
+G_BUFS = 6
+H_BUFS = 5
 DZ_BUFS = 3
-CODE_BUFS = 3
-STORE_ROWS = (2, 2, 2, 2, 2, 1, 1, 1)
-V_D = 160
-G_D = 112
-G_H = 112
-H_MID = 320
-H_LAST = 384
+H_LOADS = {0: (2,), 1: (3,), 2: (4, 5), 3: (6,), 4: (7,)}
+W_BANKS = ("w0", "w1", "w0", "w1")
+COPY_BANKS = ("c0", "c1")
+ACC_BANKS = ("a0", "a1", "a2", "a3")
+TAIL_BANKS = ("c0", "w0", "w1", "c1")
+HEAD_BANKS = {0: ACC_BANKS, 1: ("w0", "w1", "c1", "c0"), 2: ACC_BANKS, 3: ("w0", "w1", "a0", "a1")}
+CODE_BUFS = {"w": 4, "h": 4, "df": 2, "dt": 2}
+H_MID = 304
+G_D = 160
+G_H = 160
+V_D = 64
 
 
 def tile_bnn_pb_v_kernel(tc, h0, wm1, wv1, bm1, bv1, we1, be1, z, grad_out, out_0, out_1):
@@ -43,71 +48,64 @@ def tile_bnn_pb_v_kernel(tc, h0, wm1, wv1, bm1, bv1, we1, be1, z, grad_out, out_
     on_vector, on_scalar = nc.vector.tensor_copy, nc.scalar.copy
     with ExitStack() as ctx:
         const = ctx.enter_context(tc.tile_pool(name="const", bufs=1))
-        loads = ctx.enter_context(tc.tile_pool(name="loads", bufs=AHEAD))
+        loads = ctx.enter_context(tc.tile_pool(name="loads", bufs=S))
         mid = ctx.enter_context(tc.tile_pool(name="mid", bufs=2))
-        codes = ctx.enter_context(tc.tile_pool(name="codes", bufs=2))
-        outs = ctx.enter_context(tc.tile_pool(name="outs", bufs=OUT_BUFS))
-        acc_pool = ctx.enter_context(tc.psum_pool(name="acc", bufs=1))
-        psum = ctx.enter_context(tc.psum_pool(name="psum", bufs=2))
+        codes = ctx.enter_context(tc.tile_pool(name="codes", bufs=1))
+        psum = ctx.enter_context(tc.psum_pool(name="psum", bufs=1))
         ctx.enter_context(tc.manual_schedule())
 
         ident_b = const.tile([P, P], BF16, name="ident_b")
         make_identity(nc, ident_b[:])
         ident_f = const.tile([P, P], F32, name="ident_f")
         make_identity(nc, ident_f[:])
-        acc = [acc_pool.tile([P, COLS], F32, name="acc%d" % blk) for blk in range(4)]
 
-        we_t, z_t, g_t, h_t = {}, {}, {}, {}
-        wf_t, dz_t, staged, coded, o_t, w_banks = {}, {}, {}, {}, {}, {}
+        we_t, g_t, h_t = {}, {}, {}
+        z_t = [loads.tile([P, 4, COLS], F32, name="z") for s in range(S)]
+        wf_t, dz_t, staged, coded, o_t, w_banks, acc = {}, {}, {}, {}, {}, {}, {}
 
         def rows(ap):
             return ap.rearrange("(p j) w -> p j w", j=4)
 
-        def load(store, s, src, dtype, name, js=ROWS):
+        def load(store, s, src, dtype, name, bufs):
             if s < S:
-                if js.start == 0:
-                    store[s] = loads.tile([P, 4, COLS], dtype, name=name)
-                nc.sync.dma_start(out=store[s][:, js, :], in_=rows(src[s])[:, js, :])
+                store[s] = loads.tile([P, 4, COLS], dtype, name=name, bufs=bufs)
+                nc.sync.dma_start(out=store[s][:], in_=rows(src[s]))
 
-        def load_we(s, js=ROWS):
-            load(we_t, s, we1, BF16, "we", js)
+        def load_we(s):
+            load(we_t, s, we1, BF16, "we", WE_BUFS)
 
         def load_h(s):
-            load(h_t, s, h0, BF16, "h")
+            load(h_t, s, h0, BF16, "h", H_BUFS)
 
-        def load_zg(s, js=ROWS):
-            load(z_t, s, z, F32, "z", js)
-            load(g_t, s, grad_out, BF16, "g", js)
+        def load_z(s):
+            if s < S:
+                nc.sync.dma_start(out=z_t[s][:], in_=rows(z[s]))
 
-        def place(kind, s):
-            return {"w": ("e4", s, 0), "h": ("e4", s, COLS), "df": ("e5", s, 0), "dt": ("e5", s, COLS)}[kind]
+        def load_g(s):
+            load(g_t, s, grad_out, BF16, "g", G_BUFS)
 
         def stage(kind, s):
-            pair, n, at = place(kind, s)
-            if (pair, n) not in staged:
-                staged[pair, n] = mid.tile([P, 8 * COLS], BF16, name=pair, align_bytes=256)
-            return staged[pair, n][:, 4 * at : 4 * (at + COLS)]
-
-        def quantize_pair(pair, n, lo=0, hi=2 * COLS):
-            if (pair, n) not in coded:
-                words = codes.tile([P, 2 * COLS], U32, name=pair + "c", align_bytes=256, bufs=CODE_BUFS)
-                scales = codes.tile([P, 2 * COLS], U8, name=pair + "s", align_bytes=256, bufs=CODE_BUFS)
-                coded[pair, n] = (words, scales)
-            words, scales = coded[pair, n]
-            nc.vector.quantize_mx(
-                out=words[:, lo:hi].bitcast(FORMAT[pair]),
-                scales=scales[:, lo:hi],
-                in_=staged[pair, n][:, 4 * lo : 4 * hi],
-            )
+            if (kind, s) not in staged:
+                staged[kind, s] = mid.tile([P, 4 * COLS], BF16, name=kind, align_bytes=256)
+            return staged[kind, s][:]
 
         def quantize(kind, s, lo=0, hi=COLS):
-            pair, n, at = place(kind, s)
-            quantize_pair(pair, n, at + lo, at + hi)
+            if not 0 <= s < S:
+                return
+            if (kind, s) not in coded:
+                words = codes.tile([P, COLS], U32, name=kind + "c", align_bytes=256, bufs=CODE_BUFS[kind])
+                scales = codes.tile([P, COLS], U8, name=kind + "s", align_bytes=256, bufs=CODE_BUFS[kind])
+                coded[kind, s] = (words, scales)
+            words, scales = coded[kind, s]
+            nc.vector.quantize_mx(
+                out=words[:, lo:hi].bitcast(FORMAT[kind]),
+                scales=scales[:, lo:hi],
+                in_=staged[kind, s][:, 4 * lo : 4 * hi],
+            )
 
         def operand(kind, s, lo, hi):
-            pair, n, at = place(kind, s)
-            words, scales = coded[pair, n]
-            return words[:, at + lo : at + hi].bitcast(FORMAT[pair]), scales[:, at + lo : at + hi]
+            words, scales = coded[kind, s]
+            return words[:, lo:hi].bitcast(FORMAT[kind]), scales[:, lo:hi]
 
         def mask(s, js=ROWS, cols=slice(0, D2)):
             if s not in dz_t:
@@ -149,16 +147,23 @@ def tile_bnn_pb_v_kernel(tc, h0, wm1, wv1, bm1, bv1, we1, be1, z, grad_out, out_
                 op1=ALU.add,
             )
 
-        def we_cast(s, copy=on_scalar):
-            wf_t[s] = mid.tile([P, 4, P], F32, name="wf")
-            copy(out=wf_t[s][:], in_=we_t[s][:, :, PLAIN::4])
+        def we_cast(s):
+            if s < S:
+                wf_t[s] = mid.tile([P, 4, P], F32, name="wf", bufs=3)
+                on_scalar(out=wf_t[s][:], in_=we_t[s][:, :, PLAIN::4])
 
-        def w_matmul(s, j, t):
-            if t == 0:
-                w_banks[s, j] = psum.tile([P, 4, P], F32, name="w_bank")
-            nc.tensor.matmul(
-                w_banks[s, j][:, t, :], lhsT=we_t[s][:, j, t::4], rhs=ident_b[:], start=(t == 0), stop=False
+        def we_cast_on_gpsimd(s):
+            wf_t[s] = mid.tile([P, 4, P], F32, name="wf", bufs=3)
+            nc.gpsimd.tensor_scalar(
+                out=wf_t[s][:], in0=we_t[s][:, :, PLAIN::4], scalar1=1.0, scalar2=0.0, op0=ALU.mult, op1=ALU.add
             )
+
+        def w_matmuls(s, j):
+            w_banks[s, j] = psum.tile([P, 4, P], F32, name=HEAD_BANKS.get(s, W_BANKS)[j])
+            for t in range(PLAIN if s > 0 else 4):
+                nc.tensor.matmul(
+                    w_banks[s, j][:, t, :], lhsT=we_t[s][:, j, t::4], rhs=ident_b[:], start=(t == 0), stop=False
+                )
 
         def w_transposes(s, j):
             bank = w_banks[s, j]
@@ -181,20 +186,30 @@ def tile_bnn_pb_v_kernel(tc, h0, wm1, wv1, bm1, bv1, we1, be1, z, grad_out, out_
                 op1=ALU.mult,
             )
 
-        def word_bank(src, half):
-            bank = psum.tile([P, 2, 2, P], F32, name="bank")
+        turn = []
+
+        def next_bank(banks=COPY_BANKS):
+            turn.append(None)
+            return banks[len(turn) % len(banks)]
+
+        def word_bank(src, half, tag=None):
+            bank = psum.tile([P, 2, 2, P], F32, name=tag or next_bank())
             for k in range(2):
                 words = src[:, 2 * half + k, :].bitcast(F32)
                 for u in range(2):
                     nc.tensor.transpose(bank[:, k, u, :], words[:, u::2], ident_f[:])
             return bank
 
-        def dz_bank(s, half):
-            bank = word_bank(dz_t[s], half)
+        def dz_bank(s, half, copy=on_scalar, tag=None):
+            bank = word_bank(dz_t[s], half, tag)
             dt = stage("df", s)[:, 2 * COLS * half : 2 * COLS * (half + 1)].bitcast(F32)
-            on_scalar(out=dt.rearrange("p (k x u) -> p k x u", k=2, u=2), in_=bank[:].rearrange("p k u x -> p k x u"))
+            copy(out=dt.rearrange("p (k x u) -> p k x u", k=2, u=2), in_=bank[:].rearrange("p k u x -> p k x u"))
 
         def weight_grad(s, blk):
+            if s < 0:
+                return
+            if s == 0:
+                acc[blk] = psum.tile([P, COLS], F32, name=ACC_BANKS[blk])
             hc, hs = operand("h", s, P * blk, P * (blk + 1))
             dc, ds = operand("dt", s, 0, COLS)
             nc.tensor.matmul_mx(
@@ -208,14 +223,16 @@ def tile_bnn_pb_v_kernel(tc, h0, wm1, wv1, bm1, bv1, we1, be1, z, grad_out, out_
             )
 
         def finish_weight_grad(blk, copy):
-            result = loads.tile([P, COLS], F32, name="we")
+            result = loads.tile([P, COLS], F32, name="we", bufs=WE_BUFS)
             copy(out=result[:], in_=acc[blk][:])
             nc.sync.dma_start(out=out_1[P * blk : P * (blk + 1), :], in_=result[:])
 
-        def input_grad(s, j, tag="bank"):
+        def input_grad(s, j, tag=None, copy=on_scalar):
+            if s < 0:
+                return
             if j == 0:
-                o_t[s] = outs.tile([P, 4, P, 4], F32, name="o")
-            bank = psum.tile([P, 4, P], F32, name=tag)
+                o_t[s] = loads.tile([P, 4, P, 4], F32, name="z", bufs=S)
+            bank = psum.tile([P, 4, P], F32, name=tag or next_bank())
             dc, ds = operand("df", s, P * j, P * (j + 1))
             wc, ws = operand("w", s, 0, COLS)
             nc.tensor.matmul_mx(
@@ -227,38 +244,14 @@ def tile_bnn_pb_v_kernel(tc, h0, wm1, wv1, bm1, bv1, we1, be1, z, grad_out, out_
                 start=True,
                 stop=True,
             )
-            on_scalar(out=o_t[s][:, j, :, :], in_=bank[:].rearrange("p w x -> p x w"))
-            rows_a_store = STORE_ROWS[s]
-            if (j + 1) % rows_a_store == 0:
-                js = slice(j + 1 - rows_a_store, j + 1)
-                src = o_t[s][:, js, :, :].rearrange("p j x w -> p j (x w)")
-                nc.sync.dma_start(out=rows(out_0[s])[:, js, :], in_=src)
+            copy(out=o_t[s][:, j, :, :], in_=bank[:].rearrange("p w x -> p x w"))
+
+        def store(s, js=ROWS):
+            src = o_t[s][:, js, :, :].rearrange("p j x w -> p j (x w)")
+            nc.sync.dma_start(out=rows(out_0[s])[:, js, :], in_=src)
 
         wv_t = mid.tile([P, 4, D2], BF16, name="dz", align_bytes=256, bufs=DZ_BUFS)
         wm_t = mid.tile([P, 4, D2], BF16, name="dz", align_bytes=256, bufs=DZ_BUFS)
-
-        def load_moments(js):
-            nc.sync.dma_start(out=wv_t[:, js, :], in_=rows(wv1)[:, js, :])
-            nc.sync.dma_start(out=wm_t[:, js, :], in_=rows(wm1)[:, js, :])
-
-        load_moments(ROW_HALVES[0])
-        load_we(0)
-        load_moments(ROW_HALVES[1])
-        for js in ROW_HALVES:
-            load_zg(0, js)
-        load_we(1)
-        load_h(0)
-        load_zg(1, ROW_HALVES[0])
-        load_h(1)
-        load_zg(1, ROW_HALVES[1])
-        load_we(2)
-        load_zg(2)
-        load_h(2)
-        for s in range(3, AHEAD):
-            load_we(s)
-            load_h(s)
-            load_zg(s)
-
         ratio = const.tile([P, 4, 4, P], F32, name="ratio")
         std_t = const.tile([P, 4, P, 4], F32, name="std_t")
 
@@ -267,8 +260,7 @@ def tile_bnn_pb_v_kernel(tc, h0, wm1, wv1, bm1, bv1, we1, be1, z, grad_out, out_
                 out=ratio[:, j, :, :], in_=wv_t[:, j, :].rearrange("p (m t) -> p t m", t=4), func=ACT.Exp, scale=-0.5
             )
 
-        def std_rows(half):
-            bank = word_bank(wv_t, half)
+        def std_rows(half, bank):
             for k in range(2):
                 nc.scalar.activation(
                     out=std_t[:, 2 * half + k, :, :].rearrange("p x (u e) -> p x u e", e=2),
@@ -288,126 +280,175 @@ def tile_bnn_pb_v_kernel(tc, h0, wm1, wv1, bm1, bv1, we1, be1, z, grad_out, out_
             )
 
         def w_fill(s, j):
-            for t in range(PLAIN if s > 0 else 4):
-                w_matmul(s, j, t)
-            w_transposes(s, j)
+            if s < S:
+                w_matmuls(s, j)
+                w_transposes(s, j)
 
-        for j in (0, 1):
-            inverse_std(j)
+        load_we(0)
+        for js in ROW_HALVES:
+            nc.sync.dma_start(out=wv_t[:, js, :], in_=rows(wv1)[:, js, :])
+            nc.sync.dma_start(out=wm_t[:, js, :], in_=rows(wm1)[:, js, :])
+        for s in range(LEAD):
+            load_we(s + 1)
+            load_h(s)
+
+        def load_step(s):
+            load_z(s)
+            load_g(s)
+            if s == 0:
+                load_we(LEAD + 1)
+            for n in H_LOADS.get(s, ()):
+                load_h(n)
+            if s > 0:
+                load_we(s + LEAD + 1)
+
+        load_step(0)
+
+        for j in range(2):
+            w_matmuls(0, j)
+        inverse_std(0)
+        inverse_std(1)
+        banks = [word_bank(wv_t, half) for half in range(2)]
+        inverse_std(2)
+        inverse_std(3)
+        for j in range(4):
             ratio_row(j)
-        std_rows(0)
-        w_fill(0, 0)
-        for j in (2, 3):
-            inverse_std(j)
-        std_rows(1)
-        w_fill(0, 1)
-        w_out(0, 0)
-        for j in (2, 3):
-            ratio_row(j)
-        w_fill(0, 2)
-        mask(0, ROW_HALVES[0])
-        dz_bank(0, 0)
-        w_out(0, 1)
-        w_fill(0, 3)
-        mask(0, ROW_HALVES[1])
-        load_we(AHEAD)
-        load_zg(AHEAD)
-        dz_bank(0, 1)
-        we_cast(1)
-        w_out(0, 2)
-        w_fill(1, 0)
-        w_out(0, 3)
-        w_fill(1, 1)
-        h_interleave(0, on_scalar, 0, D1)
-        load_h(AHEAD)
-        quantize("w", 0)
-        quantize("df", 0)
-        d_interleave(0, on_vector, 0, D0_CUT)
-        d_interleave(0, on_scalar, D0_CUT, D2)
+        for j in range(2, 4):
+            w_matmuls(0, j)
+        for half in range(2):
+            std_rows(half, banks[half])
+        for s in range(1, LEAD + 1):
+            we_cast_on_gpsimd(s)
+        for s in range(LEAD):
+            for j in range(4):
+                w_transposes(s, j)
+                w_out(s, j)
+                w_matmuls(s + 1, j)
+                if j == 1:
+                    quantize("w", s - 1)
+            h_interleave(s, on_scalar, 0, D1)
+            load_step(s + 1)
+        for j in range(4):
+            w_transposes(LEAD, j)
 
         last = S - 1
 
-        def fill(s, j, outs_from, accs_from, between):
-            for k in range(2):
-                if outs_from[0] >= 0:
-                    input_grad(outs_from[0], outs_from[1] + k)
-                if accs_from[0] >= 0:
-                    weight_grad(accs_from[0], accs_from[1] + k)
-                w_fill(s, j + k)
-                if k == 0:
-                    between()
-
-        def mask_by_columns(s):
-            mask(s, cols=slice(0, HALF))
-            d_on_gpsimd(s, 0, G_D)
-            mask(s, cols=slice(HALF, D2))
-            load_zg(s + AHEAD)
-
-        mask(1, ROW_HALVES[0])
-        w_out(1, 0)
-        w_out(1, 1)
-        fill(1, 2, (0, 0), (-1, 0), lambda: we_cast(2))
-        load_we(1 + AHEAD)
-        h_interleave(1, on_scalar, 0, H_MID)
-        dz_bank(1, 0)
         quantize("h", 0)
-        quantize("dt", 0)
-        mask(1, ROW_HALVES[1])
-        load_zg(1 + AHEAD)
-        w_out(1, 2)
-        w_out(1, 3)
-        d_interleave(1, on_vector, 0, D2)
-        fill(2, 0, (0, 2), (0, 0), lambda: h_interleave(1, on_scalar, H_MID, D1))
-        load_h(1 + AHEAD)
-        h_interleave(2, on_scalar, 0, H_MID)
-        dz_bank(1, 1)
+        w_out(LEAD, 0)
+        w_out(LEAD, 1)
+        we_cast(LEAD + 1)
+        w_matmuls(LEAD + 1, 0)
+        w_matmuls(LEAD + 1, 1)
+        w_transposes(LEAD + 1, 0)
+        mask(0, cols=slice(0, HALF))
+        h_interleave(LEAD, on_scalar, 0, H_MID)
+        mask(0, cols=slice(HALF, D2))
+        dz_bank(0, 0)
+        dz_bank(0, 1)
+        quantize("w", LEAD - 1)
+        d_on_gpsimd(0, 0, G_D)
+        w_out(LEAD, 2)
+        w_out(LEAD, 3)
+        w_transposes(LEAD + 1, 1)
+        w_fill(LEAD + 1, 2)
+        d_interleave(0, on_vector, G_D, D2)
+        h_interleave(LEAD, on_scalar, H_MID, D1)
+        quantize("df", 0)
+        input_grad(0, 0)
+        input_grad(0, 1)
+        w_fill(LEAD + 1, 3)
+        load_step(LEAD + 1)
+        we_cast(LEAD + 2)
 
-        for s in range(2, last):
-            mask_by_columns(s)
-            w_out(s, 0)
-            w_out(s, 1)
-            fill(s, 2, (s - 2 if s > 2 else -1, 2), (s - 2, 2), lambda: we_cast(s + 1))
-            load_we(s + AHEAD)
-            h_interleave(s, on_scalar, H_MID, D1)
-            load_h(s + AHEAD)
+
+        for s in range(1, S - LEAD):
+            ahead = s + LEAD
+            d_cut = (G_D + V_D + D2) // 2
+            if s == 2:
+                quantize("h", s)
+                h_interleave(ahead, on_scalar, 0, G_H)
+            mask(s)
+            d_on_gpsimd(s, 0, G_D)
+            if s > 1:
+                quantize("df", s - 1)
+            w_out(ahead, 0)
+            w_out(ahead, 1)
+            if s > 1:
+                input_grad(s - 1, 0)
+                w_fill(ahead, 2)
+            d_interleave(s, on_scalar, G_D + V_D, d_cut)
+            if s > 1:
+                input_grad(s - 1, 1)
+                w_fill(ahead, 3)
+                we_cast(ahead + 1)
             dz_bank(s, 0)
             d_interleave(s, on_vector, G_D, G_D + V_D)
-            quantize_pair("e4", s - 1)
-            if s + 1 < last:
-                h_on_gpsimd(s + 1, 0, G_H)
-            quantize_pair("e5", s - 1)
-            w_out(s, 2)
-            w_out(s, 3)
-            cuts = (G_H, H_MID) if s + 1 < last else (H_LAST, D1)
-            fill(s + 1, 0, (s - 1, 0), (s - 1, 0), lambda: h_interleave(s + 1, on_scalar, *cuts))
-            d_interleave(s, on_scalar, G_D + V_D, D2)
+            quantize("dt", s - 1)
+            quantize("h", s + 1 if s > 1 else s)
+            later = ahead + 1 if s > 1 else ahead
+            if later < S:
+                h_on_gpsimd(later, 0, G_H)
+            else:
+                mask(s + 1, cols=slice(0, HALF))
+                d_on_gpsimd(s + 1, 0, G_D)
+            quantize("w", ahead - 1)
+            weight_grad(s - 1, 2)
+            d_interleave(s, on_scalar, d_cut, D2)
             dz_bank(s, 1)
+            w_out(ahead, 2)
+            w_out(ahead, 3)
+            w_fill(ahead + 1, 0)
+            if ahead < last:
+                h_interleave(ahead, on_scalar, G_H, H_MID)
+            input_grad(s - 1, 2)
+            weight_grad(s - 1, 3)
+            w_fill(ahead + 1, 1)
+            if ahead < last:
+                h_interleave(ahead, on_scalar, H_MID, D1)
+            input_grad(s - 1, 3)
+            weight_grad(s - 1, 0)
+            weight_grad(s - 1, 1)
+            load_step(s + LEAD + 1)
+            if s >= 4:
+                for n in range(s) if s == 4 else (s - 1,):
+                    store(n)
 
-        mask_by_columns(last)
-        w_out(last, 0)
-        w_out(last, 1)
-        fill(last, 2, (last - 2, 2), (last - 2, 2), lambda: dz_bank(last, 0))
-        dz_bank(last, 1)
-        quantize("w", last - 1)
-        quantize("df", last - 1)
-        w_out(last, 2)
-        d_interleave(last, on_vector, G_D, D2)
-        w_out(last, 3)
-        for q in range(4):
-            input_grad(last - 1, q, tag="bank" if q < 2 else "w_bank")
-        quantize("h", last - 1)
-        quantize("df", last)
+        def outs(n):
+            for q in range(4):
+                input_grad(n, q, tag=next_bank(TAIL_BANKS))
+                if q % 2:
+                    store(n, ROW_HALVES[q // 2])
+
+        def dz_banks(n):
+            for half in range(2):
+                dz_bank(n, half, on_scalar, next_bank(TAIL_BANKS))
+
+        s = last - 1
+        mask(s, cols=slice(HALF, D2))
+        dz_banks(s)
+        quantize("df", s - 1)
+        mask(last)
+        outs(s - 1)
+        quantize("df", s)
+        quantize("dt", s - 1)
+        dz_banks(last)
         quantize("w", last)
-        for q in range(4):
-            input_grad(last, q, tag="bank" if q < 2 else "w_bank")
-        quantize("dt", last - 1)
-        h_interleave(last, on_vector, 0, P)
+        d_interleave(s, on_vector, G_D, D2)
+        outs(s)
+        quantize("df", last)
+        for blk in range(2):
+            weight_grad(s - 1, blk)
+        quantize("dt", s)
+        outs(last)
+        for blk in range(2, 4):
+            weight_grad(s - 1, blk)
+        d_interleave(last, on_vector, 0, D2)
+        h_interleave(last, on_vector, G_H, D1)
+        for blk in range(4):
+            weight_grad(s, blk)
         quantize("dt", last)
         for blk in range(4):
-            weight_grad(last - 1, blk)
-        for blk in range(4):
-            if P * (blk + 1) < H_LAST:
-                h_interleave(last, on_vector, P * (blk + 1), P * (blk + 2))
             quantize("h", last, P * blk, P * (blk + 1))
             weight_grad(last, blk)
-            finish_weight_grad(blk, on_scalar)
+        for blk in range(4):
+            finish_weight_grad(blk, on_vector if blk % 2 else on_scalar)

@@ -30,17 +30,15 @@ WE_BUFS = 5
 G_BUFS = 6
 H_BUFS = 5
 DZ_BUFS = 3
-H_LOADS = {0: (2,), 1: (3,), 2: (4, 5), 3: (6,), 4: (7,)}
 W_BANKS = ("w0", "w1", "w0", "w1")
 COPY_BANKS = ("c0", "c1")
 ACC_BANKS = ("a0", "a1", "a2", "a3")
 TAIL_BANKS = ("c0", "w0", "w1", "c1")
 HEAD_BANKS = {0: ACC_BANKS, 1: ("w0", "w1", "c1", "c0"), 2: ACC_BANKS, 3: ("w0", "w1", "a0", "a1")}
-CODE_BUFS = {"w": 4, "h": 4, "df": 2, "dt": 2}
+CODE_BUFS = {"w": 4, "h": 5, "df": 2, "dt": 3}
 H_MID = 304
 G_D = 160
 G_H = 160
-V_D = 64
 
 
 def tile_bnn_pb_v_kernel(tc, h0, wm1, wv1, bm1, bv1, we1, be1, z, grad_out, out_0, out_1):
@@ -291,14 +289,14 @@ def tile_bnn_pb_v_kernel(tc, h0, wm1, wv1, bm1, bv1, we1, be1, z, grad_out, out_
         for s in range(LEAD):
             load_we(s + 1)
             load_h(s)
+        load_h(LEAD)
 
         def load_step(s):
             load_z(s)
             load_g(s)
             if s == 0:
                 load_we(LEAD + 1)
-            for n in H_LOADS.get(s, ()):
-                load_h(n)
+            load_h(s + LEAD + 1)
             if s > 0:
                 load_we(s + LEAD + 1)
 
@@ -326,6 +324,7 @@ def tile_bnn_pb_v_kernel(tc, h0, wm1, wv1, bm1, bv1, we1, be1, z, grad_out, out_
                 w_matmuls(s + 1, j)
                 if j == 1:
                     quantize("w", s - 1)
+                    quantize("h", s - 1)
             h_interleave(s, on_scalar, 0, D1)
             load_step(s + 1)
         for j in range(4):
@@ -333,15 +332,16 @@ def tile_bnn_pb_v_kernel(tc, h0, wm1, wv1, bm1, bv1, we1, be1, z, grad_out, out_
 
         last = S - 1
 
-        quantize("h", 0)
+        h_interleave(LEAD, on_scalar, 0, D1)
         w_out(LEAD, 0)
         w_out(LEAD, 1)
+        quantize("h", 1)
         we_cast(LEAD + 1)
         w_matmuls(LEAD + 1, 0)
         w_matmuls(LEAD + 1, 1)
         w_transposes(LEAD + 1, 0)
         mask(0, cols=slice(0, HALF))
-        h_interleave(LEAD, on_scalar, 0, H_MID)
+        h_interleave(LEAD + 1, on_scalar, 0, H_MID)
         mask(0, cols=slice(HALF, D2))
         dz_bank(0, 0)
         dz_bank(0, 1)
@@ -352,7 +352,7 @@ def tile_bnn_pb_v_kernel(tc, h0, wm1, wv1, bm1, bv1, we1, be1, z, grad_out, out_
         w_transposes(LEAD + 1, 1)
         w_fill(LEAD + 1, 2)
         d_interleave(0, on_vector, G_D, D2)
-        h_interleave(LEAD, on_scalar, H_MID, D1)
+        h_interleave(LEAD + 1, on_scalar, H_MID, D1)
         quantize("df", 0)
         input_grad(0, 0)
         input_grad(0, 1)
@@ -363,10 +363,7 @@ def tile_bnn_pb_v_kernel(tc, h0, wm1, wv1, bm1, bv1, we1, be1, z, grad_out, out_
 
         for s in range(1, S - LEAD):
             ahead = s + LEAD
-            d_cut = (G_D + V_D + D2) // 2
-            if s == 2:
-                quantize("h", s)
-                h_interleave(ahead, on_scalar, 0, G_H)
+            d_cut = (G_D + D2) // 2
             mask(s)
             d_on_gpsimd(s, 0, G_D)
             if s > 1:
@@ -376,16 +373,15 @@ def tile_bnn_pb_v_kernel(tc, h0, wm1, wv1, bm1, bv1, we1, be1, z, grad_out, out_
             if s > 1:
                 input_grad(s - 1, 0)
                 w_fill(ahead, 2)
-            d_interleave(s, on_scalar, G_D + V_D, d_cut)
+            d_interleave(s, on_scalar, G_D, d_cut)
             if s > 1:
                 input_grad(s - 1, 1)
                 w_fill(ahead, 3)
                 we_cast(ahead + 1)
             dz_bank(s, 0)
-            d_interleave(s, on_vector, G_D, G_D + V_D)
             quantize("dt", s - 1)
-            quantize("h", s + 1 if s > 1 else s)
-            later = ahead + 1 if s > 1 else ahead
+            quantize("h", s + 1)
+            later = ahead + 1
             if later < S:
                 h_on_gpsimd(later, 0, G_H)
             else:
@@ -393,26 +389,27 @@ def tile_bnn_pb_v_kernel(tc, h0, wm1, wv1, bm1, bv1, we1, be1, z, grad_out, out_
                 d_on_gpsimd(s + 1, 0, G_D)
             quantize("w", ahead - 1)
             weight_grad(s - 1, 2)
+            weight_grad(s - 1, 3)
             d_interleave(s, on_scalar, d_cut, D2)
             dz_bank(s, 1)
             w_out(ahead, 2)
             w_out(ahead, 3)
             w_fill(ahead + 1, 0)
             if ahead < last:
-                h_interleave(ahead, on_scalar, G_H, H_MID)
+                h_interleave(later, on_scalar, G_H, H_MID)
             input_grad(s - 1, 2)
-            weight_grad(s - 1, 3)
+            weight_grad(s - 1, 0)
             w_fill(ahead + 1, 1)
             if ahead < last:
-                h_interleave(ahead, on_scalar, H_MID, D1)
+                h_interleave(later, on_scalar, H_MID, D1)
             input_grad(s - 1, 3)
-            weight_grad(s - 1, 0)
             weight_grad(s - 1, 1)
             load_step(s + LEAD + 1)
             if s >= 4:
-                for n in range(s) if s == 4 else (s - 1,):
+                for n in range(s) if s == 4 else ():
                     store(n)
 
+        turn.clear()
         def outs(n):
             for q in range(4):
                 input_grad(n, q, tag=next_bank(TAIL_BANKS))
@@ -424,31 +421,32 @@ def tile_bnn_pb_v_kernel(tc, h0, wm1, wv1, bm1, bv1, we1, be1, z, grad_out, out_
                 dz_bank(n, half, on_scalar, next_bank(TAIL_BANKS))
 
         s = last - 1
+        for js in ROW_HALVES:
+            store(s - 2, js)
         mask(s, cols=slice(HALF, D2))
         dz_banks(s)
         quantize("df", s - 1)
         mask(last)
         outs(s - 1)
-        quantize("df", s)
         quantize("dt", s - 1)
+        quantize("df", s)
         dz_banks(last)
+        quantize("h", last)
         quantize("w", last)
-        d_interleave(s, on_vector, G_D, D2)
+        weight_grad(s - 1, 0)
+        weight_grad(s - 1, 1)
         outs(s)
+        d_interleave(s, on_vector, G_D, D2)
         quantize("df", last)
-        for blk in range(2):
-            weight_grad(s - 1, blk)
+        weight_grad(s - 1, 2)
+        weight_grad(s - 1, 3)
         quantize("dt", s)
         outs(last)
-        for blk in range(2, 4):
-            weight_grad(s - 1, blk)
         d_interleave(last, on_vector, 0, D2)
-        h_interleave(last, on_vector, G_H, D1)
         for blk in range(4):
             weight_grad(s, blk)
         quantize("dt", last)
         for blk in range(4):
-            quantize("h", last, P * blk, P * (blk + 1))
             weight_grad(last, blk)
         for blk in range(4):
-            finish_weight_grad(blk, on_vector if blk % 2 else on_scalar)
+            finish_weight_grad(blk, on_scalar if blk % 2 else on_vector)

@@ -26,10 +26,9 @@ PLAIN = 3
 STD_FLOOR = 2.0**-63
 FORMAT = {"w": E4M3, "h": E4M3, "df": E5M2, "dt": E5M2}
 LEAD = 2
-WE_BUFS = 5
-G_BUFS = 6
-H_BUFS = 5
+LOAD_BUFS = {("we", 1): 3, ("h", 1): 3, ("g", 1): 3, ("we", 2): 1, ("h", 2): 1, ("g", 2): 2}
 DZ_BUFS = 3
+STAGE_BUFS = {"w": 2, "h": 2, "df": 2, "dt": 3}
 W_BANKS = ("w0", "w1", "w0", "w1")
 COPY_BANKS = ("c0", "c1")
 ACC_BANKS = ("a0", "a1", "a2", "a3")
@@ -58,33 +57,39 @@ def tile_bnn_pb_v_kernel(tc, h0, wm1, wv1, bm1, bv1, we1, be1, z, grad_out, out_
         make_identity(nc, ident_f[:])
 
         we_t, g_t, h_t = {}, {}, {}
-        z_t = [loads.tile([P, 4, COLS], F32, name="z") for s in range(S)]
-        wf_t, dz_t, staged, coded, o_t, w_banks, acc = {}, {}, {}, {}, {}, {}, {}
+        z_all = loads.tile([P, S, 4, COLS], F32, name="z", bufs=1)
+        wf_t, dz_t, staged, coded, w_banks, acc = {}, {}, {}, {}, {}, {}
 
         def rows(ap):
             return ap.rearrange("(p j) w -> p j w", j=4)
 
-        def load(store, s, src, dtype, name, bufs):
-            if s < S:
-                store[s] = loads.tile([P, 4, COLS], dtype, name=name, bufs=bufs)
-                nc.sync.dma_start(out=store[s][:], in_=rows(src[s]))
+        def rows_of(src, first, count):
+            return src[first : first + count].rearrange("s (p j) w -> p s (j w)", j=4)
 
-        def load_we(s):
-            load(we_t, s, we1, BF16, "we", WE_BUFS)
+        def load(store, src, name, first, count=1):
+            tile = loads.tile([P, count, 4, COLS], BF16, name=name + str(count), bufs=LOAD_BUFS[name, count])
+            nc.sync.dma_start(out=tile[:].rearrange("p s j w -> p s (j w)"), in_=rows_of(src, first, count))
+            for k in range(count):
+                store[first + k] = tile[:, k, :, :]
 
-        def load_h(s):
-            load(h_t, s, h0, BF16, "h", H_BUFS)
+        def load_we(first, count=1):
+            load(we_t, we1, "we", first, count)
 
-        def load_z(s):
-            if s < S:
-                nc.sync.dma_start(out=z_t[s][:], in_=rows(z[s]))
+        def load_h(first, count=1):
+            load(h_t, h0, "h", first, count)
 
-        def load_g(s):
-            load(g_t, s, grad_out, BF16, "g", G_BUFS)
+        def load_g(first, count=1):
+            load(g_t, grad_out, "g", first, count)
+
+        def z_rows(first, count):
+            return z_all[:, first : first + count, :, :].rearrange("p s j w -> p s (j w)")
+
+        def load_z(first, count=1):
+            nc.sync.dma_start(out=z_rows(first, count), in_=rows_of(z, first, count))
 
         def stage(kind, s):
             if (kind, s) not in staged:
-                staged[kind, s] = mid.tile([P, 4 * COLS], BF16, name=kind, align_bytes=256)
+                staged[kind, s] = mid.tile([P, 4 * COLS], BF16, name=kind, align_bytes=256, bufs=STAGE_BUFS[kind])
             return staged[kind, s][:]
 
         def quantize(kind, s, lo=0, hi=COLS):
@@ -110,7 +115,7 @@ def tile_bnn_pb_v_kernel(tc, h0, wm1, wv1, bm1, bv1, we1, be1, z, grad_out, out_
                 dz_t[s] = mid.tile([P, 4, COLS], BF16, name="dz", align_bytes=256, bufs=DZ_BUFS)
             nc.vector.scalar_tensor_tensor(
                 out=dz_t[s][:, js, cols],
-                in0=z_t[s][:, js, cols],
+                in0=z_all[:, s, js, cols],
                 scalar=0.0,
                 in1=g_t[s][:, js, cols],
                 op0=ALU.is_gt,
@@ -147,11 +152,11 @@ def tile_bnn_pb_v_kernel(tc, h0, wm1, wv1, bm1, bv1, we1, be1, z, grad_out, out_
 
         def we_cast(s):
             if s < S:
-                wf_t[s] = mid.tile([P, 4, P], F32, name="wf", bufs=3)
+                wf_t[s] = mid.tile([P, 4, P], F32, name="wf")
                 on_scalar(out=wf_t[s][:], in_=we_t[s][:, :, PLAIN::4])
 
         def we_cast_on_gpsimd(s):
-            wf_t[s] = mid.tile([P, 4, P], F32, name="wf", bufs=3)
+            wf_t[s] = mid.tile([P, 4, P], F32, name="wf")
             nc.gpsimd.tensor_scalar(
                 out=wf_t[s][:], in0=we_t[s][:, :, PLAIN::4], scalar1=1.0, scalar2=0.0, op0=ALU.mult, op1=ALU.add
             )
@@ -220,16 +225,20 @@ def tile_bnn_pb_v_kernel(tc, h0, wm1, wv1, bm1, bv1, we1, be1, z, grad_out, out_
                 stop=(s == S - 1),
             )
 
+        results = {}
+
         def finish_weight_grad(blk, copy):
-            result = loads.tile([P, COLS], F32, name="we", bufs=WE_BUFS)
-            copy(out=result[:], in_=acc[blk][:])
-            nc.sync.dma_start(out=out_1[P * blk : P * (blk + 1), :], in_=result[:])
+            pair, k = divmod(blk, 2)
+            if k == 0:
+                results[pair] = mid.tile([P, 2, COLS], F32, name="w", align_bytes=256)
+            copy(out=results[pair][:, k, :], in_=acc[blk][:])
+            if k == 1:
+                dst = out_1[2 * P * pair : 2 * P * (pair + 1), :].rearrange("(k p) w -> p k w", k=2)
+                nc.sync.dma_start(out=dst, in_=results[pair][:])
 
         def input_grad(s, j, tag=None, copy=on_scalar):
             if s < 0:
                 return
-            if j == 0:
-                o_t[s] = loads.tile([P, 4, P, 4], F32, name="z", bufs=S)
             bank = psum.tile([P, 4, P], F32, name=tag or next_bank())
             dc, ds = operand("df", s, P * j, P * (j + 1))
             wc, ws = operand("w", s, 0, COLS)
@@ -242,11 +251,13 @@ def tile_bnn_pb_v_kernel(tc, h0, wm1, wv1, bm1, bv1, we1, be1, z, grad_out, out_
                 start=True,
                 stop=True,
             )
-            copy(out=o_t[s][:, j, :, :], in_=bank[:].rearrange("p w x -> p x w"))
+            copy(out=z_all[:, s, j, :].rearrange("p (x w) -> p x w", w=4), in_=bank[:].rearrange("p w x -> p x w"))
 
         def store(s, js=ROWS):
-            src = o_t[s][:, js, :, :].rearrange("p j x w -> p j (x w)")
-            nc.sync.dma_start(out=rows(out_0[s])[:, js, :], in_=src)
+            nc.sync.dma_start(out=rows(out_0[s])[:, js, :], in_=z_all[:, s, js, :])
+
+        def store_samples(first, count):
+            nc.sync.dma_start(out=rows_of(out_0, first, count), in_=z_rows(first, count))
 
         wv_t = mid.tile([P, 4, D2], BF16, name="dz", align_bytes=256, bufs=DZ_BUFS)
         wm_t = mid.tile([P, 4, D2], BF16, name="dz", align_bytes=256, bufs=DZ_BUFS)
@@ -292,15 +303,20 @@ def tile_bnn_pb_v_kernel(tc, h0, wm1, wv1, bm1, bv1, we1, be1, z, grad_out, out_
         load_h(LEAD)
 
         def load_step(s):
-            load_z(s)
-            load_g(s)
+            if s < 6:
+                load_z(s)
+            elif s == 6:
+                load_z(s, 2)
+            if s in (3, 5):
+                load_g(s, 2)
+            elif s not in (4, 6):
+                load_g(s)
             if s == 0:
                 load_we(LEAD + 1)
-            load_h(s + LEAD + 1)
-            if s > 0:
-                load_we(s + LEAD + 1)
-
-        load_step(0)
+            if s <= 3:
+                load_h(s + LEAD + 1, 2 if s == 3 else 1)
+            if 0 < s <= 3:
+                load_we(s + LEAD + 1, 2 if s == 3 else 1)
 
         for j in range(2):
             w_matmuls(0, j)
@@ -326,32 +342,33 @@ def tile_bnn_pb_v_kernel(tc, h0, wm1, wv1, bm1, bv1, we1, be1, z, grad_out, out_
                     quantize("w", s - 1)
                     quantize("h", s - 1)
             h_interleave(s, on_scalar, 0, D1)
-            load_step(s + 1)
+            load_step(s)
         for j in range(4):
             w_transposes(LEAD, j)
 
         last = S - 1
 
         h_interleave(LEAD, on_scalar, 0, D1)
+        load_step(LEAD)
         w_out(LEAD, 0)
-        w_out(LEAD, 1)
         quantize("h", 1)
+        quantize("w", 1)
         we_cast(LEAD + 1)
         w_matmuls(LEAD + 1, 0)
         w_matmuls(LEAD + 1, 1)
         w_transposes(LEAD + 1, 0)
         mask(0, cols=slice(0, HALF))
+        d_on_gpsimd(0, 0, HALF)
         h_interleave(LEAD + 1, on_scalar, 0, H_MID)
         mask(0, cols=slice(HALF, D2))
         dz_bank(0, 0)
         dz_bank(0, 1)
-        quantize("w", LEAD - 1)
-        d_on_gpsimd(0, 0, G_D)
+        w_out(LEAD, 1)
         w_out(LEAD, 2)
         w_out(LEAD, 3)
         w_transposes(LEAD + 1, 1)
         w_fill(LEAD + 1, 2)
-        d_interleave(0, on_vector, G_D, D2)
+        d_interleave(0, on_vector, HALF, D2)
         h_interleave(LEAD + 1, on_scalar, H_MID, D1)
         quantize("df", 0)
         input_grad(0, 0)
@@ -364,10 +381,14 @@ def tile_bnn_pb_v_kernel(tc, h0, wm1, wv1, bm1, bv1, we1, be1, z, grad_out, out_
         for s in range(1, S - LEAD):
             ahead = s + LEAD
             d_cut = (G_D + D2) // 2
-            mask(s)
-            d_on_gpsimd(s, 0, G_D)
             if s > 1:
+                mask(s)
+                d_on_gpsimd(s, 0, G_D)
                 quantize("df", s - 1)
+            else:
+                mask(s, cols=slice(0, HALF))
+                d_on_gpsimd(s, 0, G_D)
+                mask(s, cols=slice(HALF, D2))
             w_out(ahead, 0)
             w_out(ahead, 1)
             if s > 1:
@@ -379,17 +400,18 @@ def tile_bnn_pb_v_kernel(tc, h0, wm1, wv1, bm1, bv1, we1, be1, z, grad_out, out_
                 w_fill(ahead, 3)
                 we_cast(ahead + 1)
             dz_bank(s, 0)
-            quantize("dt", s - 1)
-            quantize("h", s + 1)
             later = ahead + 1
             if later < S:
+                quantize("dt", s - 1)
+                quantize("h", s + 1)
                 h_on_gpsimd(later, 0, G_H)
             else:
                 mask(s + 1, cols=slice(0, HALF))
                 d_on_gpsimd(s + 1, 0, G_D)
             quantize("w", ahead - 1)
-            weight_grad(s - 1, 2)
-            weight_grad(s - 1, 3)
+            if later < S:
+                weight_grad(s - 1, 2)
+                weight_grad(s - 1, 3)
             d_interleave(s, on_scalar, d_cut, D2)
             dz_bank(s, 1)
             w_out(ahead, 2)
@@ -398,21 +420,25 @@ def tile_bnn_pb_v_kernel(tc, h0, wm1, wv1, bm1, bv1, we1, be1, z, grad_out, out_
             if ahead < last:
                 h_interleave(later, on_scalar, G_H, H_MID)
             input_grad(s - 1, 2)
-            weight_grad(s - 1, 0)
+            if later < S:
+                weight_grad(s - 1, 0)
             w_fill(ahead + 1, 1)
             if ahead < last:
                 h_interleave(later, on_scalar, H_MID, D1)
             input_grad(s - 1, 3)
-            weight_grad(s - 1, 1)
-            load_step(s + LEAD + 1)
-            if s >= 4:
-                for n in range(s) if s == 4 else ():
-                    store(n)
+            if later < S:
+                weight_grad(s - 1, 1)
+            if s <= 4:
+                load_step(s + LEAD + 1)
+            if s == 4:
+                store_samples(0, 2)
+                store_samples(2, 2)
 
         turn.clear()
-        def outs(n):
+        def outs(n, beside=-1):
             for q in range(4):
                 input_grad(n, q, tag=next_bank(TAIL_BANKS))
+                weight_grad(beside, q)
                 if q % 2:
                     store(n, ROW_HALVES[q // 2])
 
@@ -420,33 +446,32 @@ def tile_bnn_pb_v_kernel(tc, h0, wm1, wv1, bm1, bv1, we1, be1, z, grad_out, out_
             for half in range(2):
                 dz_bank(n, half, on_scalar, next_bank(TAIL_BANKS))
 
+        def weight_grads(n):
+            for blk in range(4):
+                weight_grad(n, blk)
+
         s = last - 1
-        for js in ROW_HALVES:
-            store(s - 2, js)
+        store(s - 2)
         mask(s, cols=slice(HALF, D2))
         dz_banks(s)
+        quantize("dt", s - 2)
         quantize("df", s - 1)
         mask(last)
         outs(s - 1)
-        quantize("dt", s - 1)
         quantize("df", s)
         dz_banks(last)
-        quantize("h", last)
         quantize("w", last)
-        weight_grad(s - 1, 0)
-        weight_grad(s - 1, 1)
-        outs(s)
+        outs(s, s - 2)
+        quantize("dt", s - 1)
         d_interleave(s, on_vector, G_D, D2)
+        quantize("h", s)
         quantize("df", last)
-        weight_grad(s - 1, 2)
-        weight_grad(s - 1, 3)
-        quantize("dt", s)
-        outs(last)
+        outs(last, s - 1)
         d_interleave(last, on_vector, 0, D2)
-        for blk in range(4):
-            weight_grad(s, blk)
+        quantize("dt", s)
+        weight_grads(s)
+        quantize("h", last)
         quantize("dt", last)
-        for blk in range(4):
-            weight_grad(last, blk)
+        weight_grads(last)
         for blk in range(4):
             finish_weight_grad(blk, on_scalar if blk % 2 else on_vector)

@@ -32,9 +32,9 @@ STAGE_BUFS = {"w": 2, "h": 2, "df": 2, "dt": 3}
 W_BANKS = ("w0", "w1", "w0", "w1")
 COPY_BANKS = ("c0", "c1")
 ACC_BANKS = ("a0", "a1", "a2", "a3")
-TAIL_BANKS = ("c0", "w0", "w1", "c1")
+TAIL_BANKS = ("w1", "c1", "c0", "w0")
 HEAD_BANKS = {0: ACC_BANKS, 1: ("w0", "w1", "c1", "c0"), 2: ACC_BANKS, 3: ("w0", "w1", "a0", "a1")}
-CODE_BUFS = {"w": 4, "h": 5, "df": 2, "dt": 3}
+CODE_BUFS = {"w": 3, "h": 4, "df": 2, "dt": 3}
 H_MID = 304
 G_D = 160
 G_H = 160
@@ -313,7 +313,9 @@ def tile_bnn_pb_v_kernel(tc, h0, wm1, wv1, bm1, bv1, we1, be1, z, grad_out, out_
                 load_g(s)
             if s == 0:
                 load_we(LEAD + 1)
-            if s <= 3:
+            if s == 1:
+                load_h(LEAD + 1)
+            if 0 < s <= 3:
                 load_h(s + LEAD + 1, 2 if s == 3 else 1)
             if 0 < s <= 3:
                 load_we(s + LEAD + 1, 2 if s == 3 else 1)
@@ -359,8 +361,8 @@ def tile_bnn_pb_v_kernel(tc, h0, wm1, wv1, bm1, bv1, we1, be1, z, grad_out, out_
         w_transposes(LEAD + 1, 0)
         mask(0, cols=slice(0, HALF))
         d_on_gpsimd(0, 0, HALF)
-        h_interleave(LEAD + 1, on_scalar, 0, H_MID)
         mask(0, cols=slice(HALF, D2))
+        d_interleave(0, on_scalar, HALF, D2)
         dz_bank(0, 0)
         dz_bank(0, 1)
         w_out(LEAD, 1)
@@ -368,37 +370,27 @@ def tile_bnn_pb_v_kernel(tc, h0, wm1, wv1, bm1, bv1, we1, be1, z, grad_out, out_
         w_out(LEAD, 3)
         w_transposes(LEAD + 1, 1)
         w_fill(LEAD + 1, 2)
-        d_interleave(0, on_vector, HALF, D2)
-        h_interleave(LEAD + 1, on_scalar, H_MID, D1)
-        quantize("df", 0)
-        input_grad(0, 0)
-        input_grad(0, 1)
         w_fill(LEAD + 1, 3)
+        h_interleave(LEAD + 1, on_scalar, 0, D1)
         load_step(LEAD + 1)
-        we_cast(LEAD + 2)
 
 
         for s in range(1, S - LEAD):
             ahead = s + LEAD
             d_cut = (G_D + D2) // 2
-            if s > 1:
-                mask(s)
-                d_on_gpsimd(s, 0, G_D)
-                quantize("df", s - 1)
-            else:
-                mask(s, cols=slice(0, HALF))
-                d_on_gpsimd(s, 0, G_D)
-                mask(s, cols=slice(HALF, D2))
+            mask(s)
+            d_on_gpsimd(s, 0, G_D)
+            quantize("df", s - 1)
             w_out(ahead, 0)
             w_out(ahead, 1)
+            input_grad(s - 1, 0)
             if s > 1:
-                input_grad(s - 1, 0)
                 w_fill(ahead, 2)
             d_interleave(s, on_scalar, G_D, d_cut)
+            input_grad(s - 1, 1)
             if s > 1:
-                input_grad(s - 1, 1)
                 w_fill(ahead, 3)
-                we_cast(ahead + 1)
+            we_cast(ahead + 1)
             dz_bank(s, 0)
             later = ahead + 1
             if later < S:
@@ -419,13 +411,13 @@ def tile_bnn_pb_v_kernel(tc, h0, wm1, wv1, bm1, bv1, we1, be1, z, grad_out, out_
             w_fill(ahead + 1, 0)
             if ahead < last:
                 h_interleave(later, on_scalar, G_H, H_MID)
-            input_grad(s - 1, 2)
+            input_grad(s - 1, 2, None if later < S else W_BANKS[0])
             if later < S:
                 weight_grad(s - 1, 0)
             w_fill(ahead + 1, 1)
             if ahead < last:
                 h_interleave(later, on_scalar, H_MID, D1)
-            input_grad(s - 1, 3)
+            input_grad(s - 1, 3, None if later < S else W_BANKS[1])
             if later < S:
                 weight_grad(s - 1, 1)
             if s <= 4:
@@ -452,21 +444,23 @@ def tile_bnn_pb_v_kernel(tc, h0, wm1, wv1, bm1, bv1, we1, be1, z, grad_out, out_
 
         s = last - 1
         store(s - 2)
+        quantize("dt", s - 2)
+        weight_grads(s - 2)
+        d_interleave(s, on_scalar, G_D, HALF)
         mask(s, cols=slice(HALF, D2))
         dz_banks(s)
-        quantize("dt", s - 2)
         quantize("df", s - 1)
         mask(last)
         outs(s - 1)
         quantize("df", s)
         dz_banks(last)
-        quantize("w", last)
-        outs(s, s - 2)
         quantize("dt", s - 1)
-        d_interleave(s, on_vector, G_D, D2)
+        outs(s, s - 1)
+        quantize("w", last)
+        d_interleave(s, on_vector, HALF, D2)
         quantize("h", s)
         quantize("df", last)
-        outs(last, s - 1)
+        outs(last)
         d_interleave(last, on_vector, 0, D2)
         quantize("dt", s)
         weight_grads(s)

@@ -57,7 +57,7 @@ def tile_bnn_pb_v_kernel(tc, h0, wm1, wv1, bm1, bv1, we1, be1, z, grad_out, out_
         make_identity(nc, ident_f[:])
 
         we_t, g_t, h_t = {}, {}, {}
-        z_all = loads.tile([P, S, 4, COLS], F32, name="z", bufs=1)
+        z_all = loads.tile([P, S, 4, COLS], F32, name="z", bufs=1, align_bytes=256)
         wf_t, dz_t, staged, coded, w_banks, acc = {}, {}, {}, {}, {}, {}
 
         def rows(ap):
@@ -67,7 +67,8 @@ def tile_bnn_pb_v_kernel(tc, h0, wm1, wv1, bm1, bv1, we1, be1, z, grad_out, out_
             return src[first : first + count].rearrange("s (p j) w -> p s (j w)", j=4)
 
         def load(store, src, name, first, count=1):
-            tile = loads.tile([P, count, 4, COLS], BF16, name=name + str(count), bufs=LOAD_BUFS[name, count])
+            bufs = LOAD_BUFS[name, count]
+            tile = loads.tile([P, count, 4, COLS], BF16, name=name + str(count), bufs=bufs, align_bytes=256)
             nc.sync.dma_start(out=tile[:].rearrange("p s j w -> p s (j w)"), in_=rows_of(src, first, count))
             for k in range(count):
                 store[first + k] = tile[:, k, :, :]

@@ -445,14 +445,17 @@ def tile_bnn_pb_v_kernel(tc, h0, wm1, wv1, bm1, bv1, we1, be1, z, grad_out, out_
 
         s = last - 1
         store(s - 2)
-        quantize("dt", s - 2)
-        weight_grads(s - 2)
         d_interleave(s, on_scalar, G_D, HALF)
         mask(s, cols=slice(HALF, D2))
         dz_banks(s)
+        quantize("dt", s - 2)
+        weight_grad(s - 2, 0)
+        weight_grad(s - 2, 1)
         quantize("df", s - 1)
         mask(last)
         outs(s - 1)
+        weight_grad(s - 2, 2)
+        weight_grad(s - 2, 3)
         quantize("df", s)
         dz_banks(last)
         quantize("dt", s - 1)

@@ -387,6 +387,7 @@ def tile_bnn_pb_v_kernel(tc, h0, wm1, wv1, bm1, bv1, we1, be1, z, grad_out, out_
             input_grad(s - 1, 0)
             if s > 1:
                 w_fill(ahead, 2)
+            weight_grad(s - 2, 1)
             d_interleave(s, on_scalar, G_D, d_cut)
             input_grad(s - 1, 1)
             if s > 1:
@@ -419,8 +420,6 @@ def tile_bnn_pb_v_kernel(tc, h0, wm1, wv1, bm1, bv1, we1, be1, z, grad_out, out_
             if ahead < last:
                 h_interleave(later, on_scalar, H_MID, D1)
             input_grad(s - 1, 3, None if later < S else W_BANKS[1])
-            if later < S:
-                weight_grad(s - 1, 1)
             if s <= 4:
                 load_step(s + LEAD + 1)
             if s == 4:

@@ -26,7 +26,7 @@ PLAIN = 3
 STD_FLOOR = 2.0**-63
 FORMAT = {"w": E4M3, "h": E4M3, "df": E5M2, "dt": E5M2}
 LEAD = 2
-LOAD_BUFS = {("we", 1): 3, ("h", 1): 3, ("g", 1): 3, ("we", 2): 1, ("h", 2): 1, ("g", 2): 2}
+LOAD_BUFS = {("we", 1): 3, ("h", 1): 1, ("g", 1): 3, ("we", 2): 1, ("h", 2): 2, ("g", 2): 1, ("g", 3): 1}
 DZ_BUFS = 3
 STAGE_BUFS = {"w": 2, "h": 2, "df": 2, "dt": 3}
 W_BANKS = ("w0", "w1", "w0", "w1")
@@ -235,7 +235,8 @@ def tile_bnn_pb_v_kernel(tc, h0, wm1, wv1, bm1, bv1, we1, be1, z, grad_out, out_
             copy(out=results[pair][:, k, :], in_=acc[blk][:])
             if k == 1:
                 dst = out_1[2 * P * pair : 2 * P * (pair + 1), :].rearrange("(k p) w -> p k w", k=2)
-                nc.sync.dma_start(out=dst, in_=results[pair][:])
+                queue = nc.scalar if pair else nc.sync
+                queue.dma_start(out=dst, in_=results[pair][:])
 
         def input_grad(s, j, tag=None, copy=on_scalar):
             if s < 0:
@@ -254,11 +255,11 @@ def tile_bnn_pb_v_kernel(tc, h0, wm1, wv1, bm1, bv1, we1, be1, z, grad_out, out_
             )
             copy(out=z_all[:, s, j, :].rearrange("p (x w) -> p x w", w=4), in_=bank[:].rearrange("p w x -> p x w"))
 
-        def store(s, js=ROWS):
-            nc.sync.dma_start(out=rows(out_0[s])[:, js, :], in_=z_all[:, s, js, :])
+        def store(s, js=ROWS, queue=nc.sync):
+            queue.dma_start(out=rows(out_0[s])[:, js, :], in_=z_all[:, s, js, :])
 
-        def store_samples(first, count):
-            nc.sync.dma_start(out=rows_of(out_0, first, count), in_=z_rows(first, count))
+        def store_samples(first, count, queue=nc.sync):
+            queue.dma_start(out=rows_of(out_0, first, count), in_=z_rows(first, count))
 
         wv_t = mid.tile([P, 4, D2], BF16, name="dz", align_bytes=256, bufs=DZ_BUFS)
         wm_t = mid.tile([P, 4, D2], BF16, name="dz", align_bytes=256, bufs=DZ_BUFS)
@@ -298,25 +299,27 @@ def tile_bnn_pb_v_kernel(tc, h0, wm1, wv1, bm1, bv1, we1, be1, z, grad_out, out_
         for js in ROW_HALVES:
             nc.sync.dma_start(out=wv_t[:, js, :], in_=rows(wv1)[:, js, :])
             nc.sync.dma_start(out=wm_t[:, js, :], in_=rows(wm1)[:, js, :])
-        for s in range(LEAD):
-            load_we(s + 1)
-            load_h(s)
-        load_h(LEAD)
+        load_we(1)
+        load_h(0)
+        load_we(2)
+        load_h(1, 2)
 
         def load_step(s):
             if s < 6:
                 load_z(s)
             elif s == 6:
                 load_z(s, 2)
-            if s in (3, 5):
-                load_g(s, 2)
-            elif s not in (4, 6):
+            if s < 3:
                 load_g(s)
+            elif s == 3:
+                load_g(s, 2)
+            elif s == 5:
+                load_g(s, 3)
             if s == 0:
                 load_we(LEAD + 1)
             if s == 1:
-                load_h(LEAD + 1)
-            if 0 < s <= 3:
+                load_h(LEAD + 1, 2)
+            if 1 < s <= 3:
                 load_h(s + LEAD + 1, 2 if s == 3 else 1)
             if 0 < s <= 3:
                 load_we(s + LEAD + 1, 2 if s == 3 else 1)
@@ -378,6 +381,7 @@ def tile_bnn_pb_v_kernel(tc, h0, wm1, wv1, bm1, bv1, we1, be1, z, grad_out, out_
 
         for s in range(1, S - LEAD):
             ahead = s + LEAD
+            later = ahead + 1
             d_cut = (G_D + D2) // 2
             mask(s)
             d_on_gpsimd(s, 0, G_D)
@@ -393,8 +397,9 @@ def tile_bnn_pb_v_kernel(tc, h0, wm1, wv1, bm1, bv1, we1, be1, z, grad_out, out_
             if s > 1:
                 w_fill(ahead, 3)
             we_cast(ahead + 1)
+            if later == S:
+                store_samples(2, 2, nc.scalar)
             dz_bank(s, 0)
-            later = ahead + 1
             if later < S:
                 quantize("dt", s - 1)
                 quantize("h", s + 1)
@@ -424,7 +429,6 @@ def tile_bnn_pb_v_kernel(tc, h0, wm1, wv1, bm1, bv1, we1, be1, z, grad_out, out_
                 load_step(s + LEAD + 1)
             if s == 4:
                 store_samples(0, 2)
-                store_samples(2, 2)
 
         turn.clear()
         def outs(n, beside=-1):
@@ -432,7 +436,7 @@ def tile_bnn_pb_v_kernel(tc, h0, wm1, wv1, bm1, bv1, we1, be1, z, grad_out, out_
                 input_grad(n, q, tag=next_bank(TAIL_BANKS))
                 weight_grad(beside, q)
                 if q % 2:
-                    store(n, ROW_HALVES[q // 2])
+                    store(n, ROW_HALVES[q // 2], nc.scalar if (n, q) == (last, 3) else nc.sync)
 
         def dz_banks(n):
             for half in range(2):

from contextlib import ExitStack

import concourse.mybir as mybir
from concourse.masks import make_identity

S, B, D1, D2 = 8, 512, 512, 512
FLOPS = 2 * 2 * S * B * D1 * D2
BYTES = S * B * (2 * D1 + 4 * D2 + 2 * D2 + 4 * D1) + 2 * S * D1 * D2 + (2 + 2 + 4) * D1 * D2

F32 = mybir.dt.float32
BF16 = mybir.dt.bfloat16
U32 = mybir.dt.uint32
U8 = mybir.dt.uint8
E4M3 = mybir.dt.float8_e4m3fn_x4
E5M2 = mybir.dt.float8_e5m2_x4
ALU = mybir.AluOpType
ACT = mybir.ActivationFunctionType

P = 128
COLS = 512
HALF = 256
ROWS = slice(0, 4)
ROW_HALVES = (slice(0, 2), slice(2, 4))
RUN = 4
PLAIN = 3
STD_FLOOR = 2.0**-63
FORMAT = {"w": E4M3, "h": E4M3, "df": E5M2, "dt": E5M2}
LEAD = 2
LOAD_BUFS = {("we", 1): 3, ("h", 1): 1, ("g", 1): 3, ("we", 2): 1, ("h", 2): 2, ("g", 2): 1, ("g", 3): 1}
DZ_BUFS = 3
STAGE_BUFS = {"w": 2, "h": 2, "df": 2, "dt": 3}
W_BANKS = ("w0", "w1", "w0", "w1")
COPY_BANKS = ("c0", "c1")
ACC_BANKS = ("a0", "a1", "a2", "a3")
TAIL_BANKS = ("w1", "c1", "c0", "w0")
HEAD_BANKS = {0: ACC_BANKS, 1: ("w0", "w1", "c1", "c0"), 2: ACC_BANKS, 3: ("w0", "w1", "a0", "a1")}
CODE_BUFS = {"w": 3, "h": 4, "df": 2, "dt": 3}
H_MID = 304
G_D = 160
G_H = 160


def tile_bnn_pb_v_kernel(tc, h0, wm1, wv1, bm1, bv1, we1, be1, z, grad_out, out_0, out_1):
    nc = tc.nc
    on_vector, on_scalar = nc.vector.tensor_copy, nc.scalar.copy
    with ExitStack() as ctx:
        const = ctx.enter_context(tc.tile_pool(name="const", bufs=1))
        loads = ctx.enter_context(tc.tile_pool(name="loads", bufs=S))
        mid = ctx.enter_context(tc.tile_pool(name="mid", bufs=2))
        codes = ctx.enter_context(tc.tile_pool(name="codes", bufs=1))
        psum = ctx.enter_context(tc.psum_pool(name="psum", bufs=1))
        ctx.enter_context(tc.manual_schedule())

        ident_b = const.tile([P, P], BF16, name="ident_b")
        make_identity(nc, ident_b[:])
        ident_f = const.tile([P, P], F32, name="ident_f")
        make_identity(nc, ident_f[:])

        we_t, g_t, h_t = {}, {}, {}
        z_all = loads.tile([P, S, 4, COLS], F32, name="z", bufs=1, align_bytes=256)
        wf_t, dz_t, staged, coded, w_banks, acc = {}, {}, {}, {}, {}, {}

        def rows(ap):
            return ap.rearrange("(p j) w -> p j w", j=4)

        def rows_of(src, first, count):
            return src[first : first + count].rearrange("s (p j) w -> p s (j w)", j=4)

        def load(store, src, name, first, count=1):
            bufs = LOAD_BUFS[name, count]
            tile = loads.tile([P, count, 4, COLS], BF16, name=name + str(count), bufs=bufs, align_bytes=256)
            nc.sync.dma_start(out=tile[:].rearrange("p s j w -> p s (j w)"), in_=rows_of(src, first, count))
            for k in range(count):
                store[first + k] = tile[:, k, :, :]

        def load_we(first, count=1):
            load(we_t, we1, "we", first, count)

        def load_h(first, count=1):
            load(h_t, h0, "h", first, count)

        def load_g(first, count=1):
            load(g_t, grad_out, "g", first, count)

        def z_rows(first, count):
            return z_all[:, first : first + count, :, :].rearrange("p s j w -> p s (j w)")

        def load_z(first, count=1):
            nc.sync.dma_start(out=z_rows(first, count), in_=rows_of(z, first, count))

        def stage(kind, s):
            if (kind, s) not in staged:
                staged[kind, s] = mid.tile([P, 4 * COLS], BF16, name=kind, align_bytes=256, bufs=STAGE_BUFS[kind])
            return staged[kind, s][:]

        def quantize(kind, s, lo=0, hi=COLS):
            if not 0 <= s < S:
                return
            if (kind, s) not in coded:
                words = codes.tile([P, COLS], U32, name=kind + "c", align_bytes=256, bufs=CODE_BUFS[kind])
                scales = codes.tile([P, COLS], U8, name=kind + "s", align_bytes=256, bufs=CODE_BUFS[kind])
                coded[kind, s] = (words, scales)
            words, scales = coded[kind, s]
            nc.vector.quantize_mx(
                out=words[:, lo:hi].bitcast(FORMAT[kind]),
                scales=scales[:, lo:hi],
                in_=staged[kind, s][:, 4 * lo : 4 * hi],
            )

        def operand(kind, s, lo, hi):
            words, scales = coded[kind, s]
            return words[:, lo:hi].bitcast(FORMAT[kind]), scales[:, lo:hi]

        def mask(s, js=ROWS, cols=slice(0, D2)):
            if s not in dz_t:
                dz_t[s] = mid.tile([P, 4, COLS], BF16, name="dz", align_bytes=256, bufs=DZ_BUFS)
            nc.vector.scalar_tensor_tensor(
                out=dz_t[s][:, js, cols],
                in0=z_all[:, s, js, cols],
                scalar=0.0,
                in1=g_t[s][:, js, cols],
                op0=ALU.is_gt,
                op1=ALU.mult,
            )

        def interleave(copy, src, dst, lo, hi):
            copy(
                out=dst[:, 4 * lo : 4 * hi].rearrange("p (n r j) -> p n j r", r=RUN, j=4),
                in_=src[:, :, lo:hi].rearrange("p j (n r) -> p n j r", r=RUN),
            )

        def d_interleave(s, copy, lo, hi):
            interleave(copy, dz_t[s], stage("dt", s), lo, hi)

        def h_interleave(s, copy, lo, hi):
            interleave(copy, h_t[s], stage("h", s), lo, hi)

        def h_on_gpsimd(s, lo, hi):
            on_gpsimd(h_t[s], stage("h", s), lo, hi)

        def d_on_gpsimd(s, lo, hi):
            on_gpsimd(dz_t[s], stage("dt", s), lo, hi)

        def on_gpsimd(src, dst, lo, hi):
            nc.gpsimd.tensor_scalar(
                out=dst[:, 4 * lo : 4 * hi].rearrange("p (c j) -> p c j", j=4),
                in0=src[:, :, lo:hi].rearrange("p j c -> p c j"),
                scalar1=1.0,
                scalar2=0.0,
                op0=ALU.mult,
                op1=ALU.add,
            )

        def we_cast(s):
            if s < S:
                wf_t[s] = mid.tile([P, 4, P], F32, name="wf")
                on_scalar(out=wf_t[s][:], in_=we_t[s][:, :, PLAIN::4])

        def we_cast_on_gpsimd(s):
            wf_t[s] = mid.tile([P, 4, P], F32, name="wf")
            nc.gpsimd.tensor_scalar(
                out=wf_t[s][:], in0=we_t[s][:, :, PLAIN::4], scalar1=1.0, scalar2=0.0, op0=ALU.mult, op1=ALU.add
            )

        def w_matmuls(s, j):
            w_banks[s, j] = psum.tile([P, 4, P], F32, name=HEAD_BANKS.get(s, W_BANKS)[j])
            for t in range(PLAIN if s > 0 else 4):
                nc.tensor.matmul(
                    w_banks[s, j][:, t, :], lhsT=we_t[s][:, j, t::4], rhs=ident_b[:], start=(t == 0), stop=False
                )

        def w_transposes(s, j):
            bank = w_banks[s, j]
            if s > 0:
                nc.tensor.matmul(
                    bank[:, PLAIN, :], lhsT=wf_t[s][:, j, :], rhs=ident_f[:], is_transpose=True, start=False, stop=False
                )
            for t in range(4):
                nc.tensor.matmul(
                    bank[:, t, :], lhsT=ratio[:, j, t, :], rhs=ident_f[:], is_transpose=True, start=False, stop=(t == 3)
                )

        def w_out(s, j):
            nc.vector.scalar_tensor_tensor(
                out=stage("w", s)[:, COLS * j : COLS * (j + 1)].rearrange("p (x t) -> p x t", t=4),
                in0=std_t[:, j, :, :],
                scalar=STD_FLOOR,
                in1=w_banks[s, j][:].rearrange("p t x -> p x t"),
                op0=ALU.max,
                op1=ALU.mult,
            )

        turn = []

        def next_bank(banks=COPY_BANKS):
            turn.append(None)
            return banks[len(turn) % len(banks)]

        def word_bank(src, half, tag=None):
            bank = psum.tile([P, 2, 2, P], F32, name=tag or next_bank())
            for k in range(2):
                words = src[:, 2 * half + k, :].bitcast(F32)
                for u in range(2):
                    nc.tensor.transpose(bank[:, k, u, :], words[:, u::2], ident_f[:])
            return bank

        def dz_bank(s, half, copy=on_scalar, tag=None):
            bank = word_bank(dz_t[s], half, tag)
            dt = stage("df", s)[:, 2 * COLS * half : 2 * COLS * (half + 1)].bitcast(F32)
            copy(out=dt.rearrange("p (k x u) -> p k x u", k=2, u=2), in_=bank[:].rearrange("p k u x -> p k x u"))

        def weight_grad(s, blk):
            if s < 0:
                return
            if s == 0:
                acc[blk] = psum.tile([P, COLS], F32, name=ACC_BANKS[blk])
            hc, hs = operand("h", s, P * blk, P * (blk + 1))
            dc, ds = operand("dt", s, 0, COLS)
            nc.tensor.matmul_mx(
                out=acc[blk][:],
                lhsT=hc,
                lhsT_scale=hs,
                rhs=dc,
                rhs_scale=ds,
                start=(s == 0),
                stop=(s == S - 1),
            )

        results = {}

        def finish_weight_grad(blk, copy):
            pair, k = divmod(blk, 2)
            if k == 0:
                results[pair] = mid.tile([P, 2, COLS], F32, name="w", align_bytes=256)
            copy(out=results[pair][:, k, :], in_=acc[blk][:])
            if k == 1:
                dst = out_1[2 * P * pair : 2 * P * (pair + 1), :].rearrange("(k p) w -> p k w", k=2)
                queue = nc.scalar if pair else nc.sync
                queue.dma_start(out=dst, in_=results[pair][:])

        def input_grad(s, j, tag=None, copy=on_scalar):
            if s < 0:
                return
            bank = psum.tile([P, 4, P], F32, name=tag or next_bank())
            dc, ds = operand("df", s, P * j, P * (j + 1))
            wc, ws = operand("w", s, 0, COLS)
            nc.tensor.matmul_mx(
                out=bank[:].rearrange("p w x -> p (w x)"),
                lhsT=dc,
                lhsT_scale=ds,
                rhs=wc,
                rhs_scale=ws,
                start=True,
                stop=True,
            )
            copy(out=z_all[:, s, j, :].rearrange("p (x w) -> p x w", w=4), in_=bank[:].rearrange("p w x -> p x w"))

        def store(s, js=ROWS, queue=nc.sync):
            queue.dma_start(out=rows(out_0[s])[:, js, :], in_=z_all[:, s, js, :])

        def store_samples(first, count, queue=nc.sync):
            queue.dma_start(out=rows_of(out_0, first, count), in_=z_rows(first, count))

        wv_t = mid.tile([P, 4, D2], BF16, name="dz", align_bytes=256, bufs=DZ_BUFS)
        wm_t = mid.tile([P, 4, D2], BF16, name="dz", align_bytes=256, bufs=DZ_BUFS)
        ratio = const.tile([P, 4, 4, P], F32, name="ratio")
        std_t = const.tile([P, 4, P, 4], F32, name="std_t")

        def inverse_std(j):
            nc.scalar.activation(
                out=ratio[:, j, :, :], in_=wv_t[:, j, :].rearrange("p (m t) -> p t m", t=4), func=ACT.Exp, scale=-0.5
            )

        def std_rows(half, bank):
            for k in range(2):
                nc.scalar.activation(
                    out=std_t[:, 2 * half + k, :, :].rearrange("p x (u e) -> p x u e", e=2),
                    in_=bank[:, k, :, :].bitcast(BF16).rearrange("p u (x e) -> p x u e", e=2),
                    func=ACT.Exp,
                    scale=0.5,
                )

        def ratio_row(j):
            nc.vector.scalar_tensor_tensor(
                out=ratio[:, j, :, :],
                in0=ratio[:, j, :, :],
                scalar=1.0 / STD_FLOOR,
                in1=wm_t[:, j, :].rearrange("p (m t) -> p t m", t=4),
                op0=ALU.min,
                op1=ALU.mult,
            )

        def w_fill(s, j):
            if s < S:
                w_matmuls(s, j)
                w_transposes(s, j)

        load_we(0)
        for js in ROW_HALVES:
            nc.sync.dma_start(out=wv_t[:, js, :], in_=rows(wv1)[:, js, :])
            nc.sync.dma_start(out=wm_t[:, js, :], in_=rows(wm1)[:, js, :])
        load_we(1)
        load_h(0)
        load_we(2)
        load_h(1, 2)

        def load_step(s):
            if s < 6:
                load_z(s)
            elif s == 6:
                load_z(s, 2)
            if s < 3:
                load_g(s)
            elif s == 3:
                load_g(s, 2)
            elif s == 5:
                load_g(s, 3)
            if s == 0:
                load_we(LEAD + 1)
            if s == 1:
                load_h(LEAD + 1, 2)
            if 1 < s <= 3:
                load_h(s + LEAD + 1, 2 if s == 3 else 1)
            if 0 < s <= 3:
                load_we(s + LEAD + 1, 2 if s == 3 else 1)

        for j in range(2):
            w_matmuls(0, j)
        inverse_std(0)
        inverse_std(1)
        banks = [word_bank(wv_t, half) for half in range(2)]
        inverse_std(2)
        inverse_std(3)
        for j in range(4):
            ratio_row(j)
        for j in range(2, 4):
            w_matmuls(0, j)
        for half in range(2):
            std_rows(half, banks[half])
        for s in range(1, LEAD + 1):
            we_cast_on_gpsimd(s)
        for s in range(LEAD):
            for j in range(4):
                w_transposes(s, j)
                w_out(s, j)
                w_matmuls(s + 1, j)
                if j == 1:
                    quantize("w", s - 1)
                    quantize("h", s - 1)
            h_interleave(s, on_scalar, 0, D1)
            load_step(s)
        for j in range(4):
            w_transposes(LEAD, j)

        last = S - 1

        h_interleave(LEAD, on_scalar, 0, D1)
        load_step(LEAD)
        w_out(LEAD, 0)
        quantize("h", 1)
        quantize("w", 1)
        we_cast(LEAD + 1)
        w_matmuls(LEAD + 1, 0)
        w_matmuls(LEAD + 1, 1)
        w_transposes(LEAD + 1, 0)
        mask(0, cols=slice(0, HALF))
        d_on_gpsimd(0, 0, HALF)
        mask(0, cols=slice(HALF, D2))
        d_interleave(0, on_scalar, HALF, D2)
        dz_bank(0, 0)
        dz_bank(0, 1)
        w_out(LEAD, 1)
        w_out(LEAD, 2)
        w_out(LEAD, 3)
        w_transposes(LEAD + 1, 1)
        w_fill(LEAD + 1, 2)
        w_fill(LEAD + 1, 3)
        h_interleave(LEAD + 1, on_scalar, 0, D1)
        load_step(LEAD + 1)


        for s in range(1, S - LEAD):
            ahead = s + LEAD
            later = ahead + 1
            d_cut = (G_D + D2) // 2
            mask(s)
            d_on_gpsimd(s, 0, G_D)
            quantize("df", s - 1)
            w_out(ahead, 0)
            w_out(ahead, 1)
            input_grad(s - 1, 0)
            if s > 1:
                w_fill(ahead, 2)
            weight_grad(s - 2, 1)
            d_interleave(s, on_scalar, G_D, d_cut)
            input_grad(s - 1, 1)
            if s > 1:
                w_fill(ahead, 3)
            we_cast(ahead + 1)
            if later == S:
                store_samples(2, 2, nc.scalar)
            dz_bank(s, 0)
            if later < S:
                quantize("dt", s - 1)
                quantize("h", s + 1)
                h_on_gpsimd(later, 0, G_H)
            else:
                mask(s + 1, cols=slice(0, HALF))
                d_on_gpsimd(s + 1, 0, G_D)
            quantize("w", ahead - 1)
            if later < S:
                weight_grad(s - 1, 2)
                weight_grad(s - 1, 3)
            d_interleave(s, on_scalar, d_cut, D2)
            dz_bank(s, 1)
            w_out(ahead, 2)
            w_out(ahead, 3)
            w_fill(ahead + 1, 0)
            if ahead < last:
                h_interleave(later, on_scalar, G_H, H_MID)
            input_grad(s - 1, 2, None if later < S else W_BANKS[0])
            if later < S:
                weight_grad(s - 1, 0)
            w_fill(ahead + 1, 1)
            if ahead < last:
                h_interleave(later, on_scalar, H_MID, D1)
            input_grad(s - 1, 3, None if later < S else W_BANKS[1])
            if s <= 4:
                load_step(s + LEAD + 1)
            if s == 4:
                store_samples(0, 2)

        turn.clear()
        def outs(n, beside=-1):
            for q in range(4):
                input_grad(n, q, tag=next_bank(TAIL_BANKS))
                weight_grad(beside, q)
                if q % 2:
                    store(n, ROW_HALVES[q // 2], nc.scalar if (n, q) == (last, 3) else nc.sync)

        def dz_banks(n):
            for half in range(2):
                dz_bank(n, half, on_scalar, next_bank(TAIL_BANKS))

        def weight_grads(n):
            for blk in range(4):
                weight_grad(n, blk)

        s = last - 1
        store(s - 2)
        d_interleave(s, on_scalar, G_D, HALF)
        mask(s, cols=slice(HALF, D2))
        dz_banks(s)
        quantize("dt", s - 2)
        weight_grad(s - 2, 0)
        weight_grad(s - 2, 1)
        quantize("df", s - 1)
        mask(last)
        outs(s - 1)
        weight_grad(s - 2, 2)
        weight_grad(s - 2, 3)
        quantize("df", s)
        dz_banks(last)
        quantize("dt", s - 1)
        outs(s, s - 1)
        quantize("w", last)
        d_interleave(s, on_vector, HALF, D2)
        quantize("h", s)
        quantize("df", last)
        outs(last)
        d_interleave(last, on_vector, 0, D2)
        quantize("dt", s)
        weight_grads(s)
        quantize("h", last)
        quantize("dt", last)
        weight_grads(last)
        for blk in range(4):
            finish_weight_grad(blk, on_scalar if blk % 2 else on_vector)
